import numpy as np
import ml_dtypes


def mxq(x, axis, fmt="e4m3"):
    dtype, down = {"e4m3": (ml_dtypes.float8_e4m3fn, 7), "e5m2": (ml_dtypes.float8_e5m2, 14)}[fmt]
    v = np.moveaxis(np.asarray(x, np.float32).astype(ml_dtypes.bfloat16).astype(np.float64), axis, -1)
    blocks = v.reshape(v.shape[:-1] + (-1, 32))
    amax = np.abs(blocks).max(-1, keepdims=True)
    byte = np.maximum(np.where(amax > 0, np.frexp(amax)[1] - 1 + 127, 0) - down, 1)
    scale = np.exp2(byte - 127.0)
    codes = (blocks / scale).astype(np.float32).astype(dtype).astype(np.float64)
    return np.moveaxis((codes * scale).reshape(v.shape), -1, axis)


WIDE = False


def mx_kscale(k):
    if not WIDE:
        return np.ones(k)
    levels = np.array([10, -10, 5, -5, 0])
    a = np.random.permutation(np.resize(levels, k // 512 * 4)).reshape(k // 512, 4)
    idx = np.arange(k)
    return np.exp2(a[idx // 512, idx % 128 // 32])


BF16 = ml_dtypes.bfloat16


def bf(x):
    return np.asarray(x, np.float32).astype(BF16)


def f64(x):
    return np.asarray(x).astype(np.float64)


BS, SEQ, DM, H, DH, W = 2, 320, 1024, 2, 512, 32
X = BS * H
NW = SEQ // W
W2 = W + W
IGNORE = -1000000.0
JU, KU = np.triu_indices(W, 1)
POS = np.arange(SEQ).reshape(NW, W)
LA = np.concatenate([np.concatenate([np.zeros_like(POS[:1]), POS[:-1]], 0), POS], 1)
MASK = (POS[:, :, None, None] < LA[:, None, None, :]) | (LA[:, None, None, :] <= LA[:, None, :, None])


def setup_inputs():
    s = mx_kscale(DH)
    g = 1.25 * DH ** (1.0 / 6.0)
    return {"a": bf(np.random.standard_normal((X, NW, W, DH)) * g),
            "b": bf(np.random.standard_normal((X, NW, W, DH)) * g / s),
            "c": bf(np.random.standard_normal((X, NW, W, DH)) * g * s)}


def reference(a, b, c):
    a, b, c = f64(a), f64(b), f64(c)
    cq = mxq(c, 3, "e4m3")
    same = mxq(a[:, :, JU, :] * b[:, :, KU, :], 3, "e4m3")
    cross = mxq((a[:, :-1, :, None, :] * b[:, 1:, None, :, :]).reshape(X, NW - 1, W * W, DH), 3, "e4m3")
    attn = np.full((X, NW, W, W2, W2), IGNORE)
    attn[:, :, :, W + JU, W + KU] = cq @ same.swapaxes(2, 3)
    attn[:, 1:, :, JU, KU] = cq[:, 1:] @ same[:, :-1].swapaxes(2, 3)
    attn[:, 1:, :, :W, W:] = (cq[:, 1:] @ cross.swapaxes(2, 3)).reshape(X, NW - 1, W, W, W)
    attn = np.where(MASK, IGNORE, attn) / DH
    flat = attn.reshape(X, NW, W, W2 * W2)
    ex = np.exp(flat - flat.max(-1, keepdims=True))
    score = (ex / ex.sum(-1, keepdims=True)).reshape(X, NW, W, W2, W2)
    return score.sum(4), score.sum(3)

@@ -1,0 +1,355 @@
+from contextlib import ExitStack
+
+import concourse.mybir as mybir
+from concourse.masks import make_identity
+
+F32 = mybir.dt.float32
+BF16 = mybir.dt.bfloat16
+I32 = mybir.dt.int32
+U32 = mybir.dt.uint32
+U8 = mybir.dt.uint8
+FP8X4 = mybir.dt.float8_e4m3fn_x4
+ALU = mybir.AluOpType
+ACT = mybir.ActivationFunctionType
+AXIS_X = mybir.AxisListType.X
+
+P = 128
+PACK = 4
+X = 4
+NW = 10
+W = 32
+DH = 512
+TRI = W * (W - 1) // 2
+TRI_PAD = 512
+BANK = 512
+SCORE_BANKS = 7
+IGNORE = -1000000.0
+INV_DH = 1.0 / DH
+BLOCKED = -1.0e30
+
+FLOPS = 2 * W * DH * (X * NW * TRI + X * (NW - 1) * TRI + X * (NW - 1) * W * W)
+
+
+def first_pair(k):
+    return k * (k - 1) // 2
+
+
+def tile_localtrittention_pa_kernel(tc, a, b, c, out_0, out_1):
+    nc = tc.nc
+    with ExitStack() as ctx:
+        keep = ctx.enter_context(tc.tile_pool(name="keep", bufs=1))
+        psum = ctx.enter_context(tc.psum_pool(name="psum", bufs=1))
+
+        raw = {
+            "a": keep.tile([P, NW, DH], BF16, name="raw_a"),
+            "b": keep.tile([P, NW, DH], BF16, name="raw_b"),
+            "c": keep.tile([P, NW, DH], BF16, name="raw_c"),
+        }
+        a_t = keep.tile([P, NW, P, PACK], BF16, name="a_t", align_bytes=64)
+        b_t = keep.tile([P, NW, P, PACK], BF16, name="b_t", align_bytes=64)
+        ident = keep.tile([P, P], F32, name="ident")
+
+        c_wide = [keep.tile([P, X, P, PACK], BF16, name="c_wide%d" % i, align_bytes=64) for i in range(2)]
+        c_codes = [keep.tile([P, X * P], U32, name="c_codes%d" % i, align_bytes=64) for i in range(2)]
+        c_scales = [keep.tile([P, X * P], U8, name="c_scales%d" % i, align_bytes=64) for i in range(2)]
+
+        cross_keys = [keep.tile([P, W, W, PACK], BF16, name="cross_keys%d" % i, align_bytes=64) for i in range(3)]
+        cross_codes = [keep.tile([P, W * W], U32, name="cross_codes%d" % i, align_bytes=64) for i in range(X)]
+        cross_scales = [keep.tile([P, W * W], U8, name="cross_scales%d" % i, align_bytes=64) for i in range(X)]
+        same_keys = keep.tile([P, X, TRI_PAD, PACK], BF16, name="same_keys", align_bytes=64)
+        same_codes = [keep.tile([P, X, TRI_PAD], U32, name="same_codes%d" % i, align_bytes=64) for i in range(2)]
+        same_scales = [keep.tile([P, X, TRI_PAD], U8, name="same_scales%d" % i, align_bytes=64) for i in range(2)]
+
+        banks = [psum.tile([P, BANK], F32, name="bank%d" % i) for i in range(SCORE_BANKS)]
+        turned = psum.tile([P, BANK], F32, name="turned")
+
+        exp_own = [keep.tile([P, W, 2 * W], F32, name="exp_own%d" % i) for i in range(2)]
+        exp_old = [keep.tile([P, W, W], F32, name="exp_old%d" % i) for i in range(2)]
+        half_own = keep.tile([P, W - 2, 2 * W], F32, name="half_own")
+        half_old = keep.tile([P, W - 1, W], F32, name="half_old")
+
+        tops = [keep.tile([P, W + 3], F32, name="tops%d" % i) for i in range(2)]
+        tops_open = keep.tile([P, W + 3], F32, name="tops_open")
+        own_open = keep.tile([P, TRI], F32, name="own_open")
+        top = keep.tile([P, 1], F32, name="top")
+        shift = [keep.tile([P, 1], F32, name="shift%d" % i) for i in range(2)]
+        shift_k = [keep.tile([P, W], F32, name="shift_k%d" % i) for i in range(2)]
+        masked_exp = [keep.tile([P, 1], F32, name="masked_exp%d" % i) for i in range(2)]
+        k_sums = [keep.tile([P, 2 * W], F32, name="k_sums%d" % i) for i in range(2)]
+        sums = [keep.tile([P, 4 * W], F32, name="sums%d" % i) for i in range(2)]
+        full = [keep.tile([P, 4 * W], F32, name="full%d" % i) for i in range(2)]
+        total = keep.tile([P, 1], F32, name="total")
+        scale = [keep.tile([P, 1], F32, name="scale%d" % i) for i in range(2)]
+        result = keep.tile([P, NW, 4 * W], F32, name="result")
+
+        i_minus_c_int = keep.tile([P, W], I32, name="i_minus_c_int")
+        col_int = keep.tile([P, W], I32, name="col_int")
+        i_minus_c = keep.tile([P, W], F32, name="i_minus_c")
+        col = keep.tile([P, W], F32, name="col")
+        seen = keep.tile([P, W], F32, name="seen")
+        work = keep.tile([P, W], F32, name="work")
+        blocked = keep.tile([P, W + 3], F32, name="blocked")
+        blocked_own = keep.tile([P, TRI], F32, name="blocked_own")
+        ignore_col = keep.tile([P, 1], F32, name="ignore_col")
+        masked_first = keep.tile([P, 4 * W], F32, name="masked_first")
+        masked_later = keep.tile([P, 4 * W], F32, name="masked_later")
+
+        make_identity(nc, ident[:])
+
+        def bank(n, region):
+            return banks[(4 * n + region) % SCORE_BANKS]
+
+        def load_inputs():
+            for n in range(NW):
+                for name, src in (("a", a), ("b", b), ("c", c)):
+                    for x in range(X):
+                        nc.sync.dma_start(out=raw[name][x * W : (x + 1) * W, n, :], in_=src[x, n])
+
+        def zero_what_stays_zero():
+            for i in range(2):
+                nc.vector.memset(c_wide[i][:].bitcast(I32), 0)
+                nc.gpsimd.memset(exp_own[i][:], 0.0)
+                nc.gpsimd.memset(exp_old[i][:], 0.0)
+                nc.vector.memset(k_sums[i][:], 0.0)
+                nc.vector.memset(sums[i][:], 0.0)
+                nc.vector.memset(tops[i][:, 0 : W + 2], BLOCKED)
+                nc.vector.memset(tops[i][:, W + 2 : W + 3], IGNORE)
+            nc.vector.memset(same_keys[:, :, TRI:TRI_PAD, :], 0.0)
+            nc.vector.memset(ignore_col[:], IGNORE * INV_DH)
+
+        def count_rows_and_columns():
+            for x in range(X):
+                nc.gpsimd.iota(i_minus_c_int[x * W : (x + 1) * W, :], pattern=[[-1, W]], base=0, channel_multiplier=1)
+            nc.gpsimd.iota(col_int[:], pattern=[[1, W]], base=0, channel_multiplier=0)
+
+        def build_constants():
+            nc.vector.tensor_copy(out=i_minus_c[:], in_=i_minus_c_int[:])
+            nc.vector.tensor_copy(out=col[:], in_=col_int[:])
+            nc.vector.tensor_scalar(out=seen[:], in0=i_minus_c[:], scalar1=0.0, scalar2=None, op0=ALU.is_ge)
+            nc.vector.memset(blocked[:, W : W + 3], 0.0)
+            nc.vector.tensor_scalar(
+                out=blocked[:, 0:W], in0=seen[:], scalar1=1.0, scalar2=-BLOCKED, op0=ALU.subtract, op1=ALU.mult
+            )
+            for k in range(1, W):
+                nc.vector.tensor_copy(
+                    out=blocked_own[:, first_pair(k) : first_pair(k) + k],
+                    in_=blocked[:, k : k + 1].to_broadcast([P, k]),
+                )
+            nc.vector.tensor_scalar(
+                out=masked_later[:, 0:W], in0=i_minus_c[:], scalar1=-1.0, scalar2=1.0 * W, op0=ALU.mult, op1=ALU.add
+            )
+            nc.vector.tensor_scalar(out=work[:], in0=i_minus_c[:], scalar1=0.0, scalar2=-1.0, op0=ALU.max, op1=ALU.mult)
+            nc.vector.tensor_scalar(out=masked_later[:, W : 2 * W], in0=work[:], scalar1=2.0 * W, scalar2=None, op0=ALU.add)
+            nc.vector.tensor_scalar(
+                out=masked_later[:, 2 * W : 3 * W], in0=col[:], scalar1=-1.0, scalar2=2.0 * W, op0=ALU.mult, op1=ALU.add
+            )
+            nc.vector.tensor_scalar(out=work[:], in0=col[:], scalar1=1.0 * W, scalar2=-1.0, op0=ALU.add, op1=ALU.mult)
+            nc.vector.tensor_tensor(out=work[:], in0=work[:], in1=seen[:], op=ALU.mult)
+            nc.vector.tensor_scalar(out=masked_later[:, 3 * W : 4 * W], in0=work[:], scalar1=2.0 * W, scalar2=None, op0=ALU.add)
+            nc.vector.memset(masked_first[:], 2.0 * W)
+            nc.vector.tensor_copy(out=masked_first[:, W : 2 * W], in_=masked_later[:, W : 2 * W])
+            nc.vector.tensor_tensor(out=work[:], in0=col[:], in1=seen[:], op=ALU.mult)
+            nc.vector.tensor_scalar(
+                out=masked_first[:, 3 * W : 4 * W], in0=work[:], scalar1=-1.0, scalar2=2.0 * W, op0=ALU.mult, op1=ALU.add
+            )
+
+        def turn(name, n, first_col):
+            words = raw[name][:, n, :].bitcast(F32)
+            for u in range(2):
+                nc.tensor.transpose(
+                    turned[:, first_col + u * P : first_col + (u + 1) * P], words[:, u * P : (u + 1) * P], ident[:]
+                )
+            return turned[:, first_col : first_col + 2 * P].rearrange("p (u r) -> p r u", u=2)
+
+        def prepare_window(n):
+            a_words = turn("a", n, 0)
+            b_words = turn("b", n, 2 * P)
+            nc.scalar.copy(out=a_t[:, n].bitcast(F32), in_=a_words)
+            nc.scalar.copy(out=b_t[:, n].bitcast(F32), in_=b_words)
+            c_words = turn("c", n, 0)
+            for x in range(X):
+                rows = slice(x * W, (x + 1) * W)
+                nc.scalar.copy(out=c_wide[n % 2][:, x, rows, :].bitcast(F32), in_=c_words[:, rows, :])
+
+        def quantise_queries(n):
+            nc.vector.quantize_mx(
+                out=c_codes[n % 2][:].bitcast(FP8X4),
+                scales=c_scales[n % 2][:],
+                in_=c_wide[n % 2][:].rearrange("p x r t -> p (x r t)"),
+            )
+
+        def score_pass(n, region, x, codes, scales):
+            cols = slice(x * P, (x + 1) * P)
+            nc.tensor.matmul_mx(
+                out=bank(n, region)[:],
+                lhsT=c_codes[n % 2][:, cols].bitcast(FP8X4),
+                lhsT_scale=c_scales[n % 2][:, cols],
+                rhs=codes.bitcast(FP8X4),
+                rhs_scale=scales,
+                start=(x == 0),
+                stop=(x == X - 1),
+            )
+
+        def cross_product(n, x):
+            rows = slice(x * W, (x + 1) * W)
+            nc.vector.tensor_tensor(
+                out=cross_keys[x % 3][:],
+                in0=a_t[:, n - 1, rows, :].unsqueeze(1).to_broadcast([P, W, W, PACK]),
+                in1=b_t[:, n, rows, :].unsqueeze(2).to_broadcast([P, W, W, PACK]),
+                op=ALU.mult,
+            )
+
+        def cross_quantise_and_score(n, x):
+            nc.vector.quantize_mx(
+                out=cross_codes[x][:].bitcast(FP8X4),
+                scales=cross_scales[x][:],
+                in_=cross_keys[x % 3][:].rearrange("p k j t -> p (k j t)"),
+            )
+            for half in range(2):
+                cols = slice(half * BANK, (half + 1) * BANK)
+                score_pass(n, 1 + half, x, cross_codes[x][:, cols], cross_scales[x][:, cols])
+
+        def same_products(n):
+            a_win = a_t[:, n].rearrange("p (x w) t -> p x w t", x=X)
+            b_win = b_t[:, n].rearrange("p (x w) t -> p x w t", x=X)
+            for k in range(1, W):
+                nc.vector.tensor_tensor(
+                    out=same_keys[:, :, first_pair(k) : first_pair(k) + k, :],
+                    in0=a_win[:, :, 0:k, :],
+                    in1=b_win[:, :, k : k + 1, :].to_broadcast([P, X, k, PACK]),
+                    op=ALU.mult,
+                )
+
+        def same_quantise(n):
+            for half in range(2):
+                heads = slice(2 * half, 2 * half + 2)
+                nc.vector.quantize_mx(
+                    out=same_codes[n % 2][:, heads, :].rearrange("p x c -> p (x c)").bitcast(FP8X4),
+                    scales=same_scales[n % 2][:, heads, :].rearrange("p x c -> p (x c)"),
+                    in_=same_keys[:, heads, :, :].rearrange("p x c t -> p (x c t)"),
+                )
+
+        def score_same(n, region, key_window):
+            for x in range(X):
+                score_pass(n, region, x, same_codes[key_window % 2][:, x, :], same_scales[key_window % 2][:, x, :])
+
+        def row_max(n):
+            t = tops[n % 2]
+            nc.vector.tensor_tensor(out=own_open[:], in0=bank(n, 3)[:, 0:TRI], in1=blocked_own[:], op=ALU.add)
+            if n > 0:
+                nc.vector.tensor_reduce(out=t[:, W : W + 1], in_=bank(n, 0)[:, 0:TRI], axis=AXIS_X, op=ALU.max)
+                for half in range(2):
+                    nc.vector.tensor_reduce(
+                        out=t[:, half * (W // 2) : (half + 1) * (W // 2)],
+                        in_=bank(n, 1 + half)[:].rearrange("p (k j) -> p k j", j=W),
+                        axis=AXIS_X,
+                        op=ALU.max,
+                    )
+            nc.vector.tensor_reduce(out=t[:, W + 1 : W + 2], in_=own_open[:], axis=AXIS_X, op=ALU.max)
+            nc.vector.tensor_tensor(out=tops_open[:], in0=t[:], in1=blocked[:], op=ALU.add)
+            nc.vector.tensor_reduce(out=top[:], in_=tops_open[:], axis=AXIS_X, op=ALU.max)
+            nc.vector.tensor_scalar(out=shift[n % 2][:], in0=top[:], scalar1=-INV_DH, scalar2=None, op0=ALU.mult)
+            nc.vector.tensor_scalar(
+                out=shift_k[n % 2][:], in0=blocked[:, 0:W], scalar1=shift[n % 2][:, 0:1], scalar2=None, op0=ALU.add
+            )
+
+        def exponentials(n):
+            i = n % 2
+            if n > 0:
+                for k in range(1, W):
+                    nc.scalar.activation(
+                        out=exp_old[i][:, k, 0:k],
+                        in_=bank(n, 0)[:, first_pair(k) : first_pair(k) + k],
+                        func=ACT.Exp,
+                        bias=shift[i][:, 0:1],
+                        scale=INV_DH,
+                        accum_out=sums[i][:, 2 * W + k : 2 * W + k + 1],
+                    )
+                for k in range(W):
+                    first = (k % (W // 2)) * W
+                    nc.scalar.activation(
+                        out=exp_own[i][:, k, 0:W],
+                        in_=bank(n, 1 + k // (W // 2))[:, first : first + W],
+                        func=ACT.Exp,
+                        bias=shift_k[i][:, k : k + 1],
+                        scale=INV_DH,
+                        accum_out=k_sums[i][:, k : k + 1],
+                    )
+            for k in range(1, W):
+                nc.scalar.activation(
+                    out=exp_own[i][:, k, W : W + k],
+                    in_=bank(n, 3)[:, first_pair(k) : first_pair(k) + k],
+                    func=ACT.Exp,
+                    bias=shift_k[i][:, k : k + 1],
+                    scale=INV_DH,
+                    accum_out=k_sums[i][:, W + k : W + k + 1],
+                )
+            nc.scalar.activation(
+                out=masked_exp[i][:], in_=shift[i][:], func=ACT.Exp, bias=ignore_col[:, 0:1], scale=1.0
+            )
+
+        def pair_sums(n):
+            i = n % 2
+            own, old = exp_own[i][:], exp_old[i][:]
+            rows, done = W, 0
+            for level in range(5):
+                rows = rows // 2
+                own_next = sums[i][:, 0 : 2 * W].unsqueeze(1) if rows == 1 else half_own[:, done : done + rows, :]
+                old_next = half_old[:, done : done + rows, :]
+                nc.vector.tensor_tensor(out=own_next, in0=own[:, 0:rows, :], in1=own[:, rows : 2 * rows, :], op=ALU.add)
+                nc.vector.tensor_tensor(out=old_next, in0=old[:, 0:rows, :], in1=old[:, rows : 2 * rows, :], op=ALU.add)
+                own, old, done = own_next, old_next, done + rows
+            nc.vector.tensor_tensor(
+                out=sums[i][:, 3 * W : 4 * W], in0=k_sums[i][:, 0:W], in1=k_sums[i][:, W : 2 * W], op=ALU.add
+            )
+            nc.vector.tensor_tensor(out=sums[i][:, 0:W], in0=sums[i][:, 0:W], in1=old[:, 0, :], op=ALU.add)
+
+        def normalise(n):
+            i = n % 2
+            masked = masked_first if n == 0 else masked_later
+            nc.vector.scalar_tensor_tensor(
+                out=full[i][:], in0=masked[:], scalar=masked_exp[i][:, 0:1], in1=sums[i][:], op0=ALU.mult, op1=ALU.add
+            )
+            nc.vector.tensor_reduce(out=total[:], in_=full[i][:, 0 : 2 * W], axis=AXIS_X, op=ALU.add)
+            nc.vector.reciprocal(out=scale[i][:], in_=total[:])
+            nc.scalar.activation(out=result[:, n, :], in_=full[i][:], func=ACT.Copy, scale=scale[i][:, 0:1])
+
+        def store_outputs():
+            for x in range(X):
+                rows = slice(x * W, (x + 1) * W)
+                nc.sync.dma_start(out=out_0[x].rearrange("n i j -> i n j"), in_=result[rows, :, 0 : 2 * W])
+                nc.scalar.dma_start(out=out_1[x].rearrange("n i k -> i n k"), in_=result[rows, :, 2 * W : 4 * W])
+
+        with tc.manual_schedule():
+            load_inputs()
+            count_rows_and_columns()
+            zero_what_stays_zero()
+            build_constants()
+            prepare_window(0)
+            quantise_queries(0)
+            for n in range(NW + 2):
+                keys = n < NW
+                if n + 1 < NW:
+                    prepare_window(n + 1)
+                if keys and n > 0:
+                    score_same(n, 0, n - 1)
+                    cross_product(n, 0)
+                if 1 <= n <= NW:
+                    row_max(n - 1)
+                    exponentials(n - 1)
+                if n >= 2:
+                    pair_sums(n - 2)
+                    normalise(n - 2)
+                if keys and n > 0:
+                    for x in range(1, X):
+                        cross_product(n, x)
+                        cross_quantise_and_score(n, x - 1)
+                if keys:
+                    same_products(n)
+                    if n > 0:
+                        cross_quantise_and_score(n, X - 1)
+                    same_quantise(n)
+                    score_same(n, 3, n)
+                if n + 1 < NW:
+                    quantise_queries(n + 1)
+            store_outputs()

@@ -23,9 +23,11 @@ TRI = W * (W - 1) // 2
 TRI_PAD = 512
 BANK = 512
 SCORE_BANKS = 7
+OLD, CROSS_LOW, CROSS_HIGH, OWN = 0, 1, 2, 3
 IGNORE = -1000000.0
 INV_DH = 1.0 / DH
 BLOCKED = -1.0e30
+ROWS_BEFORE_SMALL = 3
 
 FLOPS = 2 * W * DH * (X * NW * TRI + X * (NW - 1) * TRI + X * (NW - 1) * W * W)
 
@@ -63,17 +65,15 @@ def tile_localtrittention_pa_kernel(tc, a, b, c, out_0, out_1):
         banks = [psum.tile([P, BANK], F32, name="bank%d" % i) for i in range(SCORE_BANKS)]
         turned = psum.tile([P, BANK], F32, name="turned")
 
-        exp_own = [keep.tile([P, W, 2 * W], F32, name="exp_own%d" % i) for i in range(2)]
-        exp_old = [keep.tile([P, W, W], F32, name="exp_old%d" % i) for i in range(2)]
-        half_own = keep.tile([P, W - 2, 2 * W], F32, name="half_own")
-        half_old = keep.tile([P, W - 1, W], F32, name="half_old")
+        exp_old_j = [keep.tile([P, 2 * W, W], F32, name="exp_old_j%d" % i) for i in range(2)]
+        exp_own_j = [keep.tile([P, W, W], F32, name="exp_own_j%d" % i) for i in range(2)]
+        unread = keep.tile([P, W * W + 2 * TRI], F32, name="unread")
 
         tops = [keep.tile([P, W + 3], F32, name="tops%d" % i) for i in range(2)]
         tops_open = keep.tile([P, W + 3], F32, name="tops_open")
         own_open = keep.tile([P, TRI], F32, name="own_open")
         top = keep.tile([P, 1], F32, name="top")
-        shift = [keep.tile([P, 1], F32, name="shift%d" % i) for i in range(2)]
-        shift_k = [keep.tile([P, W], F32, name="shift_k%d" % i) for i in range(2)]
+        shift = [keep.tile([P, W + 1], F32, name="shift%d" % i) for i in range(2)]
         masked_exp = [keep.tile([P, 1], F32, name="masked_exp%d" % i) for i in range(2)]
         k_sums = [keep.tile([P, 2 * W], F32, name="k_sums%d" % i) for i in range(2)]
         sums = [keep.tile([P, 4 * W], F32, name="sums%d" % i) for i in range(2)]
@@ -105,22 +105,20 @@ def tile_localtrittention_pa_kernel(tc, a, b, c, out_0, out_1):
                     for x in range(X):
                         nc.sync.dma_start(out=raw[name][x * W : (x + 1) * W, n, :], in_=src[x, n])
 
-        def zero_what_stays_zero():
+        def count_rows_and_columns():
+            for x in range(X):
+                nc.gpsimd.iota(i_minus_c_int[x * W : (x + 1) * W, :], pattern=[[-1, W]], base=0, channel_multiplier=1)
+            nc.gpsimd.iota(col_int[:], pattern=[[1, W]], base=0, channel_multiplier=0)
+
+        def fill_what_is_never_written():
             for i in range(2):
                 nc.vector.memset(c_wide[i][:].bitcast(I32), 0)
-                nc.gpsimd.memset(exp_own[i][:], 0.0)
-                nc.gpsimd.memset(exp_old[i][:], 0.0)
                 nc.vector.memset(k_sums[i][:], 0.0)
                 nc.vector.memset(sums[i][:], 0.0)
                 nc.vector.memset(tops[i][:, 0 : W + 2], BLOCKED)
                 nc.vector.memset(tops[i][:, W + 2 : W + 3], IGNORE)
             nc.vector.memset(same_keys[:, :, TRI:TRI_PAD, :], 0.0)
             nc.vector.memset(ignore_col[:], IGNORE * INV_DH)
-
-        def count_rows_and_columns():
-            for x in range(X):
-                nc.gpsimd.iota(i_minus_c_int[x * W : (x + 1) * W, :], pattern=[[-1, W]], base=0, channel_multiplier=1)
-            nc.gpsimd.iota(col_int[:], pattern=[[1, W]], base=0, channel_multiplier=0)
 
         def build_constants():
             nc.vector.tensor_copy(out=i_minus_c[:], in_=i_minus_c_int[:])
@@ -205,22 +203,24 @@ def tile_localtrittention_pa_kernel(tc, a, b, c, out_0, out_1):
                 scales=cross_scales[x][:],
                 in_=cross_keys[x % 3][:].rearrange("p k j t -> p (k j t)"),
             )
-            for half in range(2):
+            for half, region in enumerate((CROSS_LOW, CROSS_HIGH)):
                 cols = slice(half * BANK, (half + 1) * BANK)
-                score_pass(n, 1 + half, x, cross_codes[x][:, cols], cross_scales[x][:, cols])
+                score_pass(n, region, x, cross_codes[x][:, cols], cross_scales[x][:, cols])
 
-        def same_products(n):
+        def same_products(n, small):
             a_win = a_t[:, n].rearrange("p (x w) t -> p x w t", x=X)
             b_win = b_t[:, n].rearrange("p (x w) t -> p x w t", x=X)
-            for k in range(1, W):
+            for row, k in enumerate(reversed(range(1, W))):
                 nc.vector.tensor_tensor(
                     out=same_keys[:, :, first_pair(k) : first_pair(k) + k, :],
                     in0=a_win[:, :, 0:k, :],
                     in1=b_win[:, :, k : k + 1, :].to_broadcast([P, X, k, PACK]),
                     op=ALU.mult,
                 )
+                if 0 <= row - ROWS_BEFORE_SMALL < len(small):
+                    small[row - ROWS_BEFORE_SMALL]()
 
-        def same_quantise(n):
+        def same_quantise_and_score(n):
             for half in range(2):
                 heads = slice(2 * half, 2 * half + 2)
                 nc.vector.quantize_mx(
@@ -228,91 +228,129 @@ def tile_localtrittention_pa_kernel(tc, a, b, c, out_0, out_1):
                     scales=same_scales[n % 2][:, heads, :].rearrange("p x c -> p (x c)"),
                     in_=same_keys[:, heads, :, :].rearrange("p x c t -> p (x c t)"),
                 )
+            score_same(n, OWN, n)
 
         def score_same(n, region, key_window):
             for x in range(X):
                 score_pass(n, region, x, same_codes[key_window % 2][:, x, :], same_scales[key_window % 2][:, x, :])
 
-        def row_max(n):
-            t = tops[n % 2]
-            nc.vector.tensor_tensor(out=own_open[:], in0=bank(n, 3)[:, 0:TRI], in1=blocked_own[:], op=ALU.add)
-            if n > 0:
-                nc.vector.tensor_reduce(out=t[:, W : W + 1], in_=bank(n, 0)[:, 0:TRI], axis=AXIS_X, op=ALU.max)
-                for half in range(2):
-                    nc.vector.tensor_reduce(
-                        out=t[:, half * (W // 2) : (half + 1) * (W // 2)],
-                        in_=bank(n, 1 + half)[:].rearrange("p (k j) -> p k j", j=W),
-                        axis=AXIS_X,
-                        op=ALU.max,
-                    )
-            nc.vector.tensor_reduce(out=t[:, W + 1 : W + 2], in_=own_open[:], axis=AXIS_X, op=ALU.max)
-            nc.vector.tensor_tensor(out=tops_open[:], in0=t[:], in1=blocked[:], op=ALU.add)
+        def open_own(n):
+            nc.vector.tensor_tensor(out=own_open[:], in0=bank(n, OWN)[:, 0:TRI], in1=blocked_own[:], op=ALU.add)
+
+        def top_of_old(n):
+            nc.vector.tensor_reduce(out=tops[n % 2][:, W : W + 1], in_=bank(n, OLD)[:, 0:TRI], axis=AXIS_X, op=ALU.max)
+
+        def top_of_own(n):
+            nc.vector.tensor_reduce(out=tops[n % 2][:, W + 1 : W + 2], in_=own_open[:], axis=AXIS_X, op=ALU.max)
+
+        def tops_of_cross(n, region, first_k):
+            nc.vector.tensor_reduce(
+                out=tops[n % 2][:, first_k : first_k + W // 2],
+                in_=bank(n, region)[:].rearrange("p (k j) -> p k j", j=W),
+                axis=AXIS_X,
+                op=ALU.max,
+            )
+
+        def open_tops(n):
+            nc.vector.tensor_tensor(out=tops_open[:], in0=tops[n % 2][:], in1=blocked[:], op=ALU.add)
+
+        def top_of_all():
             nc.vector.tensor_reduce(out=top[:], in_=tops_open[:], axis=AXIS_X, op=ALU.max)
-            nc.vector.tensor_scalar(out=shift[n % 2][:], in0=top[:], scalar1=-INV_DH, scalar2=None, op0=ALU.mult)
+
+        def shifts(n):
             nc.vector.tensor_scalar(
-                out=shift_k[n % 2][:], in0=blocked[:, 0:W], scalar1=shift[n % 2][:, 0:1], scalar2=None, op0=ALU.add
+                out=shift[n % 2][:],
+                in0=blocked[:, 0 : W + 1],
+                scalar1=top[:, 0:1],
+                scalar2=INV_DH,
+                op0=ALU.subtract,
+                op1=ALU.mult,
+            )
+
+        def exponential(n, region, first_col, width, shift_col, out, accum_out):
+            nc.scalar.activation(
+                out=out,
+                in_=bank(n, region)[:, first_col : first_col + width],
+                func=ACT.Exp,
+                bias=shift[n % 2][:, shift_col : shift_col + 1],
+                scale=INV_DH,
+                accum_out=accum_out,
             )
 
         def exponentials(n):
             i = n % 2
             if n > 0:
                 for k in range(1, W):
-                    nc.scalar.activation(
-                        out=exp_old[i][:, k, 0:k],
-                        in_=bank(n, 0)[:, first_pair(k) : first_pair(k) + k],
-                        func=ACT.Exp,
-                        bias=shift[i][:, 0:1],
-                        scale=INV_DH,
-                        accum_out=sums[i][:, 2 * W + k : 2 * W + k + 1],
-                    )
+                    exponential(n, OLD, first_pair(k), k, W, exp_old_j[i][:, k, 0:k], sums[i][:, 2 * W + k : 2 * W + k + 1])
                 for k in range(W):
-                    first = (k % (W // 2)) * W
-                    nc.scalar.activation(
-                        out=exp_own[i][:, k, 0:W],
-                        in_=bank(n, 1 + k // (W // 2))[:, first : first + W],
-                        func=ACT.Exp,
-                        bias=shift_k[i][:, k : k + 1],
-                        scale=INV_DH,
-                        accum_out=k_sums[i][:, k : k + 1],
-                    )
+                    region = CROSS_LOW if k < W // 2 else CROSS_HIGH
+                    exponential(n, region, (k % (W // 2)) * W, W, k, exp_old_j[i][:, W + k, :], k_sums[i][:, k : k + 1])
             for k in range(1, W):
-                nc.scalar.activation(
-                    out=exp_own[i][:, k, W : W + k],
-                    in_=bank(n, 3)[:, first_pair(k) : first_pair(k) + k],
-                    func=ACT.Exp,
-                    bias=shift_k[i][:, k : k + 1],
-                    scale=INV_DH,
-                    accum_out=k_sums[i][:, W + k : W + k + 1],
-                )
+                exponential(n, OWN, first_pair(k), k, k, exp_own_j[i][:, k, 0:k], k_sums[i][:, W + k : W + k + 1])
             nc.scalar.activation(
-                out=masked_exp[i][:], in_=shift[i][:], func=ACT.Exp, bias=ignore_col[:, 0:1], scale=1.0
+                out=masked_exp[i][:], in_=shift[i][:, W : W + 1], func=ACT.Exp, bias=ignore_col[:, 0:1], scale=1.0
             )
 
-        def pair_sums(n):
+        def sums_over_k(n):
             i = n % 2
-            own, old = exp_own[i][:], exp_old[i][:]
-            rows, done = W, 0
-            for level in range(5):
-                rows = rows // 2
-                own_next = sums[i][:, 0 : 2 * W].unsqueeze(1) if rows == 1 else half_own[:, done : done + rows, :]
-                old_next = half_old[:, done : done + rows, :]
-                nc.vector.tensor_tensor(out=own_next, in0=own[:, 0:rows, :], in1=own[:, rows : 2 * rows, :], op=ALU.add)
-                nc.vector.tensor_tensor(out=old_next, in0=old[:, 0:rows, :], in1=old[:, rows : 2 * rows, :], op=ALU.add)
-                own, old, done = own_next, old_next, done + rows
+            used = 0
+            for j in range(W):
+                if n > 0:
+                    nc.scalar.activation(
+                        out=unread[:, used : used + 2 * W - 1 - j],
+                        in_=exp_old_j[i][:, j + 1 : 2 * W, j],
+                        func=ACT.Copy,
+                        accum_out=sums[i][:, j : j + 1],
+                    )
+                    used += 2 * W - 1 - j
+                if j < W - 1:
+                    nc.scalar.activation(
+                        out=unread[:, used : used + W - 1 - j],
+                        in_=exp_own_j[i][:, j + 1 : W, j],
+                        func=ACT.Copy,
+                        accum_out=sums[i][:, W + j : W + j + 1],
+                    )
+                    used += W - 1 - j
+
+        def join_k_sums(n):
+            i = n % 2
             nc.vector.tensor_tensor(
                 out=sums[i][:, 3 * W : 4 * W], in0=k_sums[i][:, 0:W], in1=k_sums[i][:, W : 2 * W], op=ALU.add
             )
-            nc.vector.tensor_tensor(out=sums[i][:, 0:W], in0=sums[i][:, 0:W], in1=old[:, 0, :], op=ALU.add)
 
-        def normalise(n):
+        def add_masked_pairs(n):
             i = n % 2
             masked = masked_first if n == 0 else masked_later
             nc.vector.scalar_tensor_tensor(
                 out=full[i][:], in0=masked[:], scalar=masked_exp[i][:, 0:1], in1=sums[i][:], op0=ALU.mult, op1=ALU.add
             )
-            nc.vector.tensor_reduce(out=total[:], in_=full[i][:, 0 : 2 * W], axis=AXIS_X, op=ALU.add)
-            nc.vector.reciprocal(out=scale[i][:], in_=total[:])
-            nc.scalar.activation(out=result[:, n, :], in_=full[i][:], func=ACT.Copy, scale=scale[i][:, 0:1])
+
+        def sum_of_all(n):
+            nc.vector.tensor_reduce(out=total[:], in_=full[n % 2][:, 0 : 2 * W], axis=AXIS_X, op=ALU.add)
+
+        def invert_sum(n):
+            nc.vector.reciprocal(out=scale[n % 2][:], in_=total[:])
+
+        def normalise(n):
+            nc.scalar.activation(out=result[:, n, :], in_=full[n % 2][:], func=ACT.Copy, scale=scale[n % 2][:, 0:1])
+
+        def small_instructions(n):
+            chain_1, chain_2 = [], []
+            if 1 <= n - 1 < NW:
+                chain_1 += [lambda: tops_of_cross(n - 1, CROSS_LOW, 0), lambda: tops_of_cross(n - 1, CROSS_HIGH, W // 2)]
+            if 0 <= n - 1 < NW:
+                chain_1 += [lambda: open_tops(n - 1), top_of_all, lambda: shifts(n - 1)]
+            if 0 <= n - 2:
+                chain_2 += [
+                    lambda: join_k_sums(n - 2),
+                    lambda: add_masked_pairs(n - 2),
+                    lambda: sum_of_all(n - 2),
+                    lambda: invert_sum(n - 2),
+                ]
+            mixed = []
+            for place in range(max(len(chain_1), len(chain_2))):
+                mixed += chain_1[place : place + 1] + chain_2[place : place + 1]
+            return mixed
 
         def store_outputs():
             for x in range(X):
@@ -323,33 +361,41 @@ def tile_localtrittention_pa_kernel(tc, a, b, c, out_0, out_1):
         with tc.manual_schedule():
             load_inputs()
             count_rows_and_columns()
-            zero_what_stays_zero()
+            fill_what_is_never_written()
             build_constants()
             prepare_window(0)
-            quantise_queries(0)
             for n in range(NW + 2):
-                keys = n < NW
+                small = small_instructions(n)
                 if n + 1 < NW:
                     prepare_window(n + 1)
-                if keys and n > 0:
-                    score_same(n, 0, n - 1)
-                    cross_product(n, 0)
-                if 1 <= n <= NW:
-                    row_max(n - 1)
+                if n < NW:
+                    if n > 0:
+                        score_same(n, OLD, n - 1)
+                    same_products(n, small)
+                else:
+                    for instruction in small:
+                        instruction()
+                if 0 <= n - 1 < NW:
                     exponentials(n - 1)
-                if n >= 2:
-                    pair_sums(n - 2)
+                    sums_over_k(n - 1)
+                if 0 <= n - 2:
                     normalise(n - 2)
-                if keys and n > 0:
-                    for x in range(1, X):
-                        cross_product(n, x)
-                        cross_quantise_and_score(n, x - 1)
-                if keys:
-                    same_products(n)
+                if n < NW:
+                    if n > 0:
+                        cross_product(n, 0)
+                    else:
+                        quantise_queries(0)
+                    same_quantise_and_score(n)
+                    if n > 0:
+                        for x in range(1, X):
+                            cross_product(n, x)
+                            cross_quantise_and_score(n, x - 1)
+                    open_own(n)
+                    if n > 0:
+                        top_of_old(n)
+                    top_of_own(n)
                     if n > 0:
                         cross_quantise_and_score(n, X - 1)
-                    same_quantise(n)
-                    score_same(n, 3, n)
                 if n + 1 < NW:
                     quantise_queries(n + 1)
             store_outputs()

@@ -19,21 +19,29 @@ X = 4
 NW = 10
 W = 32
 DH = 512
-TRI = W * (W - 1) // 2
-TRI_PAD = 512
+HALF = W // 2
 BANK = 512
-SCORE_BANKS = 7
-OLD, CROSS_LOW, CROSS_HIGH, OWN = 0, 1, 2, 3
+CHUNKS = BANK // P
+LOW_PAIRS = HALF * (HALF - 1) // 2
+GAP = P - LOW_PAIRS
+SAME_END = W * (W - 1) // 2 + GAP
+SCORE_BANKS = 5
+OLD, OWN, CROSS_LOW, CROSS_HIGH = 0, 1, 2, 3
+SAME, LOW, HIGH = 0, 1, 2
+LAYOUT = {OLD: SAME, OWN: SAME, CROSS_LOW: LOW, CROSS_HIGH: HIGH}
+UNUSED_ONLY, CAUSAL = 0, 1
+MASK = {OLD: UNUSED_ONLY, OWN: CAUSAL, CROSS_LOW: CAUSAL, CROSS_HIGH: CAUSAL}
+PA_OLD, PA_OWN, PB_OLD, PB_OWN = 0, W, 2 * W, 3 * W
 IGNORE = -1000000.0
 INV_DH = 1.0 / DH
-BLOCKED = -1.0e30
+MASKED = -(2.0**100)
 ROWS_BEFORE_SMALL = 3
 
-FLOPS = 2 * W * DH * (X * NW * TRI + X * (NW - 1) * TRI + X * (NW - 1) * W * W)
+FLOPS = 2 * W * DH * X * (NW * W * (W - 1) // 2 + (NW - 1) * W * (W - 1) // 2 + (NW - 1) * W * W)
 
 
 def first_pair(k):
-    return k * (k - 1) // 2
+    return k * (k - 1) // 2 + (GAP if k >= HALF else 0)
 
 
 def tile_localtrittention_pa_kernel(tc, a, b, c, out_0, out_1):
@@ -58,38 +66,42 @@ def tile_localtrittention_pa_kernel(tc, a, b, c, out_0, out_1):
         cross_keys = [keep.tile([P, W, W, PACK], BF16, name="cross_keys%d" % i, align_bytes=64) for i in range(3)]
         cross_codes = [keep.tile([P, W * W], U32, name="cross_codes%d" % i, align_bytes=64) for i in range(X)]
         cross_scales = [keep.tile([P, W * W], U8, name="cross_scales%d" % i, align_bytes=64) for i in range(X)]
-        same_keys = keep.tile([P, X, TRI_PAD, PACK], BF16, name="same_keys", align_bytes=64)
-        same_codes = [keep.tile([P, X, TRI_PAD], U32, name="same_codes%d" % i, align_bytes=64) for i in range(2)]
-        same_scales = [keep.tile([P, X, TRI_PAD], U8, name="same_scales%d" % i, align_bytes=64) for i in range(2)]
+        same_keys = keep.tile([P, X, BANK, PACK], BF16, name="same_keys", align_bytes=64)
+        same_codes = [keep.tile([P, X, BANK], U32, name="same_codes%d" % i, align_bytes=64) for i in range(2)]
+        same_scales = [keep.tile([P, X, BANK], U8, name="same_scales%d" % i, align_bytes=64) for i in range(2)]
 
         banks = [psum.tile([P, BANK], F32, name="bank%d" % i) for i in range(SCORE_BANKS)]
-        turned = psum.tile([P, BANK], F32, name="turned")
+        turned = [psum.tile([P, BANK], F32, name="turned%d" % i) for i in range(2)]
+        sums = psum.tile([P, BANK], F32, name="sums")
 
-        exp_old_j = [keep.tile([P, 2 * W, W], F32, name="exp_old_j%d" % i) for i in range(2)]
-        exp_own_j = [keep.tile([P, W, W], F32, name="exp_own_j%d" % i) for i in range(2)]
-        unread = keep.tile([P, W * W + 2 * TRI], F32, name="unread")
+        exps = keep.tile([P, 4, BANK], F32, name="exps")
+        exps_t = keep.tile([P, 4, BANK], F32, name="exps_t")
+        names = keep.tile([P, 3, BANK], F32, name="names")
+        pick = keep.tile([P, 3, CHUNKS, 2 * W], F32, name="pick")
+        mask_keys = keep.tile([P, 3, BANK, PACK], BF16, name="mask_keys", align_bytes=64)
+        mask_key_codes = keep.tile([P, 3, BANK], U32, name="mask_key_codes", align_bytes=64)
+        mask_key_scales = keep.tile([P, 3, BANK], U8, name="mask_key_scales", align_bytes=64)
+        mask_queries = keep.tile([P, 2, P, PACK], BF16, name="mask_queries", align_bytes=64)
+        mask_query_codes = keep.tile([P, 2, P], U32, name="mask_query_codes", align_bytes=64)
+        mask_query_scales = keep.tile([P, 2, P], U8, name="mask_query_scales", align_bytes=64)
 
-        tops = [keep.tile([P, W + 3], F32, name="tops%d" % i) for i in range(2)]
-        tops_open = keep.tile([P, W + 3], F32, name="tops_open")
-        own_open = keep.tile([P, TRI], F32, name="own_open")
+        tops = [keep.tile([P, 5], F32, name="tops%d" % i) for i in range(2)]
         top = keep.tile([P, 1], F32, name="top")
-        shift = [keep.tile([P, W + 1], F32, name="shift%d" % i) for i in range(2)]
+        shift = [keep.tile([P, 1], F32, name="shift%d" % i) for i in range(2)]
         masked_exp = [keep.tile([P, 1], F32, name="masked_exp%d" % i) for i in range(2)]
-        k_sums = [keep.tile([P, 2 * W], F32, name="k_sums%d" % i) for i in range(2)]
-        sums = [keep.tile([P, 4 * W], F32, name="sums%d" % i) for i in range(2)]
         full = [keep.tile([P, 4 * W], F32, name="full%d" % i) for i in range(2)]
         total = keep.tile([P, 1], F32, name="total")
         scale = [keep.tile([P, 1], F32, name="scale%d" % i) for i in range(2)]
         result = keep.tile([P, NW, 4 * W], F32, name="result")
 
+        p_minus_c_int = keep.tile([P, W], I32, name="p_minus_c_int")
+        p_minus_c = keep.tile([P, W], F32, name="p_minus_c")
         i_minus_c_int = keep.tile([P, W], I32, name="i_minus_c_int")
         col_int = keep.tile([P, W], I32, name="col_int")
         i_minus_c = keep.tile([P, W], F32, name="i_minus_c")
         col = keep.tile([P, W], F32, name="col")
         seen = keep.tile([P, W], F32, name="seen")
         work = keep.tile([P, W], F32, name="work")
-        blocked = keep.tile([P, W + 3], F32, name="blocked")
-        blocked_own = keep.tile([P, TRI], F32, name="blocked_own")
         ignore_col = keep.tile([P, 1], F32, name="ignore_col")
         masked_first = keep.tile([P, 4 * W], F32, name="masked_first")
         masked_later = keep.tile([P, 4 * W], F32, name="masked_later")
@@ -98,6 +110,9 @@ def tile_localtrittention_pa_kernel(tc, a, b, c, out_0, out_1):
 
         def bank(n, region):
             return banks[(4 * n + region) % SCORE_BANKS]
+
+        def regions(n):
+            return (OWN,) if n == 0 else (OLD, OWN, CROSS_LOW, CROSS_HIGH)
 
         def load_inputs():
             for n in range(NW):
@@ -109,30 +124,23 @@ def tile_localtrittention_pa_kernel(tc, a, b, c, out_0, out_1):
             for x in range(X):
                 nc.gpsimd.iota(i_minus_c_int[x * W : (x + 1) * W, :], pattern=[[-1, W]], base=0, channel_multiplier=1)
             nc.gpsimd.iota(col_int[:], pattern=[[1, W]], base=0, channel_multiplier=0)
+            nc.gpsimd.iota(p_minus_c_int[:], pattern=[[-1, W]], base=0, channel_multiplier=1)
 
         def fill_what_is_never_written():
             for i in range(2):
                 nc.vector.memset(c_wide[i][:].bitcast(I32), 0)
-                nc.vector.memset(k_sums[i][:], 0.0)
-                nc.vector.memset(sums[i][:], 0.0)
-                nc.vector.memset(tops[i][:, 0 : W + 2], BLOCKED)
-                nc.vector.memset(tops[i][:, W + 2 : W + 3], IGNORE)
-            nc.vector.memset(same_keys[:, :, TRI:TRI_PAD, :], 0.0)
+                nc.vector.memset(tops[i][:, 0:4], MASKED)
+                nc.vector.memset(tops[i][:, 4:5], IGNORE)
+            nc.vector.memset(same_keys[:, :, LOW_PAIRS:P, :], 0.0)
+            nc.vector.memset(same_keys[:, :, SAME_END:BANK, :], 0.0)
+            nc.vector.memset(mask_keys[:].bitcast(I32), 0)
+            nc.vector.memset(mask_queries[:].bitcast(I32), 0)
             nc.vector.memset(ignore_col[:], IGNORE * INV_DH)
 
         def build_constants():
             nc.vector.tensor_copy(out=i_minus_c[:], in_=i_minus_c_int[:])
             nc.vector.tensor_copy(out=col[:], in_=col_int[:])
             nc.vector.tensor_scalar(out=seen[:], in0=i_minus_c[:], scalar1=0.0, scalar2=None, op0=ALU.is_ge)
-            nc.vector.memset(blocked[:, W : W + 3], 0.0)
-            nc.vector.tensor_scalar(
-                out=blocked[:, 0:W], in0=seen[:], scalar1=1.0, scalar2=-BLOCKED, op0=ALU.subtract, op1=ALU.mult
-            )
-            for k in range(1, W):
-                nc.vector.tensor_copy(
-                    out=blocked_own[:, first_pair(k) : first_pair(k) + k],
-                    in_=blocked[:, k : k + 1].to_broadcast([P, k]),
-                )
             nc.vector.tensor_scalar(
                 out=masked_later[:, 0:W], in0=i_minus_c[:], scalar1=-1.0, scalar2=1.0 * W, op0=ALU.mult, op1=ALU.add
             )
@@ -151,20 +159,84 @@ def tile_localtrittention_pa_kernel(tc, a, b, c, out_0, out_1):
                 out=masked_first[:, 3 * W : 4 * W], in0=work[:], scalar1=-1.0, scalar2=2.0 * W, op0=ALU.mult, op1=ALU.add
             )
 
-        def turn(name, n, first_col):
+        def name_the_pairs():
+            for k in range(1, W):
+                nc.vector.tensor_scalar(
+                    out=names[:, SAME, first_pair(k) : first_pair(k) + k],
+                    in0=ident[:, 0:k],
+                    scalar1=ident[:, W + k : W + k + 1],
+                    scalar2=None,
+                    op0=ALU.add,
+                )
+            for cols in (slice(LOW_PAIRS, P), slice(SAME_END, BANK)):
+                nc.vector.tensor_copy(out=names[:, SAME, cols], in_=ident[:, 2 * W : 2 * W + 1].to_broadcast([P, GAP]))
+            for layout, first_k in ((LOW, 0), (HIGH, HALF)):
+                nc.vector.tensor_tensor(
+                    out=names[:, layout, :].rearrange("p (k j) -> p k j", j=W),
+                    in0=ident[:, 0:W].unsqueeze(1).to_broadcast([P, HALF, W]),
+                    in1=ident[:, W + first_k : W + first_k + HALF].unsqueeze(2).to_broadcast([P, HALF, W]),
+                    op=ALU.add,
+                )
+
+        def turn_the_names():
+            for layout in (SAME, LOW, HIGH):
+                for chunk in range(CHUNKS):
+                    cols = slice(chunk * P, (chunk + 1) * P)
+                    nc.tensor.transpose(turned[layout % 2][:, cols], names[:, layout, cols], ident[:])
+                nc.scalar.copy(
+                    out=pick[:, layout], in_=turned[layout % 2][:].rearrange("p (c r) -> p c r", r=P)[:, :, 0 : 2 * W]
+                )
+
+        def build_the_masks():
+            nc.scalar.activation(
+                out=mask_keys[:].rearrange("p l c t -> p (l c) t")[:, :, 0],
+                in_=names[:].rearrange("p l c -> p (l c)"),
+                func=ACT.Copy,
+                scale=MASKED,
+            )
+            nc.vector.tensor_copy(out=p_minus_c[:], in_=p_minus_c_int[:])
+            nc.vector.tensor_scalar(
+                out=mask_queries[:, CAUSAL].rearrange("p (x i) t -> p x i t", x=X)[:, :, :, 0],
+                in0=p_minus_c[:].unsqueeze(1).to_broadcast([P, X, W]),
+                scalar1=1.0 * W,
+                scalar2=None,
+                op0=ALU.is_gt,
+            )
+            nc.vector.tensor_scalar(
+                out=mask_queries[:, UNUSED_ONLY, :, 0],
+                in0=p_minus_c[:, W - 1 : W].to_broadcast([P, P]),
+                scalar1=1.0 * W,
+                scalar2=None,
+                op0=ALU.is_gt,
+            )
+
+        def quantise_the_masks():
+            nc.vector.quantize_mx(
+                out=mask_query_codes[:].rearrange("p m q -> p (m q)").bitcast(FP8X4),
+                scales=mask_query_scales[:].rearrange("p m q -> p (m q)"),
+                in_=mask_queries[:].rearrange("p m q t -> p (m q t)"),
+            )
+            for layout in (SAME, LOW, HIGH):
+                nc.vector.quantize_mx(
+                    out=mask_key_codes[:, layout, :].bitcast(FP8X4),
+                    scales=mask_key_scales[:, layout, :],
+                    in_=mask_keys[:, layout].rearrange("p c t -> p (c t)"),
+                )
+
+        def turn_input(name, n, place, first_col):
             words = raw[name][:, n, :].bitcast(F32)
             for u in range(2):
                 nc.tensor.transpose(
-                    turned[:, first_col + u * P : first_col + (u + 1) * P], words[:, u * P : (u + 1) * P], ident[:]
+                    turned[place][:, first_col + u * P : first_col + (u + 1) * P], words[:, u * P : (u + 1) * P], ident[:]
                 )
-            return turned[:, first_col : first_col + 2 * P].rearrange("p (u r) -> p r u", u=2)
+            return turned[place][:, first_col : first_col + 2 * P].rearrange("p (u r) -> p r u", u=2)
 
         def prepare_window(n):
-            a_words = turn("a", n, 0)
-            b_words = turn("b", n, 2 * P)
+            a_words = turn_input("a", n, 0, 0)
+            b_words = turn_input("b", n, 0, 2 * P)
+            c_words = turn_input("c", n, 1, 0)
             nc.scalar.copy(out=a_t[:, n].bitcast(F32), in_=a_words)
             nc.scalar.copy(out=b_t[:, n].bitcast(F32), in_=b_words)
-            c_words = turn("c", n, 0)
             for x in range(X):
                 rows = slice(x * W, (x + 1) * W)
                 nc.scalar.copy(out=c_wide[n % 2][:, x, rows, :].bitcast(F32), in_=c_words[:, rows, :])
@@ -176,6 +248,17 @@ def tile_localtrittention_pa_kernel(tc, a, b, c, out_0, out_1):
                 in_=c_wide[n % 2][:].rearrange("p x r t -> p (x r t)"),
             )
 
+        def open_bank(n, region):
+            nc.tensor.matmul_mx(
+                out=bank(n, region)[:],
+                lhsT=mask_query_codes[:, MASK[region], :].bitcast(FP8X4),
+                lhsT_scale=mask_query_scales[:, MASK[region], :],
+                rhs=mask_key_codes[:, LAYOUT[region], :].bitcast(FP8X4),
+                rhs_scale=mask_key_scales[:, LAYOUT[region], :],
+                start=True,
+                stop=False,
+            )
+
         def score_pass(n, region, x, codes, scales):
             cols = slice(x * P, (x + 1) * P)
             nc.tensor.matmul_mx(
@@ -184,7 +267,7 @@ def tile_localtrittention_pa_kernel(tc, a, b, c, out_0, out_1):
                 lhsT_scale=c_scales[n % 2][:, cols],
                 rhs=codes.bitcast(FP8X4),
                 rhs_scale=scales,
-                start=(x == 0),
+                start=False,
                 stop=(x == X - 1),
             )
 
@@ -205,6 +288,8 @@ def tile_localtrittention_pa_kernel(tc, a, b, c, out_0, out_1):
             )
             for half, region in enumerate((CROSS_LOW, CROSS_HIGH)):
                 cols = slice(half * BANK, (half + 1) * BANK)
+                if x == 0:
+                    open_bank(n, region)
                 score_pass(n, region, x, cross_codes[x][:, cols], cross_scales[x][:, cols])
 
         def same_products(n, small):
@@ -231,99 +316,93 @@ def tile_localtrittention_pa_kernel(tc, a, b, c, out_0, out_1):
             score_same(n, OWN, n)
 
         def score_same(n, region, key_window):
+            open_bank(n, region)
             for x in range(X):
                 score_pass(n, region, x, same_codes[key_window % 2][:, x, :], same_scales[key_window % 2][:, x, :])
 
-        def open_own(n):
-            nc.vector.tensor_tensor(out=own_open[:], in0=bank(n, OWN)[:, 0:TRI], in1=blocked_own[:], op=ALU.add)
-
-        def top_of_old(n):
-            nc.vector.tensor_reduce(out=tops[n % 2][:, W : W + 1], in_=bank(n, OLD)[:, 0:TRI], axis=AXIS_X, op=ALU.max)
-
-        def top_of_own(n):
-            nc.vector.tensor_reduce(out=tops[n % 2][:, W + 1 : W + 2], in_=own_open[:], axis=AXIS_X, op=ALU.max)
-
-        def tops_of_cross(n, region, first_k):
+        def top_of(n, region):
             nc.vector.tensor_reduce(
-                out=tops[n % 2][:, first_k : first_k + W // 2],
-                in_=bank(n, region)[:].rearrange("p (k j) -> p k j", j=W),
-                axis=AXIS_X,
-                op=ALU.max,
+                out=tops[n % 2][:, region : region + 1], in_=bank(n, region)[:], axis=AXIS_X, op=ALU.max
             )
 
-        def open_tops(n):
-            nc.vector.tensor_tensor(out=tops_open[:], in0=tops[n % 2][:], in1=blocked[:], op=ALU.add)
+        def top_of_all(n):
+            nc.vector.tensor_reduce(out=top[:], in_=tops[n % 2][:], axis=AXIS_X, op=ALU.max)
 
-        def top_of_all():
-            nc.vector.tensor_reduce(out=top[:], in_=tops_open[:], axis=AXIS_X, op=ALU.max)
+        def shift_by_top(n):
+            nc.vector.tensor_scalar(out=shift[n % 2][:], in0=top[:], scalar1=-INV_DH, scalar2=None, op0=ALU.mult)
 
-        def shifts(n):
-            nc.vector.tensor_scalar(
-                out=shift[n % 2][:],
-                in0=blocked[:, 0 : W + 1],
-                scalar1=top[:, 0:1],
-                scalar2=INV_DH,
-                op0=ALU.subtract,
-                op1=ALU.mult,
-            )
-
-        def exponential(n, region, first_col, width, shift_col, out, accum_out):
+        def exponentials_of(n, region):
             nc.scalar.activation(
-                out=out,
-                in_=bank(n, region)[:, first_col : first_col + width],
-                func=ACT.Exp,
-                bias=shift[n % 2][:, shift_col : shift_col + 1],
-                scale=INV_DH,
-                accum_out=accum_out,
+                out=exps[:, region, :], in_=bank(n, region)[:], func=ACT.Exp, bias=shift[n % 2][:, 0:1], scale=INV_DH
             )
+
+        def turn_exponentials(region):
+            for chunk in range(CHUNKS):
+                cols = slice(chunk * P, (chunk + 1) * P)
+                nc.tensor.transpose(turned[region % 2][:, cols], exps[:, region, cols], ident[:])
+
+        def keep_turned(region):
+            nc.scalar.copy(out=exps_t[:, region, :], in_=turned[region % 2][:])
 
         def exponentials(n):
-            i = n % 2
-            if n > 0:
-                for k in range(1, W):
-                    exponential(n, OLD, first_pair(k), k, W, exp_old_j[i][:, k, 0:k], sums[i][:, 2 * W + k : 2 * W + k + 1])
-                for k in range(W):
-                    region = CROSS_LOW if k < W // 2 else CROSS_HIGH
-                    exponential(n, region, (k % (W // 2)) * W, W, k, exp_old_j[i][:, W + k, :], k_sums[i][:, k : k + 1])
-            for k in range(1, W):
-                exponential(n, OWN, first_pair(k), k, k, exp_own_j[i][:, k, 0:k], k_sums[i][:, W + k : W + k + 1])
+            waiting = []
+            for region in regions(n):
+                exponentials_of(n, region)
+                turn_exponentials(region)
+                for earlier in waiting:
+                    keep_turned(earlier)
+                waiting = [region]
+            keep_turned(waiting[0])
             nc.scalar.activation(
-                out=masked_exp[i][:], in_=shift[i][:, W : W + 1], func=ACT.Exp, bias=ignore_col[:, 0:1], scale=1.0
+                out=masked_exp[n % 2][:], in_=shift[n % 2][:], func=ACT.Exp, bias=ignore_col[:, 0:1], scale=1.0
             )
 
-        def sums_over_k(n):
-            i = n % 2
-            used = 0
-            for j in range(W):
-                if n > 0:
-                    nc.scalar.activation(
-                        out=unread[:, used : used + 2 * W - 1 - j],
-                        in_=exp_old_j[i][:, j + 1 : 2 * W, j],
-                        func=ACT.Copy,
-                        accum_out=sums[i][:, j : j + 1],
-                    )
-                    used += 2 * W - 1 - j
-                if j < W - 1:
-                    nc.scalar.activation(
-                        out=unread[:, used : used + W - 1 - j],
-                        in_=exp_own_j[i][:, j + 1 : W, j],
-                        func=ACT.Copy,
-                        accum_out=sums[i][:, W + j : W + j + 1],
-                    )
-                    used += W - 1 - j
+        def add_up(out_col, table_col, width, pieces):
+            for place, (region, chunk) in enumerate(pieces):
+                nc.tensor.matmul(
+                    out=sums[:, out_col : out_col + width],
+                    lhsT=exps_t[:, region, chunk * P : (chunk + 1) * P],
+                    rhs=pick[:, LAYOUT[region], chunk, table_col : table_col + width],
+                    start=(place == 0),
+                    stop=(place == len(pieces) - 1),
+                )
 
-        def join_k_sums(n):
-            i = n % 2
-            nc.vector.tensor_tensor(
-                out=sums[i][:, 3 * W : 4 * W], in0=k_sums[i][:, 0:W], in1=k_sums[i][:, W : 2 * W], op=ALU.add
-            )
+        def sums_of_group(n):
+            def chunks(region, first, last):
+                return [(region, chunk) for chunk in range(first, last)] if region in regions(n) else []
+
+            add_up(PA_OWN, 0, W, chunks(OWN, 0, CHUNKS))
+            add_up(PB_OWN, W, HALF, chunks(OWN, 0, 1) + chunks(CROSS_LOW, 0, CHUNKS))
+            add_up(PB_OWN + HALF, W + HALF, HALF, chunks(OWN, 1, CHUNKS) + chunks(CROSS_HIGH, 0, CHUNKS))
+            add_up(PB_OLD, W, HALF, chunks(OLD, 0, 1))
+            add_up(PB_OLD + HALF, W + HALF, HALF, chunks(OLD, 1, CHUNKS))
+            add_up(PA_OLD, 0, W, chunks(OLD, 0, CHUNKS) + chunks(CROSS_LOW, 0, CHUNKS) + chunks(CROSS_HIGH, 0, CHUNKS))
+
+        def by_window(columns):
+            return columns.rearrange("p (s h r) -> p s h r", s=2, h=2)
 
         def add_masked_pairs(n):
-            i = n % 2
-            masked = masked_first if n == 0 else masked_later
-            nc.vector.scalar_tensor_tensor(
-                out=full[i][:], in0=masked[:], scalar=masked_exp[i][:, 0:1], in1=sums[i][:], op0=ALU.mult, op1=ALU.add
-            )
+            each = masked_exp[n % 2][:, 0:1]
+            if n == 0:
+                nc.vector.tensor_scalar(
+                    out=by_window(full[0][:])[:, :, 0, :],
+                    in0=by_window(masked_first[:])[:, :, 0, :],
+                    scalar1=each,
+                    scalar2=None,
+                    op0=ALU.mult,
+                )
+                nc.vector.scalar_tensor_tensor(
+                    out=by_window(full[0][:])[:, :, 1, :],
+                    in0=by_window(masked_first[:])[:, :, 1, :],
+                    scalar=each,
+                    in1=by_window(sums[:, 0 : 4 * W])[:, :, 1, :],
+                    op0=ALU.mult,
+                    op1=ALU.add,
+                )
+            else:
+                nc.vector.scalar_tensor_tensor(
+                    out=full[n % 2][:], in0=masked_later[:], scalar=each, in1=sums[:, 0 : 4 * W], op0=ALU.mult, op1=ALU.add
+                )
 
         def sum_of_all(n):
             nc.vector.tensor_reduce(out=total[:], in_=full[n % 2][:, 0 : 2 * W], axis=AXIS_X, op=ALU.add)
@@ -337,16 +416,11 @@ def tile_localtrittention_pa_kernel(tc, a, b, c, out_0, out_1):
         def small_instructions(n):
             chain_1, chain_2 = [], []
             if 1 <= n - 1 < NW:
-                chain_1 += [lambda: tops_of_cross(n - 1, CROSS_LOW, 0), lambda: tops_of_cross(n - 1, CROSS_HIGH, W // 2)]
+                chain_1 += [lambda: top_of(n - 1, CROSS_LOW), lambda: top_of(n - 1, CROSS_HIGH)]
             if 0 <= n - 1 < NW:
-                chain_1 += [lambda: open_tops(n - 1), top_of_all, lambda: shifts(n - 1)]
+                chain_1 += [lambda: top_of_all(n - 1), lambda: shift_by_top(n - 1)]
             if 0 <= n - 2:
-                chain_2 += [
-                    lambda: join_k_sums(n - 2),
-                    lambda: add_masked_pairs(n - 2),
-                    lambda: sum_of_all(n - 2),
-                    lambda: invert_sum(n - 2),
-                ]
+                chain_2 += [lambda: add_masked_pairs(n - 2), lambda: sum_of_all(n - 2), lambda: invert_sum(n - 2)]
             mixed = []
             for place in range(max(len(chain_1), len(chain_2))):
                 mixed += chain_1[place : place + 1] + chain_2[place : place + 1]
@@ -363,7 +437,10 @@ def tile_localtrittention_pa_kernel(tc, a, b, c, out_0, out_1):
             count_rows_and_columns()
             fill_what_is_never_written()
             build_constants()
+            name_the_pairs()
             prepare_window(0)
+            build_the_masks()
+            turn_the_names()
             for n in range(NW + 2):
                 small = small_instructions(n)
                 if n + 1 < NW:
@@ -377,7 +454,7 @@ def tile_localtrittention_pa_kernel(tc, a, b, c, out_0, out_1):
                         instruction()
                 if 0 <= n - 1 < NW:
                     exponentials(n - 1)
-                    sums_over_k(n - 1)
+                    sums_of_group(n - 1)
                 if 0 <= n - 2:
                     normalise(n - 2)
                 if n < NW:
@@ -385,16 +462,15 @@ def tile_localtrittention_pa_kernel(tc, a, b, c, out_0, out_1):
                         cross_product(n, 0)
                     else:
                         quantise_queries(0)
+                        quantise_the_masks()
                     same_quantise_and_score(n)
                     if n > 0:
                         for x in range(1, X):
                             cross_product(n, x)
                             cross_quantise_and_score(n, x - 1)
-                    open_own(n)
+                    top_of(n, OWN)
                     if n > 0:
-                        top_of_old(n)
-                    top_of_own(n)
-                    if n > 0:
+                        top_of(n, OLD)
                         cross_quantise_and_score(n, X - 1)
                 if n + 1 < NW:
                     quantise_queries(n + 1)

@@ -18,30 +18,33 @@ PACK = 4
 X = 4
 NW = 10
 W = 32
+HALF_W = W // 2
 DH = 512
-HALF = W // 2
+TRI = W * (W - 1) // 2
 BANK = 512
-CHUNKS = BANK // P
-LOW_PAIRS = HALF * (HALF - 1) // 2
-GAP = P - LOW_PAIRS
-SAME_END = W * (W - 1) // 2 + GAP
-SCORE_BANKS = 5
-OLD, OWN, CROSS_LOW, CROSS_HIGH = 0, 1, 2, 3
-SAME, LOW, HIGH = 0, 1, 2
-LAYOUT = {OLD: SAME, OWN: SAME, CROSS_LOW: LOW, CROSS_HIGH: HIGH}
-UNUSED_ONLY, CAUSAL = 0, 1
-MASK = {OLD: UNUSED_ONLY, OWN: CAUSAL, CROSS_LOW: CAUSAL, CROSS_HIGH: CAUSAL}
+SCORE_BANKS = 7
+OLD, CROSS_LOW, CROSS_HIGH, OWN = 0, 1, 2, 3
+FIRST, LAST, NONE = 0, 1, 2
 PA_OLD, PA_OWN, PB_OLD, PB_OWN = 0, W, 2 * W, 3 * W
 IGNORE = -1000000.0
 INV_DH = 1.0 / DH
 MASKED = -(2.0**100)
-ROWS_BEFORE_SMALL = 3
+ROWS_BEFORE_SHORT = 3
 
-FLOPS = 2 * W * DH * X * (NW * W * (W - 1) // 2 + (NW - 1) * W * (W - 1) // 2 + (NW - 1) * W * W)
+FLOPS = 2 * W * DH * (X * NW * TRI + X * (NW - 1) * TRI + X * (NW - 1) * W * W)
 
 
 def first_pair(k):
-    return k * (k - 1) // 2 + (GAP if k >= HALF else 0)
+    return k * (k - 1) // 2
+
+
+def weave(long_ones, short_ones):
+    for place, long_one in enumerate(long_ones):
+        long_one()
+        for short_one in short_ones[place : place + 1]:
+            short_one()
+    for short_one in short_ones[len(long_ones) :]:
+        short_one()
 
 
 def tile_localtrittention_pa_kernel(tc, a, b, c, out_0, out_1):
@@ -70,25 +73,26 @@ def tile_localtrittention_pa_kernel(tc, a, b, c, out_0, out_1):
         same_codes = [keep.tile([P, X, BANK], U32, name="same_codes%d" % i, align_bytes=64) for i in range(2)]
         same_scales = [keep.tile([P, X, BANK], U8, name="same_scales%d" % i, align_bytes=64) for i in range(2)]
 
-        banks = [psum.tile([P, BANK], F32, name="bank%d" % i) for i in range(SCORE_BANKS)]
-        turned = [psum.tile([P, BANK], F32, name="turned%d" % i) for i in range(2)]
-        sums = psum.tile([P, BANK], F32, name="sums")
-
-        exps = keep.tile([P, 4, BANK], F32, name="exps")
-        exps_t = keep.tile([P, 4, BANK], F32, name="exps_t")
-        names = keep.tile([P, 3, BANK], F32, name="names")
-        pick = keep.tile([P, 3, CHUNKS, 2 * W], F32, name="pick")
+        mask_queries = keep.tile([P, P, PACK], BF16, name="mask_queries", align_bytes=64)
+        mask_query_codes = keep.tile([P, P], U32, name="mask_query_codes", align_bytes=64)
+        mask_query_scales = keep.tile([P, P], U8, name="mask_query_scales", align_bytes=64)
         mask_keys = keep.tile([P, 3, BANK, PACK], BF16, name="mask_keys", align_bytes=64)
         mask_key_codes = keep.tile([P, 3, BANK], U32, name="mask_key_codes", align_bytes=64)
         mask_key_scales = keep.tile([P, 3, BANK], U8, name="mask_key_scales", align_bytes=64)
-        mask_queries = keep.tile([P, 2, P, PACK], BF16, name="mask_queries", align_bytes=64)
-        mask_query_codes = keep.tile([P, 2, P], U32, name="mask_query_codes", align_bytes=64)
-        mask_query_scales = keep.tile([P, 2, P], U8, name="mask_query_scales", align_bytes=64)
 
-        tops = [keep.tile([P, 5], F32, name="tops%d" % i) for i in range(2)]
-        top = keep.tile([P, 1], F32, name="top")
-        shift = [keep.tile([P, 1], F32, name="shift%d" % i) for i in range(2)]
-        masked_exp = [keep.tile([P, 1], F32, name="masked_exp%d" % i) for i in range(2)]
+        banks = [psum.tile([P, BANK], F32, name="bank%d" % i) for i in range(SCORE_BANKS)]
+        turned = psum.tile([P, BANK], F32, name="turned")
+
+        exp_old_j = [keep.tile([P, 2 * W, W], F32, name="exp_old_j%d" % i) for i in range(2)]
+        exp_own_j = [keep.tile([P, W, W], F32, name="exp_own_j%d" % i) for i in range(2)]
+        unread = keep.tile([P, W * W + 2 * TRI], F32, name="unread")
+
+        tops = [keep.tile([P, 4], F32, name="tops%d" % i) for i in range(2)]
+        top_first = keep.tile([P, 1], F32, name="top_first")
+        shifts = [keep.tile([P, 3], F32, name="shifts%d" % i) for i in range(2)]
+        lowest = [keep.tile([P, 1], F32, name="lowest%d" % i) for i in range(2)]
+        factors = [keep.tile([P, 3], F32, name="factors%d" % i) for i in range(2)]
+        sums = [[keep.tile([P, 4 * W], F32, name="sums%d_%d" % (half, i)) for i in range(2)] for half in (FIRST, LAST)]
         full = [keep.tile([P, 4 * W], F32, name="full%d" % i) for i in range(2)]
         total = keep.tile([P, 1], F32, name="total")
         scale = [keep.tile([P, 1], F32, name="scale%d" % i) for i in range(2)]
@@ -102,7 +106,6 @@ def tile_localtrittention_pa_kernel(tc, a, b, c, out_0, out_1):
         col = keep.tile([P, W], F32, name="col")
         seen = keep.tile([P, W], F32, name="seen")
         work = keep.tile([P, W], F32, name="work")
-        ignore_col = keep.tile([P, 1], F32, name="ignore_col")
         masked_first = keep.tile([P, 4 * W], F32, name="masked_first")
         masked_later = keep.tile([P, 4 * W], F32, name="masked_later")
 
@@ -111,8 +114,8 @@ def tile_localtrittention_pa_kernel(tc, a, b, c, out_0, out_1):
         def bank(n, region):
             return banks[(4 * n + region) % SCORE_BANKS]
 
-        def regions(n):
-            return (OWN,) if n == 0 else (OLD, OWN, CROSS_LOW, CROSS_HIGH)
+        def mask_of(region):
+            return region - 1
 
         def load_inputs():
             for n in range(NW):
@@ -127,19 +130,22 @@ def tile_localtrittention_pa_kernel(tc, a, b, c, out_0, out_1):
             nc.gpsimd.iota(p_minus_c_int[:], pattern=[[-1, W]], base=0, channel_multiplier=1)
 
         def fill_what_is_never_written():
+            nc.gpsimd.memset(mask_keys[:].bitcast(F32), 0.0)
+            nc.gpsimd.memset(exp_old_j[(NW - 1) % 2][:, 0:W, :], 0.0)
+            nc.gpsimd.memset(exp_own_j[(NW - 1) % 2][:], 0.0)
+            nc.vector.memset(mask_queries[:].bitcast(I32), 0)
             for i in range(2):
                 nc.vector.memset(c_wide[i][:].bitcast(I32), 0)
-                nc.vector.memset(tops[i][:, 0:4], MASKED)
-                nc.vector.memset(tops[i][:, 4:5], IGNORE)
-            nc.vector.memset(same_keys[:, :, LOW_PAIRS:P, :], 0.0)
-            nc.vector.memset(same_keys[:, :, SAME_END:BANK, :], 0.0)
-            nc.vector.memset(mask_keys[:].bitcast(I32), 0)
-            nc.vector.memset(mask_queries[:].bitcast(I32), 0)
-            nc.vector.memset(ignore_col[:], IGNORE * INV_DH)
+                nc.vector.memset(sums[FIRST][i][:], 0.0)
+                nc.vector.memset(sums[LAST][i][:], 0.0)
+                nc.vector.memset(tops[i][:], MASKED)
+                nc.vector.memset(shifts[i][:, NONE : NONE + 1], -IGNORE * INV_DH)
+            nc.vector.memset(same_keys[:, :, TRI:BANK, :], 0.0)
 
         def build_constants():
             nc.vector.tensor_copy(out=i_minus_c[:], in_=i_minus_c_int[:])
             nc.vector.tensor_copy(out=col[:], in_=col_int[:])
+            nc.vector.tensor_copy(out=p_minus_c[:], in_=p_minus_c_int[:])
             nc.vector.tensor_scalar(out=seen[:], in0=i_minus_c[:], scalar1=0.0, scalar2=None, op0=ALU.is_ge)
             nc.vector.tensor_scalar(
                 out=masked_later[:, 0:W], in0=i_minus_c[:], scalar1=-1.0, scalar2=1.0 * W, op0=ALU.mult, op1=ALU.add
@@ -159,84 +165,56 @@ def tile_localtrittention_pa_kernel(tc, a, b, c, out_0, out_1):
                 out=masked_first[:, 3 * W : 4 * W], in0=work[:], scalar1=-1.0, scalar2=2.0 * W, op0=ALU.mult, op1=ALU.add
             )
 
-        def name_the_pairs():
-            for k in range(1, W):
-                nc.vector.tensor_scalar(
-                    out=names[:, SAME, first_pair(k) : first_pair(k) + k],
-                    in0=ident[:, 0:k],
-                    scalar1=ident[:, W + k : W + k + 1],
-                    scalar2=None,
-                    op0=ALU.add,
-                )
-            for cols in (slice(LOW_PAIRS, P), slice(SAME_END, BANK)):
-                nc.vector.tensor_copy(out=names[:, SAME, cols], in_=ident[:, 2 * W : 2 * W + 1].to_broadcast([P, GAP]))
-            for layout, first_k in ((LOW, 0), (HIGH, HALF)):
-                nc.vector.tensor_tensor(
-                    out=names[:, layout, :].rearrange("p (k j) -> p k j", j=W),
-                    in0=ident[:, 0:W].unsqueeze(1).to_broadcast([P, HALF, W]),
-                    in1=ident[:, W + first_k : W + first_k + HALF].unsqueeze(2).to_broadcast([P, HALF, W]),
-                    op=ALU.add,
-                )
-
-        def turn_the_names():
-            for layout in (SAME, LOW, HIGH):
-                for chunk in range(CHUNKS):
-                    cols = slice(chunk * P, (chunk + 1) * P)
-                    nc.tensor.transpose(turned[layout % 2][:, cols], names[:, layout, cols], ident[:])
-                nc.scalar.copy(
-                    out=pick[:, layout], in_=turned[layout % 2][:].rearrange("p (c r) -> p c r", r=P)[:, :, 0 : 2 * W]
-                )
-
         def build_the_masks():
-            nc.scalar.activation(
-                out=mask_keys[:].rearrange("p l c t -> p (l c) t")[:, :, 0],
-                in_=names[:].rearrange("p l c -> p (l c)"),
-                func=ACT.Copy,
-                scale=MASKED,
-            )
-            nc.vector.tensor_copy(out=p_minus_c[:], in_=p_minus_c_int[:])
             nc.vector.tensor_scalar(
-                out=mask_queries[:, CAUSAL].rearrange("p (x i) t -> p x i t", x=X)[:, :, :, 0],
+                out=mask_queries[:].rearrange("p (x i) t -> p x i t", x=X)[:, :, :, 0],
                 in0=p_minus_c[:].unsqueeze(1).to_broadcast([P, X, W]),
-                scalar1=1.0 * W,
+                scalar1=0.0,
                 scalar2=None,
                 op0=ALU.is_gt,
             )
-            nc.vector.tensor_scalar(
-                out=mask_queries[:, UNUSED_ONLY, :, 0],
-                in0=p_minus_c[:, W - 1 : W].to_broadcast([P, P]),
-                scalar1=1.0 * W,
-                scalar2=None,
-                op0=ALU.is_gt,
-            )
+            for region, first_k in ((CROSS_LOW, 0), (CROSS_HIGH, HALF_W)):
+                nc.scalar.activation(
+                    out=mask_keys[:, mask_of(region)].rearrange("p (k j) t -> p k j t", j=W)[:, :, :, 0],
+                    in_=ident[:, first_k : first_k + HALF_W].unsqueeze(2).to_broadcast([P, HALF_W, W]),
+                    func=ACT.Copy,
+                    scale=MASKED,
+                )
+            for k in range(1, W):
+                nc.scalar.activation(
+                    out=mask_keys[:, mask_of(OWN), first_pair(k) : first_pair(k) + k, 0],
+                    in_=ident[:, k : k + 1].to_broadcast([P, k]),
+                    func=ACT.Copy,
+                    scale=MASKED,
+                )
 
         def quantise_the_masks():
             nc.vector.quantize_mx(
-                out=mask_query_codes[:].rearrange("p m q -> p (m q)").bitcast(FP8X4),
-                scales=mask_query_scales[:].rearrange("p m q -> p (m q)"),
-                in_=mask_queries[:].rearrange("p m q t -> p (m q t)"),
+                out=mask_query_codes[:].bitcast(FP8X4),
+                scales=mask_query_scales[:],
+                in_=mask_queries[:].rearrange("p q t -> p (q t)"),
             )
-            for layout in (SAME, LOW, HIGH):
+            for region in (OWN, CROSS_LOW, CROSS_HIGH):
                 nc.vector.quantize_mx(
-                    out=mask_key_codes[:, layout, :].bitcast(FP8X4),
-                    scales=mask_key_scales[:, layout, :],
-                    in_=mask_keys[:, layout].rearrange("p c t -> p (c t)"),
+                    out=mask_key_codes[:, mask_of(region), :].bitcast(FP8X4),
+                    scales=mask_key_scales[:, mask_of(region), :],
+                    in_=mask_keys[:, mask_of(region)].rearrange("p c t -> p (c t)"),
                 )
 
-        def turn_input(name, n, place, first_col):
+        def turn(name, n, first_col):
             words = raw[name][:, n, :].bitcast(F32)
             for u in range(2):
                 nc.tensor.transpose(
-                    turned[place][:, first_col + u * P : first_col + (u + 1) * P], words[:, u * P : (u + 1) * P], ident[:]
+                    turned[:, first_col + u * P : first_col + (u + 1) * P], words[:, u * P : (u + 1) * P], ident[:]
                 )
-            return turned[place][:, first_col : first_col + 2 * P].rearrange("p (u r) -> p r u", u=2)
+            return turned[:, first_col : first_col + 2 * P].rearrange("p (u r) -> p r u", u=2)
 
         def prepare_window(n):
-            a_words = turn_input("a", n, 0, 0)
-            b_words = turn_input("b", n, 0, 2 * P)
-            c_words = turn_input("c", n, 1, 0)
+            a_words = turn("a", n, 0)
+            b_words = turn("b", n, 2 * P)
             nc.scalar.copy(out=a_t[:, n].bitcast(F32), in_=a_words)
             nc.scalar.copy(out=b_t[:, n].bitcast(F32), in_=b_words)
+            c_words = turn("c", n, 0)
             for x in range(X):
                 rows = slice(x * W, (x + 1) * W)
                 nc.scalar.copy(out=c_wide[n % 2][:, x, rows, :].bitcast(F32), in_=c_words[:, rows, :])
@@ -248,18 +226,20 @@ def tile_localtrittention_pa_kernel(tc, a, b, c, out_0, out_1):
                 in_=c_wide[n % 2][:].rearrange("p x r t -> p (x r t)"),
             )
 
-        def open_bank(n, region):
+        def mask_pass(n, region):
             nc.tensor.matmul_mx(
                 out=bank(n, region)[:],
-                lhsT=mask_query_codes[:, MASK[region], :].bitcast(FP8X4),
-                lhsT_scale=mask_query_scales[:, MASK[region], :],
-                rhs=mask_key_codes[:, LAYOUT[region], :].bitcast(FP8X4),
-                rhs_scale=mask_key_scales[:, LAYOUT[region], :],
+                lhsT=mask_query_codes[:].bitcast(FP8X4),
+                lhsT_scale=mask_query_scales[:],
+                rhs=mask_key_codes[:, mask_of(region), :].bitcast(FP8X4),
+                rhs_scale=mask_key_scales[:, mask_of(region), :],
                 start=True,
                 stop=False,
             )
 
         def score_pass(n, region, x, codes, scales):
+            if x == 0 and region != OLD:
+                mask_pass(n, region)
             cols = slice(x * P, (x + 1) * P)
             nc.tensor.matmul_mx(
                 out=bank(n, region)[:],
@@ -267,7 +247,7 @@ def tile_localtrittention_pa_kernel(tc, a, b, c, out_0, out_1):
                 lhsT_scale=c_scales[n % 2][:, cols],
                 rhs=codes.bitcast(FP8X4),
                 rhs_scale=scales,
-                start=False,
+                start=(x == 0 and region == OLD),
                 stop=(x == X - 1),
             )
 
@@ -288,121 +268,115 @@ def tile_localtrittention_pa_kernel(tc, a, b, c, out_0, out_1):
             )
             for half, region in enumerate((CROSS_LOW, CROSS_HIGH)):
                 cols = slice(half * BANK, (half + 1) * BANK)
-                if x == 0:
-                    open_bank(n, region)
                 score_pass(n, region, x, cross_codes[x][:, cols], cross_scales[x][:, cols])
 
-        def same_products(n, small):
+        def same_product(n, k):
             a_win = a_t[:, n].rearrange("p (x w) t -> p x w t", x=X)
             b_win = b_t[:, n].rearrange("p (x w) t -> p x w t", x=X)
-            for row, k in enumerate(reversed(range(1, W))):
-                nc.vector.tensor_tensor(
-                    out=same_keys[:, :, first_pair(k) : first_pair(k) + k, :],
-                    in0=a_win[:, :, 0:k, :],
-                    in1=b_win[:, :, k : k + 1, :].to_broadcast([P, X, k, PACK]),
-                    op=ALU.mult,
-                )
-                if 0 <= row - ROWS_BEFORE_SMALL < len(small):
-                    small[row - ROWS_BEFORE_SMALL]()
+            nc.vector.tensor_tensor(
+                out=same_keys[:, :, first_pair(k) : first_pair(k) + k, :],
+                in0=a_win[:, :, 0:k, :],
+                in1=b_win[:, :, k : k + 1, :].to_broadcast([P, X, k, PACK]),
+                op=ALU.mult,
+            )
 
-        def same_quantise_and_score(n):
-            for half in range(2):
-                heads = slice(2 * half, 2 * half + 2)
-                nc.vector.quantize_mx(
-                    out=same_codes[n % 2][:, heads, :].rearrange("p x c -> p (x c)").bitcast(FP8X4),
-                    scales=same_scales[n % 2][:, heads, :].rearrange("p x c -> p (x c)"),
-                    in_=same_keys[:, heads, :, :].rearrange("p x c t -> p (x c t)"),
-                )
-            score_same(n, OWN, n)
+        def same_quantise(n, half):
+            heads = slice(2 * half, 2 * half + 2)
+            nc.vector.quantize_mx(
+                out=same_codes[n % 2][:, heads, :].rearrange("p x c -> p (x c)").bitcast(FP8X4),
+                scales=same_scales[n % 2][:, heads, :].rearrange("p x c -> p (x c)"),
+                in_=same_keys[:, heads, :, :].rearrange("p x c t -> p (x c t)"),
+            )
 
         def score_same(n, region, key_window):
-            open_bank(n, region)
             for x in range(X):
                 score_pass(n, region, x, same_codes[key_window % 2][:, x, :], same_scales[key_window % 2][:, x, :])
 
         def top_of(n, region):
+            width = BANK if region in (CROSS_LOW, CROSS_HIGH) else TRI
             nc.vector.tensor_reduce(
-                out=tops[n % 2][:, region : region + 1], in_=bank(n, region)[:], axis=AXIS_X, op=ALU.max
+                out=tops[n % 2][:, region : region + 1], in_=bank(n, region)[:, 0:width], axis=AXIS_X, op=ALU.max
             )
 
-        def top_of_all(n):
-            nc.vector.tensor_reduce(out=top[:], in_=tops[n % 2][:], axis=AXIS_X, op=ALU.max)
+        def top_of_first_half(n):
+            nc.vector.tensor_reduce(out=top_first[:], in_=tops[n % 2][:, OLD : CROSS_HIGH + 1], axis=AXIS_X, op=ALU.max)
 
-        def shift_by_top(n):
-            nc.vector.tensor_scalar(out=shift[n % 2][:], in0=top[:], scalar1=-INV_DH, scalar2=None, op0=ALU.mult)
+        def shift_of(n, half, top):
+            nc.vector.tensor_scalar(
+                out=shifts[n % 2][:, half : half + 1], in0=top, scalar1=IGNORE, scalar2=-INV_DH, op0=ALU.max, op1=ALU.mult
+            )
 
-        def exponentials_of(n, region):
+        def lowest_shift(n):
+            nc.vector.tensor_reduce(out=lowest[n % 2][:], in_=shifts[n % 2][:], axis=AXIS_X, op=ALU.min)
+
+        def factors_of(n):
             nc.scalar.activation(
-                out=exps[:, region, :], in_=bank(n, region)[:], func=ACT.Exp, bias=shift[n % 2][:, 0:1], scale=INV_DH
+                out=factors[n % 2][:], in_=shifts[n % 2][:], func=ACT.Exp, bias=lowest[n % 2][:, 0:1], scale=-1.0
             )
 
-        def turn_exponentials(region):
-            for chunk in range(CHUNKS):
-                cols = slice(chunk * P, (chunk + 1) * P)
-                nc.tensor.transpose(turned[region % 2][:, cols], exps[:, region, cols], ident[:])
-
-        def keep_turned(region):
-            nc.scalar.copy(out=exps_t[:, region, :], in_=turned[region % 2][:])
-
-        def exponentials(n):
-            waiting = []
-            for region in regions(n):
-                exponentials_of(n, region)
-                turn_exponentials(region)
-                for earlier in waiting:
-                    keep_turned(earlier)
-                waiting = [region]
-            keep_turned(waiting[0])
+        def exponential(n, region, first_col, width, half, out, sum_col):
             nc.scalar.activation(
-                out=masked_exp[n % 2][:], in_=shift[n % 2][:], func=ACT.Exp, bias=ignore_col[:, 0:1], scale=1.0
+                out=out,
+                in_=bank(n, region)[:, first_col : first_col + width],
+                func=ACT.Exp,
+                bias=shifts[n % 2][:, half : half + 1],
+                scale=INV_DH,
+                accum_out=sums[half][n % 2][:, sum_col : sum_col + 1],
             )
 
-        def add_up(out_col, table_col, width, pieces):
-            for place, (region, chunk) in enumerate(pieces):
-                nc.tensor.matmul(
-                    out=sums[:, out_col : out_col + width],
-                    lhsT=exps_t[:, region, chunk * P : (chunk + 1) * P],
-                    rhs=pick[:, LAYOUT[region], chunk, table_col : table_col + width],
-                    start=(place == 0),
-                    stop=(place == len(pieces) - 1),
-                )
+        def sum_over_k(n, half, column, first_unread, sum_col):
+            nc.scalar.activation(
+                out=unread[:, first_unread : first_unread + column.shape[1]],
+                in_=column,
+                func=ACT.Copy,
+                accum_out=sums[half][n % 2][:, sum_col : sum_col + 1],
+            )
 
-        def sums_of_group(n):
-            def chunks(region, first, last):
-                return [(region, chunk) for chunk in range(first, last)] if region in regions(n) else []
+        def first_half(n):
+            i = n % 2
+            for k in range(1, W):
+                exponential(n, OLD, first_pair(k), k, FIRST, exp_old_j[i][:, k, 0:k], PB_OLD + k)
+            for k in range(W):
+                region = CROSS_LOW if k < HALF_W else CROSS_HIGH
+                exponential(n, region, (k % HALF_W) * W, W, FIRST, exp_old_j[i][:, W + k, :], PB_OWN + k)
+            if n < NW - 1:
+                used = 0
+                for j in range(W):
+                    sum_over_k(n, FIRST, exp_old_j[i][:, j + 1 : 2 * W, j], used, PA_OLD + j)
+                    used += 2 * W - 1 - j
 
-            add_up(PA_OWN, 0, W, chunks(OWN, 0, CHUNKS))
-            add_up(PB_OWN, W, HALF, chunks(OWN, 0, 1) + chunks(CROSS_LOW, 0, CHUNKS))
-            add_up(PB_OWN + HALF, W + HALF, HALF, chunks(OWN, 1, CHUNKS) + chunks(CROSS_HIGH, 0, CHUNKS))
-            add_up(PB_OLD, W, HALF, chunks(OLD, 0, 1))
-            add_up(PB_OLD + HALF, W + HALF, HALF, chunks(OLD, 1, CHUNKS))
-            add_up(PA_OLD, 0, W, chunks(OLD, 0, CHUNKS) + chunks(CROSS_LOW, 0, CHUNKS) + chunks(CROSS_HIGH, 0, CHUNKS))
+        def last_half(n):
+            i = n % 2
+            for k in range(1, W):
+                exponential(n, OWN, first_pair(k), k, LAST, exp_own_j[i][:, k, 0:k], PB_OWN + k)
+            if n < NW - 1:
+                used = W * W + TRI
+                for j in range(W - 1):
+                    sum_over_k(n, LAST, exp_own_j[i][:, j + 1 : W, j], used, PA_OWN + j)
+                    used += W - 1 - j
 
-        def by_window(columns):
-            return columns.rearrange("p (s h r) -> p s h r", s=2, h=2)
+        def last_sums_over_k(half):
+            i = (NW - 1) % 2
+            rows, sum_col = ((exp_old_j[i], PA_OLD), (exp_own_j[i], PA_OWN))[half]
+            nc.vector.tensor_reduce(
+                out=sums[half][i][:, sum_col : sum_col + W], in_=rows[:].rearrange("p k j -> p j k"), axis=AXIS_X, op=ALU.add
+            )
 
         def add_masked_pairs(n):
-            each = masked_exp[n % 2][:, 0:1]
-            if n == 0:
-                nc.vector.tensor_scalar(
-                    out=by_window(full[0][:])[:, :, 0, :],
-                    in0=by_window(masked_first[:])[:, :, 0, :],
-                    scalar1=each,
-                    scalar2=None,
-                    op0=ALU.mult,
-                )
-                nc.vector.scalar_tensor_tensor(
-                    out=by_window(full[0][:])[:, :, 1, :],
-                    in0=by_window(masked_first[:])[:, :, 1, :],
-                    scalar=each,
-                    in1=by_window(sums[:, 0 : 4 * W])[:, :, 1, :],
-                    op0=ALU.mult,
-                    op1=ALU.add,
-                )
-            else:
-                nc.vector.scalar_tensor_tensor(
-                    out=full[n % 2][:], in0=masked_later[:], scalar=each, in1=sums[:, 0 : 4 * W], op0=ALU.mult, op1=ALU.add
-                )
+            masked = masked_first if n == 0 else masked_later
+            nc.vector.tensor_scalar(
+                out=full[n % 2][:], in0=masked[:], scalar1=factors[n % 2][:, NONE : NONE + 1], scalar2=None, op0=ALU.mult
+            )
+
+        def add_half(n, half):
+            nc.vector.scalar_tensor_tensor(
+                out=full[n % 2][:],
+                in0=sums[half][n % 2][:],
+                scalar=factors[n % 2][:, half : half + 1],
+                in1=full[n % 2][:],
+                op0=ALU.mult,
+                op1=ALU.add,
+            )
 
         def sum_of_all(n):
             nc.vector.tensor_reduce(out=total[:], in_=full[n % 2][:, 0 : 2 * W], axis=AXIS_X, op=ALU.add)
@@ -412,19 +386,6 @@ def tile_localtrittention_pa_kernel(tc, a, b, c, out_0, out_1):
 
         def normalise(n):
             nc.scalar.activation(out=result[:, n, :], in_=full[n % 2][:], func=ACT.Copy, scale=scale[n % 2][:, 0:1])
-
-        def small_instructions(n):
-            chain_1, chain_2 = [], []
-            if 1 <= n - 1 < NW:
-                chain_1 += [lambda: top_of(n - 1, CROSS_LOW), lambda: top_of(n - 1, CROSS_HIGH)]
-            if 0 <= n - 1 < NW:
-                chain_1 += [lambda: top_of_all(n - 1), lambda: shift_by_top(n - 1)]
-            if 0 <= n - 2:
-                chain_2 += [lambda: add_masked_pairs(n - 2), lambda: sum_of_all(n - 2), lambda: invert_sum(n - 2)]
-            mixed = []
-            for place in range(max(len(chain_1), len(chain_2))):
-                mixed += chain_1[place : place + 1] + chain_2[place : place + 1]
-            return mixed
 
         def store_outputs():
             for x in range(X):
@@ -437,41 +398,70 @@ def tile_localtrittention_pa_kernel(tc, a, b, c, out_0, out_1):
             count_rows_and_columns()
             fill_what_is_never_written()
             build_constants()
-            name_the_pairs()
             prepare_window(0)
             build_the_masks()
-            turn_the_names()
-            for n in range(NW + 2):
-                small = small_instructions(n)
+            for n in range(NW + 1):
+                before = n - 1
+                makes_keys = n < NW
+                has_cross = 0 < n < NW
+                if has_cross:
+                    score_same(n, OLD, n - 1)
                 if n + 1 < NW:
                     prepare_window(n + 1)
-                if n < NW:
-                    if n > 0:
-                        score_same(n, OLD, n - 1)
-                    same_products(n, small)
-                else:
-                    for instruction in small:
-                        instruction()
-                if 0 <= n - 1 < NW:
-                    exponentials(n - 1)
-                    sums_of_group(n - 1)
-                if 0 <= n - 2:
-                    normalise(n - 2)
-                if n < NW:
-                    if n > 0:
-                        cross_product(n, 0)
-                    else:
-                        quantise_queries(0)
-                        quantise_the_masks()
-                    same_quantise_and_score(n)
-                    if n > 0:
-                        for x in range(1, X):
-                            cross_product(n, x)
-                            cross_quantise_and_score(n, x - 1)
-                    top_of(n, OWN)
-                    if n > 0:
-                        top_of(n, OLD)
-                        cross_quantise_and_score(n, X - 1)
+
+                long_ones, short_ones = [], []
+                if has_cross:
+                    long_ones += [lambda: cross_product(n, 0)]
+                    for x in range(1, X):
+                        long_ones += [lambda x=x: cross_product(n, x), lambda x=x: cross_quantise_and_score(n, x - 1)]
+                    long_ones += [lambda: cross_quantise_and_score(n, X - 1)]
+                if before >= 0:
+                    short_ones += [
+                        lambda: top_of(before, OWN),
+                        lambda: shift_of(before, LAST, tops[before % 2][:, OWN : OWN + 1]),
+                        lambda: lowest_shift(before),
+                    ]
+                if has_cross:
+                    short_ones += [lambda: top_of(n, OLD)]
+                weave(long_ones, short_ones)
+                if before >= 0:
+                    factors_of(before)
+                    last_half(before)
+
+                long_ones, short_ones = [], []
+                if makes_keys:
+                    long_ones += [lambda k=k: same_product(n, k) for k in reversed(range(1, W))]
+                if has_cross:
+                    short_ones += [lambda: top_of(n, CROSS_LOW)]
+                if before >= 0:
+                    short_ones += [lambda: add_masked_pairs(before)]
+                if has_cross:
+                    short_ones += [lambda: top_of(n, CROSS_HIGH)]
+                if before == NW - 1:
+                    short_ones += [lambda: last_sums_over_k(FIRST)]
+                if before >= 0:
+                    short_ones += [lambda: add_half(before, FIRST)]
+                if makes_keys:
+                    short_ones += [lambda: top_of_first_half(n), lambda: shift_of(n, FIRST, top_first[:])]
+                weave(long_ones[:ROWS_BEFORE_SHORT], [])
+                weave(long_ones[ROWS_BEFORE_SHORT:], short_ones)
+                if has_cross:
+                    first_half(n)
+
+                long_ones, short_ones = [], []
+                if n == 0:
+                    long_ones += [lambda: quantise_queries(0), quantise_the_masks]
                 if n + 1 < NW:
-                    quantise_queries(n + 1)
+                    long_ones += [lambda: quantise_queries(n + 1)]
+                if makes_keys:
+                    long_ones += [lambda: same_quantise(n, 0), lambda: same_quantise(n, 1)]
+                if before == NW - 1:
+                    short_ones += [lambda: last_sums_over_k(LAST)]
+                if before >= 0:
+                    short_ones += [lambda: add_half(before, LAST), lambda: sum_of_all(before), lambda: invert_sum(before)]
+                weave(long_ones, short_ones)
+                if makes_keys:
+                    score_same(n, OWN, n)
+                if before >= 0:
+                    normalise(before)
             store_outputs()

@@ -22,13 +22,15 @@ HALF_W = W // 2
 DH = 512
 TRI = W * (W - 1) // 2
 BANK = 512
-SCORE_BANKS = 7
+SCORE_BANKS = 6
 OLD, CROSS_LOW, CROSS_HIGH, OWN = 0, 1, 2, 3
 FIRST, LAST, NONE = 0, 1, 2
 PA_OLD, PA_OWN, PB_OLD, PB_OWN = 0, W, 2 * W, 3 * W
 IGNORE = -1000000.0
 INV_DH = 1.0 / DH
 MASKED = -(2.0**100)
+SHARED_ROWS = 6
+VECTOR_ROWS = W - SHARED_ROWS
 ROWS_BEFORE_SHORT = 3
 
 FLOPS = 2 * W * DH * (X * NW * TRI + X * (NW - 1) * TRI + X * (NW - 1) * W * W)
@@ -59,7 +61,7 @@ def tile_localtrittention_pa_kernel(tc, a, b, c, out_0, out_1):
             "c": keep.tile([P, NW, DH], BF16, name="raw_c"),
         }
         a_t = keep.tile([P, NW, P, PACK], BF16, name="a_t", align_bytes=64)
-        b_t = keep.tile([P, NW, P, PACK], BF16, name="b_t", align_bytes=64)
+        b_shared = [keep.tile([P, X, SHARED_ROWS, PACK], BF16, name="b_shared%d" % i, align_bytes=64) for i in range(2)]
         ident = keep.tile([P, P], F32, name="ident")
 
         c_wide = [keep.tile([P, X, P, PACK], BF16, name="c_wide%d" % i, align_bytes=64) for i in range(2)]
@@ -81,7 +83,7 @@ def tile_localtrittention_pa_kernel(tc, a, b, c, out_0, out_1):
         mask_key_scales = keep.tile([P, 3, BANK], U8, name="mask_key_scales", align_bytes=64)
 
         banks = [psum.tile([P, BANK], F32, name="bank%d" % i) for i in range(SCORE_BANKS)]
-        turned = psum.tile([P, BANK], F32, name="turned")
+        turned = [psum.tile([P, BANK], F32, name="turned%d" % i) for i in range(2)]
 
         exp_old_j = [keep.tile([P, 2 * W, W], F32, name="exp_old_j%d" % i) for i in range(2)]
         exp_own_j = [keep.tile([P, W, W], F32, name="exp_own_j%d" % i) for i in range(2)]
@@ -201,20 +203,28 @@ def tile_localtrittention_pa_kernel(tc, a, b, c, out_0, out_1):
                     in_=mask_keys[:, mask_of(region)].rearrange("p c t -> p (c t)"),
                 )
 
-        def turn(name, n, first_col):
+        def turn(name, n):
             words = raw[name][:, n, :].bitcast(F32)
+            if name == "b":
+                turned_words = turned[n % 2][:, 0 : 2 * P].rearrange("p (r u) -> p r u", u=2)
+            else:
+                turned_words = turned[n % 2][:, 2 * P : 4 * P].rearrange("p (u r) -> p r u", u=2)
             for u in range(2):
-                nc.tensor.transpose(
-                    turned[:, first_col + u * P : first_col + (u + 1) * P], words[:, u * P : (u + 1) * P], ident[:]
-                )
-            return turned[:, first_col : first_col + 2 * P].rearrange("p (u r) -> p r u", u=2)
+                nc.tensor.transpose(turned_words[:, :, u], words[:, u * P : (u + 1) * P], ident[:])
+            return turned_words
+
+        def b_in_psum(n):
+            return turned[n % 2][:, 0 : 2 * P].bitcast(BF16).rearrange("p (r t) -> p r t", t=PACK)
 
         def prepare_window(n):
-            a_words = turn("a", n, 0)
-            b_words = turn("b", n, 2 * P)
+            a_words = turn("a", n)
+            b_words = turn("b", n)
             nc.scalar.copy(out=a_t[:, n].bitcast(F32), in_=a_words)
-            nc.scalar.copy(out=b_t[:, n].bitcast(F32), in_=b_words)
-            c_words = turn("c", n, 0)
+            nc.scalar.copy(
+                out=b_shared[n % 2][:].rearrange("p x k t -> p x (k t)").bitcast(F32),
+                in_=b_words.rearrange("p (x k) u -> p x (k u)", x=X)[:, :, 2 * VECTOR_ROWS : 2 * W],
+            )
+            c_words = turn("c", n)
             for x in range(X):
                 rows = slice(x * W, (x + 1) * W)
                 nc.scalar.copy(out=c_wide[n % 2][:, x, rows, :].bitcast(F32), in_=c_words[:, rows, :])
@@ -253,10 +263,16 @@ def tile_localtrittention_pa_kernel(tc, a, b, c, out_0, out_1):
 
         def cross_product(n, x):
             rows = slice(x * W, (x + 1) * W)
+            nc.gpsimd.tensor_tensor(
+                out=cross_keys[x % 3][:, VECTOR_ROWS:W],
+                in0=a_t[:, n - 1, rows, :].unsqueeze(1).to_broadcast([P, SHARED_ROWS, W, PACK]),
+                in1=b_shared[n % 2][:, x].unsqueeze(2).to_broadcast([P, SHARED_ROWS, W, PACK]),
+                op=ALU.mult,
+            )
             nc.vector.tensor_tensor(
-                out=cross_keys[x % 3][:],
-                in0=a_t[:, n - 1, rows, :].unsqueeze(1).to_broadcast([P, W, W, PACK]),
-                in1=b_t[:, n, rows, :].unsqueeze(2).to_broadcast([P, W, W, PACK]),
+                out=cross_keys[x % 3][:, 0:VECTOR_ROWS],
+                in0=a_t[:, n - 1, rows, :].unsqueeze(1).to_broadcast([P, VECTOR_ROWS, W, PACK]),
+                in1=b_in_psum(n)[:, x * W : x * W + VECTOR_ROWS, :].unsqueeze(2).to_broadcast([P, VECTOR_ROWS, W, PACK]),
                 op=ALU.mult,
             )
 
@@ -272,7 +288,7 @@ def tile_localtrittention_pa_kernel(tc, a, b, c, out_0, out_1):
 
         def same_product(n, k):
             a_win = a_t[:, n].rearrange("p (x w) t -> p x w t", x=X)
-            b_win = b_t[:, n].rearrange("p (x w) t -> p x w t", x=X)
+            b_win = b_in_psum(n).rearrange("p (x w) t -> p x w t", x=X)
             nc.vector.tensor_tensor(
                 out=same_keys[:, :, first_pair(k) : first_pair(k) + k, :],
                 in0=a_win[:, :, 0:k, :],

@@ -29,9 +29,8 @@ PA_OLD, PA_OWN, PB_OLD, PB_OWN = 0, W, 2 * W, 3 * W
 IGNORE = -1000000.0
 INV_DH = 1.0 / DH
 MASKED = -(2.0**100)
-SHARED_ROWS = 6
-VECTOR_ROWS = W - SHARED_ROWS
-ROWS_BEFORE_SHORT = 3
+SHARED_ROWS = 11
+SHARED_ROWS_AT_END = 6
 
 FLOPS = 2 * W * DH * (X * NW * TRI + X * (NW - 1) * TRI + X * (NW - 1) * W * W)
 
@@ -68,7 +67,7 @@ def tile_localtrittention_pa_kernel(tc, a, b, c, out_0, out_1):
         c_codes = [keep.tile([P, X * P], U32, name="c_codes%d" % i, align_bytes=64) for i in range(2)]
         c_scales = [keep.tile([P, X * P], U8, name="c_scales%d" % i, align_bytes=64) for i in range(2)]
 
-        cross_keys = [keep.tile([P, W, W, PACK], BF16, name="cross_keys%d" % i, align_bytes=64) for i in range(3)]
+        cross_keys = [keep.tile([P, W, W, PACK], BF16, name="cross_keys%d" % i, align_bytes=64) for i in range(X)]
         cross_codes = [keep.tile([P, W * W], U32, name="cross_codes%d" % i, align_bytes=64) for i in range(X)]
         cross_scales = [keep.tile([P, W * W], U8, name="cross_scales%d" % i, align_bytes=64) for i in range(X)]
         same_keys = keep.tile([P, X, BANK, PACK], BF16, name="same_keys", align_bytes=64)
@@ -222,7 +221,7 @@ def tile_localtrittention_pa_kernel(tc, a, b, c, out_0, out_1):
             nc.scalar.copy(out=a_t[:, n].bitcast(F32), in_=a_words)
             nc.scalar.copy(
                 out=b_shared[n % 2][:].rearrange("p x k t -> p x (k t)").bitcast(F32),
-                in_=b_words.rearrange("p (x k) u -> p x (k u)", x=X)[:, :, 2 * VECTOR_ROWS : 2 * W],
+                in_=b_words.rearrange("p (x k) u -> p x (k u)", x=X)[:, :, 2 * (W - SHARED_ROWS) : 2 * W],
             )
             c_words = turn("c", n)
             for x in range(X):
@@ -261,27 +260,35 @@ def tile_localtrittention_pa_kernel(tc, a, b, c, out_0, out_1):
                 stop=(x == X - 1),
             )
 
-        def cross_product(n, x):
-            rows = slice(x * W, (x + 1) * W)
+        def shared_rows(n):
+            return SHARED_ROWS_AT_END if n == NW - 1 else SHARED_ROWS
+
+        def cross_product_shared(n, x):
+            rows = shared_rows(n)
             nc.gpsimd.tensor_tensor(
-                out=cross_keys[x % 3][:, VECTOR_ROWS:W],
-                in0=a_t[:, n - 1, rows, :].unsqueeze(1).to_broadcast([P, SHARED_ROWS, W, PACK]),
-                in1=b_shared[n % 2][:, x].unsqueeze(2).to_broadcast([P, SHARED_ROWS, W, PACK]),
-                op=ALU.mult,
-            )
-            nc.vector.tensor_tensor(
-                out=cross_keys[x % 3][:, 0:VECTOR_ROWS],
-                in0=a_t[:, n - 1, rows, :].unsqueeze(1).to_broadcast([P, VECTOR_ROWS, W, PACK]),
-                in1=b_in_psum(n)[:, x * W : x * W + VECTOR_ROWS, :].unsqueeze(2).to_broadcast([P, VECTOR_ROWS, W, PACK]),
+                out=cross_keys[x][:, W - rows : W],
+                in0=a_t[:, n - 1, x * W : (x + 1) * W, :].unsqueeze(1).to_broadcast([P, rows, W, PACK]),
+                in1=b_shared[n % 2][:, x, SHARED_ROWS - rows : SHARED_ROWS].unsqueeze(2).to_broadcast([P, rows, W, PACK]),
                 op=ALU.mult,
             )
 
-        def cross_quantise_and_score(n, x):
+        def cross_product(n, x):
+            rows = W - shared_rows(n)
+            nc.vector.tensor_tensor(
+                out=cross_keys[x][:, 0:rows],
+                in0=a_t[:, n - 1, x * W : (x + 1) * W, :].unsqueeze(1).to_broadcast([P, rows, W, PACK]),
+                in1=b_in_psum(n)[:, x * W : x * W + rows, :].unsqueeze(2).to_broadcast([P, rows, W, PACK]),
+                op=ALU.mult,
+            )
+
+        def cross_quantise(x):
             nc.vector.quantize_mx(
                 out=cross_codes[x][:].bitcast(FP8X4),
                 scales=cross_scales[x][:],
-                in_=cross_keys[x % 3][:].rearrange("p k j t -> p (k j t)"),
+                in_=cross_keys[x][:].rearrange("p k j t -> p (k j t)"),
             )
+
+        def score_cross(n, x):
             for half, region in enumerate((CROSS_LOW, CROSS_HIGH)):
                 cols = slice(half * BANK, (half + 1) * BANK)
                 score_pass(n, region, x, cross_codes[x][:, cols], cross_scales[x][:, cols])
@@ -348,30 +355,32 @@ def tile_localtrittention_pa_kernel(tc, a, b, c, out_0, out_1):
                 accum_out=sums[half][n % 2][:, sum_col : sum_col + 1],
             )
 
-        def first_half(n):
+        def first_exponentials(n):
             i = n % 2
             for k in range(1, W):
                 exponential(n, OLD, first_pair(k), k, FIRST, exp_old_j[i][:, k, 0:k], PB_OLD + k)
             for k in range(W):
                 region = CROSS_LOW if k < HALF_W else CROSS_HIGH
                 exponential(n, region, (k % HALF_W) * W, W, FIRST, exp_old_j[i][:, W + k, :], PB_OWN + k)
-            if n < NW - 1:
-                used = 0
-                for j in range(W):
-                    sum_over_k(n, FIRST, exp_old_j[i][:, j + 1 : 2 * W, j], used, PA_OLD + j)
-                    used += 2 * W - 1 - j
 
-        def last_half(n):
+        def first_sums_over_k(n):
+            used = 0
+            for j in range(W):
+                sum_over_k(n, FIRST, exp_old_j[n % 2][:, j + 1 : 2 * W, j], used, PA_OLD + j)
+                used += 2 * W - 1 - j
+
+        def last_exponentials(n):
             i = n % 2
             for k in range(1, W):
                 exponential(n, OWN, first_pair(k), k, LAST, exp_own_j[i][:, k, 0:k], PB_OWN + k)
-            if n < NW - 1:
-                used = W * W + TRI
-                for j in range(W - 1):
-                    sum_over_k(n, LAST, exp_own_j[i][:, j + 1 : W, j], used, PA_OWN + j)
-                    used += W - 1 - j
 
-        def last_sums_over_k(half):
+        def last_sums_over_k(n):
+            used = W * W + TRI
+            for j in range(W - 1):
+                sum_over_k(n, LAST, exp_own_j[n % 2][:, j + 1 : W, j], used, PA_OWN + j)
+                used += W - 1 - j
+
+        def vector_sums_over_k(half):
             i = (NW - 1) % 2
             rows, sum_col = ((exp_old_j[i], PA_OLD), (exp_own_j[i], PA_OWN))[half]
             nc.vector.tensor_reduce(
@@ -409,6 +418,38 @@ def tile_localtrittention_pa_kernel(tc, a, b, c, out_0, out_1):
                 nc.sync.dma_start(out=out_0[x].rearrange("n i j -> i n j"), in_=result[rows, :, 0 : 2 * W])
                 nc.scalar.dma_start(out=out_1[x].rearrange("n i k -> i n k"), in_=result[rows, :, 2 * W : 4 * W])
 
+        def keys(n):
+            return [lambda k=k: same_product(n, k) for k in reversed(range(1, W))]
+
+        def crosses(n):
+            return [lambda x=x: cross_product(n, x) for x in range(X)]
+
+        def last_shift(g):
+            return [lambda: top_of(g, OWN), lambda: shift_of(g, LAST, tops[g % 2][:, OWN : OWN + 1])]
+
+        def first_tops(g):
+            return [lambda: top_of(g, CROSS_LOW), lambda: top_of(g, CROSS_HIGH)] if g > 0 else []
+
+        def first_shift(g):
+            return [lambda: top_of_first_half(g), lambda: shift_of(g, FIRST, top_first[:])]
+
+        def finish(g):
+            return [
+                lambda: add_masked_pairs(g),
+                lambda: add_half(g, FIRST),
+                lambda: add_half(g, LAST),
+                lambda: sum_of_all(g),
+                lambda: invert_sum(g),
+            ]
+
+        def exponentials_and_sums(g):
+            last_exponentials(g)
+            last_sums_over_k(g)
+            if g > 0:
+                first_exponentials(g)
+                first_sums_over_k(g)
+            factors_of(g)
+
         with tc.manual_schedule():
             load_inputs()
             count_rows_and_columns()
@@ -416,68 +457,70 @@ def tile_localtrittention_pa_kernel(tc, a, b, c, out_0, out_1):
             build_constants()
             prepare_window(0)
             build_the_masks()
-            for n in range(NW + 1):
-                before = n - 1
-                makes_keys = n < NW
-                has_cross = 0 < n < NW
-                if has_cross:
-                    score_same(n, OLD, n - 1)
+            for n in range(NW):
+                at_end = n == NW - 1
+                has_cross = n > 0
+                g = n - 1
                 if n + 1 < NW:
                     prepare_window(n + 1)
-
-                long_ones, short_ones = [], []
                 if has_cross:
-                    long_ones += [lambda: cross_product(n, 0)]
-                    for x in range(1, X):
-                        long_ones += [lambda x=x: cross_product(n, x), lambda x=x: cross_quantise_and_score(n, x - 1)]
-                    long_ones += [lambda: cross_quantise_and_score(n, X - 1)]
-                if before >= 0:
-                    short_ones += [
-                        lambda: top_of(before, OWN),
-                        lambda: shift_of(before, LAST, tops[before % 2][:, OWN : OWN + 1]),
-                        lambda: lowest_shift(before),
-                    ]
-                if has_cross:
-                    short_ones += [lambda: top_of(n, OLD)]
-                weave(long_ones, short_ones)
-                if before >= 0:
-                    factors_of(before)
-                    last_half(before)
-
-                long_ones, short_ones = [], []
-                if makes_keys:
-                    long_ones += [lambda k=k: same_product(n, k) for k in reversed(range(1, W))]
-                if has_cross:
-                    short_ones += [lambda: top_of(n, CROSS_LOW)]
-                if before >= 0:
-                    short_ones += [lambda: add_masked_pairs(before)]
-                if has_cross:
-                    short_ones += [lambda: top_of(n, CROSS_HIGH)]
-                if before == NW - 1:
-                    short_ones += [lambda: last_sums_over_k(FIRST)]
-                if before >= 0:
-                    short_ones += [lambda: add_half(before, FIRST)]
-                if makes_keys:
-                    short_ones += [lambda: top_of_first_half(n), lambda: shift_of(n, FIRST, top_first[:])]
-                weave(long_ones[:ROWS_BEFORE_SHORT], [])
-                weave(long_ones[ROWS_BEFORE_SHORT:], short_ones)
-                if has_cross:
-                    first_half(n)
-
-                long_ones, short_ones = [], []
-                if n == 0:
-                    long_ones += [lambda: quantise_queries(0), quantise_the_masks]
-                if n + 1 < NW:
-                    long_ones += [lambda: quantise_queries(n + 1)]
-                if makes_keys:
-                    long_ones += [lambda: same_quantise(n, 0), lambda: same_quantise(n, 1)]
-                if before == NW - 1:
-                    short_ones += [lambda: last_sums_over_k(LAST)]
-                if before >= 0:
-                    short_ones += [lambda: add_half(before, LAST), lambda: sum_of_all(before), lambda: invert_sum(before)]
-                weave(long_ones, short_ones)
-                if makes_keys:
+                    score_same(n, OLD, n - 1)
+                    for x in (X - 1, 0, 1, 2):
+                        cross_product_shared(n, x)
+                if not at_end:
+                    long_ones = (crosses(n) if has_cross else []) + keys(n)
+                    short_ones = []
+                    if g >= 0:
+                        short_ones += last_shift(g) + first_tops(g) + first_shift(g) + [lambda: lowest_shift(g)]
+                    if g >= 1:
+                        short_ones += finish(g - 1)
+                    if has_cross:
+                        short_ones += [lambda: top_of(n, OLD)]
+                    weave(long_ones, short_ones)
+                    if g >= 0:
+                        exponentials_and_sums(g)
+                    if g >= 1:
+                        normalise(g - 1)
+                    if n == 0:
+                        quantise_queries(0)
+                        quantise_the_masks()
+                    quantise_queries(n + 1)
+                    same_quantise(n, 0)
+                    same_quantise(n, 1)
                     score_same(n, OWN, n)
-                if before >= 0:
-                    normalise(before)
+                    if has_cross:
+                        for x in range(X):
+                            cross_quantise(x)
+                            score_cross(n, x)
+                else:
+                    weave(crosses(n), last_shift(g) + first_tops(g))
+                    weave(
+                        [lambda x=x: cross_quantise(x) for x in range(X)],
+                        first_shift(g) + [lambda: lowest_shift(g)] + [lambda: top_of(n, OLD)],
+                    )
+                    exponentials_and_sums(g)
+                    for x in range(X):
+                        score_cross(n, x)
+                    weave(keys(n)[:5], finish(g - 1))
+                    weave(keys(n)[5:], first_tops(n) + first_shift(n))
+                    normalise(g - 1)
+                    first_exponentials(n)
+                    same_quantise(n, 0)
+                    same_quantise(n, 1)
+                    score_same(n, OWN, n)
+
+            last, before = NW - 1, NW - 2
+            for short_one in last_shift(last) + [lambda: lowest_shift(last)] + finish(before):
+                short_one()
+            factors_of(last)
+            last_exponentials(last)
+            normalise(before)
+            vector_sums_over_k(FIRST)
+            add_masked_pairs(last)
+            add_half(last, FIRST)
+            vector_sums_over_k(LAST)
+            add_half(last, LAST)
+            sum_of_all(last)
+            invert_sum(last)
+            normalise(last)
             store_outputs()

@@ -28,9 +28,9 @@ FIRST, LAST, NONE = 0, 1, 2
 PA_OLD, PA_OWN, PB_OLD, PB_OWN = 0, W, 2 * W, 3 * W
 IGNORE = -1000000.0
 INV_DH = 1.0 / DH
-MASKED = -(2.0**100)
-SHARED_ROWS = 11
+SHARED_ROWS = 8
 SHARED_ROWS_AT_END = 6
+MASKED = -(2.0**100)
 
 FLOPS = 2 * W * DH * (X * NW * TRI + X * (NW - 1) * TRI + X * (NW - 1) * W * W)
 
@@ -63,9 +63,11 @@ def tile_localtrittention_pa_kernel(tc, a, b, c, out_0, out_1):
         b_shared = [keep.tile([P, X, SHARED_ROWS, PACK], BF16, name="b_shared%d" % i, align_bytes=64) for i in range(2)]
         ident = keep.tile([P, P], F32, name="ident")
 
-        c_wide = [keep.tile([P, X, P, PACK], BF16, name="c_wide%d" % i, align_bytes=64) for i in range(2)]
-        c_codes = [keep.tile([P, X * P], U32, name="c_codes%d" % i, align_bytes=64) for i in range(2)]
-        c_scales = [keep.tile([P, X * P], U8, name="c_scales%d" % i, align_bytes=64) for i in range(2)]
+        c_t = [keep.tile([P, P, PACK], BF16, name="c_t%d" % i, align_bytes=64) for i in range(2)]
+        c_codes = [keep.tile([P, P], U32, name="c_codes%d" % i, align_bytes=64) for i in range(2)]
+        c_scales = [keep.tile([P, P], U8, name="c_scales%d" % i, align_bytes=64) for i in range(2)]
+        wide_codes = [keep.tile([P, X * (P + W)], U32, name="wide_codes%d" % i, align_bytes=64) for i in range(2)]
+        wide_scales = [keep.tile([P, X * (P + W)], U8, name="wide_scales%d" % i, align_bytes=64) for i in range(2)]
 
         cross_keys = [keep.tile([P, W, W, PACK], BF16, name="cross_keys%d" % i, align_bytes=64) for i in range(X)]
         cross_codes = [keep.tile([P, W * W], U32, name="cross_codes%d" % i, align_bytes=64) for i in range(X)]
@@ -86,17 +88,25 @@ def tile_localtrittention_pa_kernel(tc, a, b, c, out_0, out_1):
 
         exp_old_j = [keep.tile([P, 2 * W, W], F32, name="exp_old_j%d" % i) for i in range(2)]
         exp_own_j = [keep.tile([P, W, W], F32, name="exp_own_j%d" % i) for i in range(2)]
-        unread = keep.tile([P, W * W + 2 * TRI], F32, name="unread")
+        folded = keep.tile([P, W, W], F32, name="folded")
+        folded_last = keep.tile([P, W, W], F32, name="folded_last")
+        unread = keep.tile([P, W * W + TRI], F32, name="unread")
+        gate = keep.tile([P, 1], U32, name="gate")
 
-        tops = [keep.tile([P, 4], F32, name="tops%d" % i) for i in range(2)]
-        top_first = keep.tile([P, 1], F32, name="top_first")
-        shifts = [keep.tile([P, 3], F32, name="shifts%d" % i) for i in range(2)]
-        lowest = [keep.tile([P, 1], F32, name="lowest%d" % i) for i in range(2)]
-        factors = [keep.tile([P, 3], F32, name="factors%d" % i) for i in range(2)]
-        sums = [[keep.tile([P, 4 * W], F32, name="sums%d_%d" % (half, i)) for i in range(2)] for half in (FIRST, LAST)]
+        tops = [keep.tile([P, 5], F32, name="tops%d" % i) for i in range(2)]
+        top = [keep.tile([P, 1], F32, name="top%d" % i) for i in range(2)]
+        shift = [keep.tile([P, 1], F32, name="shift%d" % i) for i in range(2)]
+        masked_part = [keep.tile([P, 1], F32, name="masked_part%d" % i) for i in range(2)]
+        sums = [keep.tile([P, 4 * W], F32, name="sums%d" % i) for i in range(2)]
+        own_rows = [keep.tile([P, W], F32, name="own_rows%d" % i) for i in range(2)]
         full = [keep.tile([P, 4 * W], F32, name="full%d" % i) for i in range(2)]
         total = keep.tile([P, 1], F32, name="total")
         scale = [keep.tile([P, 1], F32, name="scale%d" % i) for i in range(2)]
+        top_first = keep.tile([P, 1], F32, name="top_first")
+        half_shifts = keep.tile([P, 3], F32, name="half_shifts")
+        lowest = keep.tile([P, 1], F32, name="lowest")
+        factors = keep.tile([P, 3], F32, name="factors")
+        half_sums = [keep.tile([P, 4 * W], F32, name="half_sums%d" % half) for half in (FIRST, LAST)]
         result = keep.tile([P, NW, 4 * W], F32, name="result")
 
         p_minus_c_int = keep.tile([P, W], I32, name="p_minus_c_int")
@@ -118,11 +128,10 @@ def tile_localtrittention_pa_kernel(tc, a, b, c, out_0, out_1):
         def mask_of(region):
             return region - 1
 
-        def load_inputs():
-            for n in range(NW):
-                for name, src in (("a", a), ("b", b), ("c", c)):
-                    for x in range(X):
-                        nc.sync.dma_start(out=raw[name][x * W : (x + 1) * W, n, :], in_=src[x, n])
+        def load_window(n):
+            for name, src, queue in (("a", a, nc.sync), ("b", b, nc.scalar if n == 0 else nc.sync), ("c", c, nc.sync)):
+                for x in range(X):
+                    queue.dma_start(out=raw[name][x * W : (x + 1) * W, n, :], in_=src[x, n])
 
         def count_rows_and_columns():
             for x in range(X):
@@ -132,15 +141,20 @@ def tile_localtrittention_pa_kernel(tc, a, b, c, out_0, out_1):
 
         def fill_what_is_never_written():
             nc.gpsimd.memset(mask_keys[:].bitcast(F32), 0.0)
-            nc.gpsimd.memset(exp_old_j[(NW - 1) % 2][:, 0:W, :], 0.0)
-            nc.gpsimd.memset(exp_own_j[(NW - 1) % 2][:], 0.0)
+            for i in range(2):
+                nc.gpsimd.memset(exp_old_j[i][:], 0.0)
+                nc.gpsimd.memset(exp_own_j[i][:], 0.0)
             nc.vector.memset(mask_queries[:].bitcast(I32), 0)
             for i in range(2):
-                nc.vector.memset(c_wide[i][:].bitcast(I32), 0)
-                nc.vector.memset(sums[FIRST][i][:], 0.0)
-                nc.vector.memset(sums[LAST][i][:], 0.0)
-                nc.vector.memset(tops[i][:], MASKED)
-                nc.vector.memset(shifts[i][:, NONE : NONE + 1], -IGNORE * INV_DH)
+                nc.vector.memset(wide_codes[i][:].bitcast(I32), 0)
+                nc.vector.memset(wide_scales[i][:].bitcast(I32), 0)
+                nc.vector.memset(c_scales[i][:].bitcast(I32), 0)
+                nc.vector.memset(sums[i][:], 0.0)
+                nc.vector.memset(own_rows[i][:], 0.0)
+                nc.vector.memset(half_sums[i][:], 0.0)
+                nc.vector.memset(tops[i][:, 0:4], MASKED)
+                nc.vector.memset(tops[i][:, 4:5], IGNORE)
+            nc.vector.memset(half_shifts[:, NONE : NONE + 1], -IGNORE * INV_DH)
             nc.vector.memset(same_keys[:, :, TRI:BANK, :], 0.0)
 
         def build_constants():
@@ -223,17 +237,19 @@ def tile_localtrittention_pa_kernel(tc, a, b, c, out_0, out_1):
                 out=b_shared[n % 2][:].rearrange("p x k t -> p x (k t)").bitcast(F32),
                 in_=b_words.rearrange("p (x k) u -> p x (k u)", x=X)[:, :, 2 * (W - SHARED_ROWS) : 2 * W],
             )
-            c_words = turn("c", n)
-            for x in range(X):
-                rows = slice(x * W, (x + 1) * W)
-                nc.scalar.copy(out=c_wide[n % 2][:, x, rows, :].bitcast(F32), in_=c_words[:, rows, :])
+            nc.scalar.copy(out=c_t[n % 2][:].bitcast(F32), in_=turn("c", n))
 
         def quantise_queries(n):
             nc.vector.quantize_mx(
                 out=c_codes[n % 2][:].bitcast(FP8X4),
                 scales=c_scales[n % 2][:],
-                in_=c_wide[n % 2][:].rearrange("p x r t -> p (x r t)"),
+                in_=c_t[n % 2][:].rearrange("p r t -> p (r t)"),
             )
+            for wide, narrow, words in ((wide_codes, c_codes, W), (wide_scales, c_scales, W // PACK)):
+                nc.sync.dma_start(
+                    out=wide[n % 2][:].bitcast(I32).rearrange("p (x q) -> p x q", x=X)[:, :, 0:words],
+                    in_=narrow[n % 2][:].bitcast(I32).rearrange("p (x i) -> p x i", x=X),
+                )
 
         def mask_pass(n, region):
             nc.tensor.matmul_mx(
@@ -252,8 +268,8 @@ def tile_localtrittention_pa_kernel(tc, a, b, c, out_0, out_1):
             cols = slice(x * P, (x + 1) * P)
             nc.tensor.matmul_mx(
                 out=bank(n, region)[:],
-                lhsT=c_codes[n % 2][:, cols].bitcast(FP8X4),
-                lhsT_scale=c_scales[n % 2][:, cols],
+                lhsT=wide_codes[n % 2][:, cols].bitcast(FP8X4),
+                lhsT_scale=wide_scales[n % 2][:, cols],
                 rhs=codes.bitcast(FP8X4),
                 rhs_scale=scales,
                 start=(x == 0 and region == OLD),
@@ -321,206 +337,273 @@ def tile_localtrittention_pa_kernel(tc, a, b, c, out_0, out_1):
                 out=tops[n % 2][:, region : region + 1], in_=bank(n, region)[:, 0:width], axis=AXIS_X, op=ALU.max
             )
 
-        def top_of_first_half(n):
-            nc.vector.tensor_reduce(out=top_first[:], in_=tops[n % 2][:, OLD : CROSS_HIGH + 1], axis=AXIS_X, op=ALU.max)
+        def top_of_all(g):
+            nc.vector.tensor_reduce(out=top[g % 2][:], in_=tops[g % 2][:], axis=AXIS_X, op=ALU.max)
 
-        def shift_of(n, half, top):
+        def shift_of(g):
+            nc.scalar.activation(out=shift[g % 2][:], in_=top[g % 2][:], func=ACT.Copy, scale=-INV_DH)
+            nc.scalar.activation(
+                out=masked_part[g % 2][:], in_=tops[g % 2][:, 4:5], func=ACT.Exp, bias=shift[g % 2][:, 0:1], scale=INV_DH
+            )
+
+        def top_of_first_half():
+            nc.vector.tensor_reduce(out=top_first[:], in_=tops[(NW - 1) % 2][:, OLD : CROSS_HIGH + 1], axis=AXIS_X, op=ALU.max)
+
+        def half_shift_of(half, half_top):
             nc.vector.tensor_scalar(
-                out=shifts[n % 2][:, half : half + 1], in0=top, scalar1=IGNORE, scalar2=-INV_DH, op0=ALU.max, op1=ALU.mult
+                out=half_shifts[:, half : half + 1], in0=half_top, scalar1=IGNORE, scalar2=-INV_DH, op0=ALU.max, op1=ALU.mult
             )
 
-        def lowest_shift(n):
-            nc.vector.tensor_reduce(out=lowest[n % 2][:], in_=shifts[n % 2][:], axis=AXIS_X, op=ALU.min)
+        def lowest_shift():
+            nc.vector.tensor_reduce(out=lowest[:], in_=half_shifts[:], axis=AXIS_X, op=ALU.min)
 
-        def factors_of(n):
-            nc.scalar.activation(
-                out=factors[n % 2][:], in_=shifts[n % 2][:], func=ACT.Exp, bias=lowest[n % 2][:, 0:1], scale=-1.0
-            )
+        def factors_of_halves():
+            nc.scalar.activation(out=factors[:], in_=half_shifts[:], func=ACT.Exp, bias=lowest[:, 0:1], scale=-1.0)
 
-        def exponential(n, region, first_col, width, half, out, sum_col):
+        def exponential(n, region, k, first_col, width, row):
+            own_half = LAST if region == OWN else FIRST
+            if n == NW - 1:
+                bias, target = half_shifts[:, own_half : own_half + 1], half_sums[own_half]
+            else:
+                bias, target = shift[n % 2][:, 0:1], sums[n % 2]
+            if region == OLD:
+                sum_col = PB_OLD + k
+            else:
+                sum_col = PB_OWN + k
+                if region == OWN and n < NW - 1:
+                    target, sum_col = own_rows[n % 2], k
             nc.scalar.activation(
-                out=out,
+                out=row,
                 in_=bank(n, region)[:, first_col : first_col + width],
                 func=ACT.Exp,
-                bias=shifts[n % 2][:, half : half + 1],
+                bias=bias,
                 scale=INV_DH,
-                accum_out=sums[half][n % 2][:, sum_col : sum_col + 1],
+                accum_out=target[:, sum_col : sum_col + 1],
             )
 
-        def sum_over_k(n, half, column, first_unread, sum_col):
-            nc.scalar.activation(
-                out=unread[:, first_unread : first_unread + column.shape[1]],
-                in_=column,
-                func=ACT.Copy,
-                accum_out=sums[half][n % 2][:, sum_col : sum_col + 1],
-            )
-
-        def first_exponentials(n):
-            i = n % 2
+        def old_exponentials(n):
             for k in range(1, W):
-                exponential(n, OLD, first_pair(k), k, FIRST, exp_old_j[i][:, k, 0:k], PB_OLD + k)
+                exponential(n, OLD, k, first_pair(k), k, exp_old_j[n % 2][:, k, 0:k])
+
+        def cross_exponentials(n):
             for k in range(W):
                 region = CROSS_LOW if k < HALF_W else CROSS_HIGH
-                exponential(n, region, (k % HALF_W) * W, W, FIRST, exp_old_j[i][:, W + k, :], PB_OWN + k)
+                exponential(n, region, k, (k % HALF_W) * W, W, exp_old_j[n % 2][:, W + k, :])
 
-        def first_sums_over_k(n):
+        def own_exponentials(n):
+            for k in range(1, W):
+                exponential(n, OWN, k, first_pair(k), k, exp_own_j[n % 2][:, k, 0:k])
+
+        def scalar_sums_over_k(n):
             used = 0
             for j in range(W):
-                sum_over_k(n, FIRST, exp_old_j[n % 2][:, j + 1 : 2 * W, j], used, PA_OLD + j)
-                used += 2 * W - 1 - j
+                column = exp_old_j[n % 2][:, j + 1 : 2 * W, j]
+                nc.scalar.activation(
+                    out=unread[:, used : used + column.shape[1]],
+                    in_=column,
+                    func=ACT.Copy,
+                    accum_out=sums[n % 2][:, PA_OLD + j : PA_OLD + j + 1],
+                )
+                used += column.shape[1]
 
-        def last_exponentials(n):
-            i = n % 2
-            for k in range(1, W):
-                exponential(n, OWN, first_pair(k), k, LAST, exp_own_j[i][:, k, 0:k], PB_OWN + k)
+        def gpsimd_sums_over_k(n, rows, sum_col):
+            count = rows.shape[1] // 2
+            while count >= 1:
+                out = folded[:, 0:count, :] if count > 1 else sums[n % 2][:, sum_col : sum_col + W].unsqueeze(1)
+                nc.gpsimd.tensor_tensor(out=out, in0=rows[:, 0:count, :], in1=rows[:, count : 2 * count, :], op=ALU.add)
+                rows = folded
+                count //= 2
 
-        def last_sums_over_k(n):
-            used = W * W + TRI
-            for j in range(W - 1):
-                sum_over_k(n, LAST, exp_own_j[n % 2][:, j + 1 : W, j], used, PA_OWN + j)
-                used += W - 1 - j
-
-        def vector_sums_over_k(half):
-            i = (NW - 1) % 2
-            rows, sum_col = ((exp_old_j[i], PA_OLD), (exp_own_j[i], PA_OWN))[half]
+        def vector_sums_over_k(half, rows, sum_col):
+            count = rows.shape[1] // 2
+            while count >= HALF_W:
+                nc.vector.tensor_tensor(
+                    out=folded_last[:, 0:count, :], in0=rows[:, 0:count, :], in1=rows[:, count : 2 * count, :], op=ALU.add
+                )
+                rows = folded_last
+                count //= 2
             nc.vector.tensor_reduce(
-                out=sums[half][i][:, sum_col : sum_col + W], in_=rows[:].rearrange("p k j -> p j k"), axis=AXIS_X, op=ALU.add
+                out=half_sums[half][:, sum_col : sum_col + W],
+                in_=rows[:, 0:HALF_W, :].rearrange("p k j -> p j k"),
+                axis=AXIS_X,
+                op=ALU.add,
             )
 
-        def add_masked_pairs(n):
-            masked = masked_first if n == 0 else masked_later
-            nc.vector.tensor_scalar(
-                out=full[n % 2][:], in0=masked[:], scalar1=factors[n % 2][:, NONE : NONE + 1], scalar2=None, op0=ALU.mult
-            )
-
-        def add_half(n, half):
+        def add_masked_pairs(g):
             nc.vector.scalar_tensor_tensor(
-                out=full[n % 2][:],
-                in0=sums[half][n % 2][:],
-                scalar=factors[n % 2][:, half : half + 1],
-                in1=full[n % 2][:],
+                out=full[g % 2][:],
+                in0=(masked_first if g == 0 else masked_later)[:],
+                scalar=masked_part[g % 2][:, 0:1],
+                in1=sums[g % 2][:],
                 op0=ALU.mult,
                 op1=ALU.add,
             )
 
-        def sum_of_all(n):
-            nc.vector.tensor_reduce(out=total[:], in_=full[n % 2][:, 0 : 2 * W], axis=AXIS_X, op=ALU.add)
+        def add_own_rows(g):
+            pb_own = full[g % 2][:, PB_OWN : PB_OWN + W]
+            nc.vector.tensor_tensor(out=pb_own, in0=pb_own, in1=own_rows[g % 2][:], op=ALU.add)
 
-        def invert_sum(n):
-            nc.vector.reciprocal(out=scale[n % 2][:], in_=total[:])
+        def add_masked_pairs_to_halves():
+            nc.vector.tensor_scalar(
+                out=full[(NW - 1) % 2][:], in0=masked_later[:], scalar1=factors[:, NONE : NONE + 1], scalar2=None, op0=ALU.mult
+            )
 
-        def normalise(n):
-            nc.scalar.activation(out=result[:, n, :], in_=full[n % 2][:], func=ACT.Copy, scale=scale[n % 2][:, 0:1])
+        def add_half(half):
+            whole = full[(NW - 1) % 2][:]
+            nc.vector.scalar_tensor_tensor(
+                out=whole, in0=half_sums[half][:], scalar=factors[:, half : half + 1], in1=whole, op0=ALU.mult, op1=ALU.add
+            )
 
-        def store_outputs():
+        def sum_of_all(g):
+            nc.vector.tensor_reduce(out=total[:], in_=full[g % 2][:, 0 : 2 * W], axis=AXIS_X, op=ALU.add)
+
+        def invert_sum(g):
+            nc.vector.reciprocal(out=scale[g % 2][:], in_=total[:])
+
+        def normalise(g):
+            nc.scalar.activation(out=result[:, g, :], in_=full[g % 2][:], func=ACT.Copy, scale=scale[g % 2][:, 0:1])
+
+        def normalise_last():
+            g = NW - 1
+            nc.vector.tensor_scalar(
+                out=result[:, g, :], in0=full[g % 2][:], scalar1=scale[g % 2][:, 0:1], scalar2=None, op0=ALU.mult
+            )
+
+        def store_outputs(first, end):
             for x in range(X):
                 rows = slice(x * W, (x + 1) * W)
-                nc.sync.dma_start(out=out_0[x].rearrange("n i j -> i n j"), in_=result[rows, :, 0 : 2 * W])
-                nc.scalar.dma_start(out=out_1[x].rearrange("n i k -> i n k"), in_=result[rows, :, 2 * W : 4 * W])
+                nc.sync.dma_start(
+                    out=out_0[x].rearrange("n i j -> i n j")[:, first:end], in_=result[rows, first:end, 0 : 2 * W]
+                )
+                nc.scalar.dma_start(
+                    out=out_1[x].rearrange("n i k -> i n k")[:, first:end], in_=result[rows, first:end, 2 * W : 4 * W]
+                )
 
         def keys(n):
-            return [lambda k=k: same_product(n, k) for k in reversed(range(1, W))]
+            return [lambda k=k: same_product(n, k) for k in range(1, W)]
 
         def crosses(n):
             return [lambda x=x: cross_product(n, x) for x in range(X)]
 
-        def last_shift(g):
-            return [lambda: top_of(g, OWN), lambda: shift_of(g, LAST, tops[g % 2][:, OWN : OWN + 1])]
-
-        def first_tops(g):
-            return [lambda: top_of(g, CROSS_LOW), lambda: top_of(g, CROSS_HIGH)] if g > 0 else []
-
-        def first_shift(g):
-            return [lambda: top_of_first_half(g), lambda: shift_of(g, FIRST, top_first[:])]
+        def tops_of(g):
+            regions = (CROSS_LOW, CROSS_HIGH, OWN) if g > 0 else (OWN,)
+            return [lambda region=region: top_of(g, region) for region in regions] + [lambda: top_of_all(g)]
 
         def finish(g):
             return [
                 lambda: add_masked_pairs(g),
-                lambda: add_half(g, FIRST),
-                lambda: add_half(g, LAST),
+                lambda: add_own_rows(g),
                 lambda: sum_of_all(g),
                 lambda: invert_sum(g),
             ]
 
-        def exponentials_and_sums(g):
-            last_exponentials(g)
-            last_sums_over_k(g)
-            if g > 0:
-                first_exponentials(g)
-                first_sums_over_k(g)
-            factors_of(g)
+        def wait_for_quantising():
+            nc.gpsimd.tensor_copy(out=gate[:], in_=cross_codes[X - 1][:, 0:1])
 
         with tc.manual_schedule():
-            load_inputs()
+            load_window(0)
             count_rows_and_columns()
             fill_what_is_never_written()
             build_constants()
             prepare_window(0)
+            load_window(1)
             build_the_masks()
-            for n in range(NW):
-                at_end = n == NW - 1
+            for n in range(NW - 1):
                 has_cross = n > 0
                 g = n - 1
-                if n + 1 < NW:
-                    prepare_window(n + 1)
+                prepare_window(n + 1)
+                if n + 2 < NW:
+                    load_window(n + 2)
                 if has_cross:
                     score_same(n, OLD, n - 1)
-                    for x in (X - 1, 0, 1, 2):
-                        cross_product_shared(n, x)
-                if not at_end:
-                    long_ones = (crosses(n) if has_cross else []) + keys(n)
-                    short_ones = []
-                    if g >= 0:
-                        short_ones += last_shift(g) + first_tops(g) + first_shift(g) + [lambda: lowest_shift(g)]
                     if g >= 1:
-                        short_ones += finish(g - 1)
-                    if has_cross:
-                        short_ones += [lambda: top_of(n, OLD)]
-                    weave(long_ones, short_ones)
-                    if g >= 0:
-                        exponentials_and_sums(g)
+                        wait_for_quantising()
+                        gpsimd_sums_over_k(g - 1, exp_own_j[(g - 1) % 2], PA_OWN)
+                    for x in range(X):
+                        cross_product_shared(n, x)
+                if n == 0:
+                    weave(keys(0)[:HALF_W], [])
+                    quantise_queries(0)
+                    weave(keys(0)[HALF_W:], [])
+                    quantise_the_masks()
+                else:
+                    long_ones = crosses(n) + keys(n)
+                    weave(long_ones[:-10], tops_of(g) + [lambda: top_of(n, OLD)])
+                    weave(long_ones[-10:], finish(g - 1) if g >= 1 else [])
+                if g >= 0:
+                    shift_of(g)
+                    if g > 0:
+                        cross_exponentials(g)
+                        old_exponentials(g)
+                    own_exponentials(g)
+                    if g > 0:
+                        scalar_sums_over_k(g)
                     if g >= 1:
                         normalise(g - 1)
-                    if n == 0:
-                        quantise_queries(0)
-                        quantise_the_masks()
-                    quantise_queries(n + 1)
-                    same_quantise(n, 0)
-                    same_quantise(n, 1)
-                    score_same(n, OWN, n)
-                    if has_cross:
-                        for x in range(X):
-                            cross_quantise(x)
-                            score_cross(n, x)
-                else:
-                    weave(crosses(n), last_shift(g) + first_tops(g))
-                    weave(
-                        [lambda x=x: cross_quantise(x) for x in range(X)],
-                        first_shift(g) + [lambda: lowest_shift(g)] + [lambda: top_of(n, OLD)],
-                    )
-                    exponentials_and_sums(g)
+                quantise_queries(n + 1)
+                same_quantise(n, 0)
+                same_quantise(n, 1)
+                score_same(n, OWN, n)
+                if has_cross:
                     for x in range(X):
+                        cross_quantise(x)
                         score_cross(n, x)
-                    weave(keys(n)[:5], finish(g - 1))
-                    weave(keys(n)[5:], first_tops(n) + first_shift(n))
-                    normalise(g - 1)
-                    first_exponentials(n)
-                    same_quantise(n, 0)
-                    same_quantise(n, 1)
-                    score_same(n, OWN, n)
 
-            last, before = NW - 1, NW - 2
-            for short_one in last_shift(last) + [lambda: lowest_shift(last)] + finish(before):
+            n, g = NW - 1, NW - 2
+            score_same(n, OLD, n - 1)
+            wait_for_quantising()
+            for x in range(X):
+                cross_product_shared(n, x)
+            gpsimd_sums_over_k(g - 1, exp_own_j[(g - 1) % 2], PA_OWN)
+            cross_product(n, 0)
+            top_of(g, CROSS_LOW)
+            top_of(g, CROSS_HIGH)
+            top_of(g, OWN)
+            cross_product(n, 1)
+            top_of_all(g)
+            shift_of(g)
+            weave([lambda: cross_product(n, 2), lambda: cross_product(n, 3)], [lambda: top_of(n, OLD)])
+            for x in range(X):
+                cross_quantise(x)
+            old_exponentials(g)
+            cross_exponentials(g)
+            own_exponentials(g)
+            for x in range(X):
+                score_cross(n, x)
+            weave(keys(n)[:HALF_W], [])
+            weave(
+                keys(n)[HALF_W:],
+                finish(g - 1)
+                + [
+                    lambda: top_of(n, CROSS_LOW),
+                    lambda: top_of(n, CROSS_HIGH),
+                    top_of_first_half,
+                    lambda: half_shift_of(FIRST, top_first[:]),
+                ],
+            )
+            normalise(g - 1)
+            store_outputs(0, g)
+            cross_exponentials(n)
+            old_exponentials(n)
+            gpsimd_sums_over_k(g, exp_own_j[g % 2], PA_OWN)
+            gpsimd_sums_over_k(g, exp_old_j[g % 2], PA_OLD)
+            same_quantise(n, 0)
+            same_quantise(n, 1)
+            score_same(n, OWN, n)
+            top_of(n, OWN)
+            half_shift_of(LAST, tops[n % 2][:, OWN : OWN + 1])
+            lowest_shift()
+            factors_of_halves()
+            own_exponentials(n)
+            vector_sums_over_k(FIRST, exp_old_j[n % 2], PA_OLD)
+            for short_one in finish(g):
                 short_one()
-            factors_of(last)
-            last_exponentials(last)
-            normalise(before)
-            vector_sums_over_k(FIRST)
-            add_masked_pairs(last)
-            add_half(last, FIRST)
-            vector_sums_over_k(LAST)
-            add_half(last, LAST)
-            sum_of_all(last)
-            invert_sum(last)
-            normalise(last)
-            store_outputs()
+            normalise(g)
+            add_masked_pairs_to_halves()
+            add_half(FIRST)
+            vector_sums_over_k(LAST, exp_own_j[n % 2], PA_OWN)
+            add_half(LAST)
+            sum_of_all(n)
+            invert_sum(n)
+            normalise_last()
+            store_outputs(g, NW)

@@ -28,8 +28,10 @@ FIRST, LAST, NONE = 0, 1, 2
 PA_OLD, PA_OWN, PB_OLD, PB_OWN = 0, W, 2 * W, 3 * W
 IGNORE = -1000000.0
 INV_DH = 1.0 / DH
-SHARED_ROWS = 8
-SHARED_ROWS_AT_END = 6
+SHARED_ROWS = 5
+SHARED_ROWS_AT_END = 4
+LAST_ROWS = 8
+ROWS_BEFORE_TOPS = 6
 MASKED = -(2.0**100)
 
 FLOPS = 2 * W * DH * (X * NW * TRI + X * (NW - 1) * TRI + X * (NW - 1) * W * W)
@@ -390,6 +392,25 @@ def tile_localtrittention_pa_kernel(tc, a, b, c, out_0, out_1):
                 region = CROSS_LOW if k < HALF_W else CROSS_HIGH
                 exponential(n, region, k, (k % HALF_W) * W, W, exp_old_j[n % 2][:, W + k, :])
 
+        def cross_exponentials_of_last():
+            for half, region in enumerate((CROSS_LOW, CROSS_HIGH)):
+                rows = slice(W + half * HALF_W, W + (half + 1) * HALF_W)
+                nc.scalar.activation(
+                    out=exp_old_j[(NW - 1) % 2][:, rows, :].rearrange("p k j -> p (k j)"),
+                    in_=bank(NW - 1, region)[:],
+                    func=ACT.Exp,
+                    bias=half_shifts[:, FIRST : FIRST + 1],
+                    scale=INV_DH,
+                )
+
+        def cross_sums_over_j_of_last():
+            nc.vector.tensor_reduce(
+                out=half_sums[FIRST][:, PB_OWN : PB_OWN + W],
+                in_=exp_old_j[(NW - 1) % 2][:, W : 2 * W, :],
+                axis=AXIS_X,
+                op=ALU.add,
+            )
+
         def own_exponentials(n):
             for k in range(1, W):
                 exponential(n, OWN, k, first_pair(k), k, exp_own_j[n % 2][:, k, 0:k])
@@ -416,7 +437,7 @@ def tile_localtrittention_pa_kernel(tc, a, b, c, out_0, out_1):
 
         def vector_sums_over_k(half, rows, sum_col):
             count = rows.shape[1] // 2
-            while count >= HALF_W:
+            while count >= LAST_ROWS:
                 nc.vector.tensor_tensor(
                     out=folded_last[:, 0:count, :], in0=rows[:, 0:count, :], in1=rows[:, count : 2 * count, :], op=ALU.add
                 )
@@ -424,7 +445,7 @@ def tile_localtrittention_pa_kernel(tc, a, b, c, out_0, out_1):
                 count //= 2
             nc.vector.tensor_reduce(
                 out=half_sums[half][:, sum_col : sum_col + W],
-                in_=rows[:, 0:HALF_W, :].rearrange("p k j -> p j k"),
+                in_=rows[:, 0:LAST_ROWS, :].rearrange("p k j -> p j k"),
                 axis=AXIS_X,
                 op=ALU.add,
             )
@@ -570,20 +591,20 @@ def tile_localtrittention_pa_kernel(tc, a, b, c, out_0, out_1):
             own_exponentials(g)
             for x in range(X):
                 score_cross(n, x)
-            weave(keys(n)[:HALF_W], [])
+            weave(keys(n)[:ROWS_BEFORE_TOPS], [])
             weave(
-                keys(n)[HALF_W:],
-                finish(g - 1)
-                + [
+                keys(n)[ROWS_BEFORE_TOPS:],
+                [
                     lambda: top_of(n, CROSS_LOW),
                     lambda: top_of(n, CROSS_HIGH),
                     top_of_first_half,
                     lambda: half_shift_of(FIRST, top_first[:]),
-                ],
+                ]
+                + finish(g - 1),
             )
             normalise(g - 1)
             store_outputs(0, g)
-            cross_exponentials(n)
+            cross_exponentials_of_last()
             old_exponentials(n)
             gpsimd_sums_over_k(g, exp_own_j[g % 2], PA_OWN)
             gpsimd_sums_over_k(g, exp_old_j[g % 2], PA_OLD)
@@ -595,6 +616,7 @@ def tile_localtrittention_pa_kernel(tc, a, b, c, out_0, out_1):
             lowest_shift()
             factors_of_halves()
             own_exponentials(n)
+            cross_sums_over_j_of_last()
             vector_sums_over_k(FIRST, exp_old_j[n % 2], PA_OLD)
             for short_one in finish(g):
                 short_one()

@@ -28,8 +28,6 @@ FIRST, LAST, NONE = 0, 1, 2
 PA_OLD, PA_OWN, PB_OLD, PB_OWN = 0, W, 2 * W, 3 * W
 IGNORE = -1000000.0
 INV_DH = 1.0 / DH
-SHARED_ROWS = 5
-SHARED_ROWS_AT_END = 4
 LAST_ROWS = 8
 ROWS_BEFORE_TOPS = 6
 MASKED = -(2.0**100)
@@ -62,7 +60,6 @@ def tile_localtrittention_pa_kernel(tc, a, b, c, out_0, out_1):
             "c": keep.tile([P, NW, DH], BF16, name="raw_c"),
         }
         a_t = keep.tile([P, NW, P, PACK], BF16, name="a_t", align_bytes=64)
-        b_shared = [keep.tile([P, X, SHARED_ROWS, PACK], BF16, name="b_shared%d" % i, align_bytes=64) for i in range(2)]
         ident = keep.tile([P, P], F32, name="ident")
 
         c_t = [keep.tile([P, P, PACK], BF16, name="c_t%d" % i, align_bytes=64) for i in range(2)]
@@ -92,8 +89,7 @@ def tile_localtrittention_pa_kernel(tc, a, b, c, out_0, out_1):
         exp_own_j = [keep.tile([P, W, W], F32, name="exp_own_j%d" % i) for i in range(2)]
         folded = keep.tile([P, W, W], F32, name="folded")
         folded_last = keep.tile([P, W, W], F32, name="folded_last")
-        unread = keep.tile([P, W * W + TRI], F32, name="unread")
-        gate = keep.tile([P, 1], U32, name="gate")
+        unread = keep.tile([P, W * W + 2 * TRI], F32, name="unread")
 
         tops = [keep.tile([P, 5], F32, name="tops%d" % i) for i in range(2)]
         top = [keep.tile([P, 1], F32, name="top%d" % i) for i in range(2)]
@@ -233,12 +229,8 @@ def tile_localtrittention_pa_kernel(tc, a, b, c, out_0, out_1):
 
         def prepare_window(n):
             a_words = turn("a", n)
-            b_words = turn("b", n)
+            turn("b", n)
             nc.scalar.copy(out=a_t[:, n].bitcast(F32), in_=a_words)
-            nc.scalar.copy(
-                out=b_shared[n % 2][:].rearrange("p x k t -> p x (k t)").bitcast(F32),
-                in_=b_words.rearrange("p (x k) u -> p x (k u)", x=X)[:, :, 2 * (W - SHARED_ROWS) : 2 * W],
-            )
             nc.scalar.copy(out=c_t[n % 2][:].bitcast(F32), in_=turn("c", n))
 
         def quantise_queries(n):
@@ -278,24 +270,12 @@ def tile_localtrittention_pa_kernel(tc, a, b, c, out_0, out_1):
                 stop=(x == X - 1),
             )
 
-        def shared_rows(n):
-            return SHARED_ROWS_AT_END if n == NW - 1 else SHARED_ROWS
-
-        def cross_product_shared(n, x):
-            rows = shared_rows(n)
-            nc.gpsimd.tensor_tensor(
-                out=cross_keys[x][:, W - rows : W],
-                in0=a_t[:, n - 1, x * W : (x + 1) * W, :].unsqueeze(1).to_broadcast([P, rows, W, PACK]),
-                in1=b_shared[n % 2][:, x, SHARED_ROWS - rows : SHARED_ROWS].unsqueeze(2).to_broadcast([P, rows, W, PACK]),
-                op=ALU.mult,
-            )
-
         def cross_product(n, x):
-            rows = W - shared_rows(n)
+            rows = slice(x * W, (x + 1) * W)
             nc.vector.tensor_tensor(
-                out=cross_keys[x][:, 0:rows],
-                in0=a_t[:, n - 1, x * W : (x + 1) * W, :].unsqueeze(1).to_broadcast([P, rows, W, PACK]),
-                in1=b_in_psum(n)[:, x * W : x * W + rows, :].unsqueeze(2).to_broadcast([P, rows, W, PACK]),
+                out=cross_keys[x][:],
+                in0=a_t[:, n - 1, rows, :].unsqueeze(1).to_broadcast([P, W, W, PACK]),
+                in1=b_in_psum(n)[:, rows, :].unsqueeze(2).to_broadcast([P, W, W, PACK]),
                 op=ALU.mult,
             )
 
@@ -418,14 +398,17 @@ def tile_localtrittention_pa_kernel(tc, a, b, c, out_0, out_1):
         def scalar_sums_over_k(n):
             used = 0
             for j in range(W):
-                column = exp_old_j[n % 2][:, j + 1 : 2 * W, j]
-                nc.scalar.activation(
-                    out=unread[:, used : used + column.shape[1]],
-                    in_=column,
-                    func=ACT.Copy,
-                    accum_out=sums[n % 2][:, PA_OLD + j : PA_OLD + j + 1],
-                )
-                used += column.shape[1]
+                columns = [(exp_own_j[n % 2][:, j + 1 : W, j], PA_OWN + j)] if j < W - 1 else []
+                if n > 0:
+                    columns.append((exp_old_j[n % 2][:, j + 1 : 2 * W, j], PA_OLD + j))
+                for column, sum_col in columns:
+                    nc.scalar.activation(
+                        out=unread[:, used : used + column.shape[1]],
+                        in_=column,
+                        func=ACT.Copy,
+                        accum_out=sums[n % 2][:, sum_col : sum_col + 1],
+                    )
+                    used += column.shape[1]
 
         def gpsimd_sums_over_k(n, rows, sum_col):
             count = rows.shape[1] // 2
@@ -518,9 +501,6 @@ def tile_localtrittention_pa_kernel(tc, a, b, c, out_0, out_1):
                 lambda: invert_sum(g),
             ]
 
-        def wait_for_quantising():
-            nc.gpsimd.tensor_copy(out=gate[:], in_=cross_codes[X - 1][:, 0:1])
-
         with tc.manual_schedule():
             load_window(0)
             count_rows_and_columns()
@@ -537,11 +517,6 @@ def tile_localtrittention_pa_kernel(tc, a, b, c, out_0, out_1):
                     load_window(n + 2)
                 if has_cross:
                     score_same(n, OLD, n - 1)
-                    if g >= 1:
-                        wait_for_quantising()
-                        gpsimd_sums_over_k(g - 1, exp_own_j[(g - 1) % 2], PA_OWN)
-                    for x in range(X):
-                        cross_product_shared(n, x)
                 if n == 0:
                     weave(keys(0)[:HALF_W], [])
                     quantise_queries(0)
@@ -557,8 +532,7 @@ def tile_localtrittention_pa_kernel(tc, a, b, c, out_0, out_1):
                         cross_exponentials(g)
                         old_exponentials(g)
                     own_exponentials(g)
-                    if g > 0:
-                        scalar_sums_over_k(g)
+                    scalar_sums_over_k(g)
                     if g >= 1:
                         normalise(g - 1)
                 quantise_queries(n + 1)
@@ -572,10 +546,6 @@ def tile_localtrittention_pa_kernel(tc, a, b, c, out_0, out_1):
 
             n, g = NW - 1, NW - 2
             score_same(n, OLD, n - 1)
-            wait_for_quantising()
-            for x in range(X):
-                cross_product_shared(n, x)
-            gpsimd_sums_over_k(g - 1, exp_own_j[(g - 1) % 2], PA_OWN)
             cross_product(n, 0)
             top_of(g, CROSS_LOW)
             top_of(g, CROSS_HIGH)

@@ -36,7 +36,8 @@ FLOPS = 2 * W * DH * (X * NW * TRI + X * (NW - 1) * TRI + X * (NW - 1) * W * W)
 
 
 def first_pair(k):
-    return k * (k - 1) // 2
+    u = k % HALF_W
+    return HALF_W * u + u * u - (u if k < HALF_W else 0)
 
 
 def weave(long_ones, short_ones):
@@ -75,12 +76,12 @@ def tile_localtrittention_pa_kernel(tc, a, b, c, out_0, out_1):
         same_codes = [keep.tile([P, X, BANK], U32, name="same_codes%d" % i, align_bytes=64) for i in range(2)]
         same_scales = [keep.tile([P, X, BANK], U8, name="same_scales%d" % i, align_bytes=64) for i in range(2)]
 
-        mask_queries = keep.tile([P, P, PACK], BF16, name="mask_queries", align_bytes=64)
-        mask_query_codes = keep.tile([P, P], U32, name="mask_query_codes", align_bytes=64)
-        mask_query_scales = keep.tile([P, P], U8, name="mask_query_scales", align_bytes=64)
-        mask_keys = keep.tile([P, 3, BANK, PACK], BF16, name="mask_keys", align_bytes=64)
-        mask_key_codes = keep.tile([P, 3, BANK], U32, name="mask_key_codes", align_bytes=64)
-        mask_key_scales = keep.tile([P, 3, BANK], U8, name="mask_key_scales", align_bytes=64)
+        mask_queries = keep.tile([P, 2, P, PACK], BF16, name="mask_queries", align_bytes=64)
+        mask_query_codes = keep.tile([P, 2, P], U32, name="mask_query_codes", align_bytes=64)
+        mask_query_scales = keep.tile([P, 2, P], U8, name="mask_query_scales", align_bytes=64)
+        mask_keys = keep.tile([P, 2, BANK, PACK], BF16, name="mask_keys", align_bytes=64)
+        mask_key_codes = keep.tile([P, 2, BANK], U32, name="mask_key_codes", align_bytes=64)
+        mask_key_scales = keep.tile([P, 2, BANK], U8, name="mask_key_scales", align_bytes=64)
 
         banks = [psum.tile([P, BANK], F32, name="bank%d" % i) for i in range(SCORE_BANKS)]
         turned = [psum.tile([P, BANK], F32, name="turned%d" % i) for i in range(2)]
@@ -89,7 +90,8 @@ def tile_localtrittention_pa_kernel(tc, a, b, c, out_0, out_1):
         exp_own_j = [keep.tile([P, W, W], F32, name="exp_own_j%d" % i) for i in range(2)]
         folded = keep.tile([P, W, W], F32, name="folded")
         folded_last = keep.tile([P, W, W], F32, name="folded_last")
-        unread = keep.tile([P, W * W + 2 * TRI], F32, name="unread")
+        unread = keep.tile([P, W * W + TRI], F32, name="unread")
+        gate = keep.tile([P, 1], U32, name="gate")
 
         tops = [keep.tile([P, 5], F32, name="tops%d" % i) for i in range(2)]
         top = [keep.tile([P, 1], F32, name="top%d" % i) for i in range(2)]
@@ -118,13 +120,11 @@ def tile_localtrittention_pa_kernel(tc, a, b, c, out_0, out_1):
         masked_first = keep.tile([P, 4 * W], F32, name="masked_first")
         masked_later = keep.tile([P, 4 * W], F32, name="masked_later")
 
-        make_identity(nc, ident[:])
-
         def bank(n, region):
             return banks[(4 * n + region) % SCORE_BANKS]
 
-        def mask_of(region):
-            return region - 1
+        def masks_of(region):
+            return (1 if region == CROSS_HIGH else 0), (0 if region == OWN else 1)
 
         def load_window(n):
             for name, src, queue in (("a", a, nc.sync), ("b", b, nc.scalar if n == 0 else nc.sync), ("c", c, nc.sync)):
@@ -132,33 +132,36 @@ def tile_localtrittention_pa_kernel(tc, a, b, c, out_0, out_1):
                     queue.dma_start(out=raw[name][x * W : (x + 1) * W, n, :], in_=src[x, n])
 
         def count_rows_and_columns():
+            nc.gpsimd.iota(p_minus_c_int[:], pattern=[[-1, W]], base=0, channel_multiplier=1)
+            make_identity(nc, ident[:])
             for x in range(X):
                 nc.gpsimd.iota(i_minus_c_int[x * W : (x + 1) * W, :], pattern=[[-1, W]], base=0, channel_multiplier=1)
             nc.gpsimd.iota(col_int[:], pattern=[[1, W]], base=0, channel_multiplier=0)
-            nc.gpsimd.iota(p_minus_c_int[:], pattern=[[-1, W]], base=0, channel_multiplier=1)
 
         def fill_what_is_never_written():
-            nc.gpsimd.memset(mask_keys[:].bitcast(F32), 0.0)
+            nc.gpsimd.memset(mask_keys[:, 1].bitcast(I32), 0)
+            nc.gpsimd.memset(mask_keys[:, 0].bitcast(I32), 0)
+            nc.gpsimd.memset(same_keys[:, :, TRI:BANK, :], 0.0)
             for i in range(2):
-                nc.gpsimd.memset(exp_old_j[i][:], 0.0)
-                nc.gpsimd.memset(exp_own_j[i][:], 0.0)
-            nc.vector.memset(mask_queries[:].bitcast(I32), 0)
-            for i in range(2):
-                nc.vector.memset(wide_codes[i][:].bitcast(I32), 0)
-                nc.vector.memset(wide_scales[i][:].bitcast(I32), 0)
-                nc.vector.memset(c_scales[i][:].bitcast(I32), 0)
-                nc.vector.memset(sums[i][:], 0.0)
-                nc.vector.memset(own_rows[i][:], 0.0)
-                nc.vector.memset(half_sums[i][:], 0.0)
+                nc.gpsimd.memset(wide_codes[i][:].bitcast(I32), 0)
+                nc.gpsimd.memset(wide_scales[i][:].bitcast(I32), 0)
+                nc.gpsimd.memset(c_scales[i][:].bitcast(I32), 0)
+                nc.gpsimd.memset(sums[i][:], 0.0)
+                nc.gpsimd.memset(own_rows[i][:], 0.0)
+                nc.gpsimd.memset(half_sums[i][:], 0.0)
                 nc.vector.memset(tops[i][:, 0:4], MASKED)
                 nc.vector.memset(tops[i][:, 4:5], IGNORE)
-            nc.vector.memset(half_shifts[:, NONE : NONE + 1], -IGNORE * INV_DH)
-            nc.vector.memset(same_keys[:, :, TRI:BANK, :], 0.0)
+            nc.gpsimd.memset(half_shifts[:, NONE : NONE + 1], -IGNORE * INV_DH)
+
+        def clear_exponentials():
+            zero = p_minus_c[:, 0:1].unsqueeze(2).to_broadcast([P, W, W])
+            for i in range(2):
+                for rows in (exp_own_j[i][:], exp_old_j[i][:, 0:W, :]):
+                    nc.scalar.activation(out=rows, in_=zero, func=ACT.Copy, scale=0.0)
 
         def build_constants():
             nc.vector.tensor_copy(out=i_minus_c[:], in_=i_minus_c_int[:])
             nc.vector.tensor_copy(out=col[:], in_=col_int[:])
-            nc.vector.tensor_copy(out=p_minus_c[:], in_=p_minus_c_int[:])
             nc.vector.tensor_scalar(out=seen[:], in0=i_minus_c[:], scalar1=0.0, scalar2=None, op0=ALU.is_ge)
             nc.vector.tensor_scalar(
                 out=masked_later[:, 0:W], in0=i_minus_c[:], scalar1=-1.0, scalar2=1.0 * W, op0=ALU.mult, op1=ALU.add
@@ -179,40 +182,43 @@ def tile_localtrittention_pa_kernel(tc, a, b, c, out_0, out_1):
             )
 
         def build_the_masks():
-            nc.vector.tensor_scalar(
-                out=mask_queries[:].rearrange("p (x i) t -> p x i t", x=X)[:, :, :, 0],
-                in0=p_minus_c[:].unsqueeze(1).to_broadcast([P, X, W]),
-                scalar1=0.0,
-                scalar2=None,
-                op0=ALU.is_gt,
-            )
-            for region, first_k in ((CROSS_LOW, 0), (CROSS_HIGH, HALF_W)):
-                nc.scalar.activation(
-                    out=mask_keys[:, mask_of(region)].rearrange("p (k j) t -> p k j t", j=W)[:, :, :, 0],
-                    in_=ident[:, first_k : first_k + HALF_W].unsqueeze(2).to_broadcast([P, HALF_W, W]),
-                    func=ACT.Copy,
-                    scale=MASKED,
+            nc.vector.memset(mask_queries[:].bitcast(I32), 0)
+            nc.vector.tensor_copy(out=p_minus_c[:], in_=p_minus_c_int[:])
+            for high in range(2):
+                nc.vector.tensor_scalar(
+                    out=mask_queries[:, high].rearrange("p (x i) t -> p x i t", x=X)[:, :, :, 0],
+                    in0=p_minus_c[:].unsqueeze(1).to_broadcast([P, X, W]),
+                    scalar1=-1.0 * HALF_W * high,
+                    scalar2=None,
+                    op0=ALU.is_gt,
                 )
+            nc.scalar.activation(
+                out=mask_keys[:, 1].rearrange("p (k j) t -> p k j t", j=W)[:, :, :, 0],
+                in_=ident[:, 0:HALF_W].unsqueeze(2).to_broadcast([P, HALF_W, W]),
+                func=ACT.Copy,
+                scale=MASKED,
+            )
             for k in range(1, W):
                 nc.scalar.activation(
-                    out=mask_keys[:, mask_of(OWN), first_pair(k) : first_pair(k) + k, 0],
+                    out=mask_keys[:, 0, first_pair(k) : first_pair(k) + k, 0],
                     in_=ident[:, k : k + 1].to_broadcast([P, k]),
                     func=ACT.Copy,
                     scale=MASKED,
                 )
 
-        def quantise_the_masks():
+        def quantise_mask_queries():
             nc.vector.quantize_mx(
-                out=mask_query_codes[:].bitcast(FP8X4),
-                scales=mask_query_scales[:],
-                in_=mask_queries[:].rearrange("p q t -> p (q t)"),
+                out=mask_query_codes[:].rearrange("p h q -> p (h q)").bitcast(FP8X4),
+                scales=mask_query_scales[:].rearrange("p h q -> p (h q)"),
+                in_=mask_queries[:].rearrange("p h q t -> p (h q t)"),
             )
-            for region in (OWN, CROSS_LOW, CROSS_HIGH):
-                nc.vector.quantize_mx(
-                    out=mask_key_codes[:, mask_of(region), :].bitcast(FP8X4),
-                    scales=mask_key_scales[:, mask_of(region), :],
-                    in_=mask_keys[:, mask_of(region)].rearrange("p c t -> p (c t)"),
-                )
+
+        def quantise_mask_keys(table):
+            nc.vector.quantize_mx(
+                out=mask_key_codes[:, table, :].bitcast(FP8X4),
+                scales=mask_key_scales[:, table, :],
+                in_=mask_keys[:, table].rearrange("p c t -> p (c t)"),
+            )
 
         def turn(name, n):
             words = raw[name][:, n, :].bitcast(F32)
@@ -230,7 +236,7 @@ def tile_localtrittention_pa_kernel(tc, a, b, c, out_0, out_1):
         def prepare_window(n):
             a_words = turn("a", n)
             turn("b", n)
-            nc.scalar.copy(out=a_t[:, n].bitcast(F32), in_=a_words)
+            (nc.vector.tensor_copy if n == 0 else nc.scalar.copy)(out=a_t[:, n].bitcast(F32), in_=a_words)
             nc.scalar.copy(out=c_t[n % 2][:].bitcast(F32), in_=turn("c", n))
 
         def quantise_queries(n):
@@ -246,12 +252,13 @@ def tile_localtrittention_pa_kernel(tc, a, b, c, out_0, out_1):
                 )
 
         def mask_pass(n, region):
+            queries, keys_of_mask = masks_of(region)
             nc.tensor.matmul_mx(
                 out=bank(n, region)[:],
-                lhsT=mask_query_codes[:].bitcast(FP8X4),
-                lhsT_scale=mask_query_scales[:],
-                rhs=mask_key_codes[:, mask_of(region), :].bitcast(FP8X4),
-                rhs_scale=mask_key_scales[:, mask_of(region), :],
+                lhsT=mask_query_codes[:, queries, :].bitcast(FP8X4),
+                lhsT_scale=mask_query_scales[:, queries, :],
+                rhs=mask_key_codes[:, keys_of_mask, :].bitcast(FP8X4),
+                rhs_scale=mask_key_scales[:, keys_of_mask, :],
                 start=True,
                 stop=False,
             )
@@ -343,24 +350,18 @@ def tile_localtrittention_pa_kernel(tc, a, b, c, out_0, out_1):
             nc.scalar.activation(out=factors[:], in_=half_shifts[:], func=ACT.Exp, bias=lowest[:, 0:1], scale=-1.0)
 
         def exponential(n, region, k, first_col, width, row):
-            own_half = LAST if region == OWN else FIRST
+            scores = bank(n, region)[:, first_col : first_col + width]
             if n == NW - 1:
-                bias, target = half_shifts[:, own_half : own_half + 1], half_sums[own_half]
+                half = LAST if region == OWN else FIRST
+                nc.scalar.activation(out=row, in_=scores, func=ACT.Exp, bias=half_shifts[:, half : half + 1], scale=INV_DH)
+                return
+            if region == OWN:
+                sum_out = own_rows[n % 2][:, k : k + 1]
             else:
-                bias, target = shift[n % 2][:, 0:1], sums[n % 2]
-            if region == OLD:
-                sum_col = PB_OLD + k
-            else:
-                sum_col = PB_OWN + k
-                if region == OWN and n < NW - 1:
-                    target, sum_col = own_rows[n % 2], k
+                sum_col = (PB_OLD if region == OLD else PB_OWN) + k
+                sum_out = sums[n % 2][:, sum_col : sum_col + 1]
             nc.scalar.activation(
-                out=row,
-                in_=bank(n, region)[:, first_col : first_col + width],
-                func=ACT.Exp,
-                bias=bias,
-                scale=INV_DH,
-                accum_out=target[:, sum_col : sum_col + 1],
+                out=row, in_=scores, func=ACT.Exp, bias=shift[n % 2][:, 0:1], scale=INV_DH, accum_out=sum_out
             )
 
         def old_exponentials(n):
@@ -383,12 +384,9 @@ def tile_localtrittention_pa_kernel(tc, a, b, c, out_0, out_1):
                     scale=INV_DH,
                 )
 
-        def cross_sums_over_j_of_last():
+        def sums_over_j_of_last(half, rows, sum_col):
             nc.vector.tensor_reduce(
-                out=half_sums[FIRST][:, PB_OWN : PB_OWN + W],
-                in_=exp_old_j[(NW - 1) % 2][:, W : 2 * W, :],
-                axis=AXIS_X,
-                op=ALU.add,
+                out=half_sums[half][:, sum_col : sum_col + rows.shape[1]], in_=rows[:], axis=AXIS_X, op=ALU.add
             )
 
         def own_exponentials(n):
@@ -398,17 +396,14 @@ def tile_localtrittention_pa_kernel(tc, a, b, c, out_0, out_1):
         def scalar_sums_over_k(n):
             used = 0
             for j in range(W):
-                columns = [(exp_own_j[n % 2][:, j + 1 : W, j], PA_OWN + j)] if j < W - 1 else []
-                if n > 0:
-                    columns.append((exp_old_j[n % 2][:, j + 1 : 2 * W, j], PA_OLD + j))
-                for column, sum_col in columns:
-                    nc.scalar.activation(
-                        out=unread[:, used : used + column.shape[1]],
-                        in_=column,
-                        func=ACT.Copy,
-                        accum_out=sums[n % 2][:, sum_col : sum_col + 1],
-                    )
-                    used += column.shape[1]
+                column = exp_old_j[n % 2][:, j + 1 : 2 * W, j]
+                nc.scalar.activation(
+                    out=unread[:, used : used + column.shape[1]],
+                    in_=column,
+                    func=ACT.Copy,
+                    accum_out=(half_sums[FIRST] if n == NW - 1 else sums[n % 2])[:, PA_OLD + j : PA_OLD + j + 1],
+                )
+                used += column.shape[1]
 
         def gpsimd_sums_over_k(n, rows, sum_col):
             count = rows.shape[1] // 2
@@ -501,14 +496,19 @@ def tile_localtrittention_pa_kernel(tc, a, b, c, out_0, out_1):
                 lambda: invert_sum(g),
             ]
 
+        def wait_for_quantising():
+            nc.gpsimd.tensor_copy(out=gate[:], in_=cross_codes[X - 1][:, 0:1])
+
         with tc.manual_schedule():
             load_window(0)
             count_rows_and_columns()
             fill_what_is_never_written()
+            build_the_masks()
             build_constants()
+            quantise_mask_queries()
             prepare_window(0)
             load_window(1)
-            build_the_masks()
+            clear_exponentials()
             for n in range(NW - 1):
                 has_cross = n > 0
                 g = n - 1
@@ -517,11 +517,15 @@ def tile_localtrittention_pa_kernel(tc, a, b, c, out_0, out_1):
                     load_window(n + 2)
                 if has_cross:
                     score_same(n, OLD, n - 1)
+                if g >= 1:
+                    wait_for_quantising()
+                    gpsimd_sums_over_k(g - 1, exp_own_j[(g - 1) % 2], PA_OWN)
                 if n == 0:
                     weave(keys(0)[:HALF_W], [])
                     quantise_queries(0)
                     weave(keys(0)[HALF_W:], [])
-                    quantise_the_masks()
+                    quantise_mask_keys(0)
+                    quantise_mask_keys(1)
                 else:
                     long_ones = crosses(n) + keys(n)
                     weave(long_ones[:-10], tops_of(g) + [lambda: top_of(n, OLD)])
@@ -532,7 +536,8 @@ def tile_localtrittention_pa_kernel(tc, a, b, c, out_0, out_1):
                         cross_exponentials(g)
                         old_exponentials(g)
                     own_exponentials(g)
-                    scalar_sums_over_k(g)
+                    if g > 0:
+                        scalar_sums_over_k(g)
                     if g >= 1:
                         normalise(g - 1)
                 quantise_queries(n + 1)
@@ -546,6 +551,8 @@ def tile_localtrittention_pa_kernel(tc, a, b, c, out_0, out_1):
 
             n, g = NW - 1, NW - 2
             score_same(n, OLD, n - 1)
+            wait_for_quantising()
+            gpsimd_sums_over_k(g - 1, exp_own_j[(g - 1) % 2], PA_OWN)
             cross_product(n, 0)
             top_of(g, CROSS_LOW)
             top_of(g, CROSS_HIGH)
@@ -576,23 +583,24 @@ def tile_localtrittention_pa_kernel(tc, a, b, c, out_0, out_1):
             store_outputs(0, g)
             cross_exponentials_of_last()
             old_exponentials(n)
+            scalar_sums_over_k(n)
             gpsimd_sums_over_k(g, exp_own_j[g % 2], PA_OWN)
             gpsimd_sums_over_k(g, exp_old_j[g % 2], PA_OLD)
             same_quantise(n, 0)
             same_quantise(n, 1)
             score_same(n, OWN, n)
+            sums_over_j_of_last(FIRST, exp_old_j[n % 2], PB_OLD)
             top_of(n, OWN)
             half_shift_of(LAST, tops[n % 2][:, OWN : OWN + 1])
             lowest_shift()
             factors_of_halves()
             own_exponentials(n)
-            cross_sums_over_j_of_last()
-            vector_sums_over_k(FIRST, exp_old_j[n % 2], PA_OLD)
             for short_one in finish(g):
                 short_one()
             normalise(g)
             add_masked_pairs_to_halves()
             add_half(FIRST)
+            sums_over_j_of_last(LAST, exp_own_j[n % 2], PB_OWN)
             vector_sums_over_k(LAST, exp_own_j[n % 2], PA_OWN)
             add_half(LAST)
             sum_of_all(n)

@@ -22,12 +22,17 @@ HALF_W = W // 2
 DH = 512
 TRI = W * (W - 1) // 2
 BANK = 512
-SCORE_BANKS = 6
+SCORE_BANKS = 5
 OLD, CROSS_LOW, CROSS_HIGH, OWN = 0, 1, 2, 3
 FIRST, LAST, NONE = 0, 1, 2
-PA_OLD, PA_OWN, PB_OLD, PB_OWN = 0, W, 2 * W, 3 * W
+PB_OLD, PA_OLD, PB_OWN, PA_OWN = 0, W, 2 * W, 3 * W
+TOP_SQUARE = HALF_W * HALF_W
+LEVELS = (16, 8, 4, 2, 1)
 IGNORE = -1000000.0
 INV_DH = 1.0 / DH
+SHARED_ROWS = 5
+SCALAR_ROWS = 3
+VECTOR_ROWS = W - SHARED_ROWS - SCALAR_ROWS
 LAST_ROWS = 8
 ROWS_BEFORE_TOPS = 6
 MASKED = -(2.0**100)
@@ -35,9 +40,8 @@ MASKED = -(2.0**100)
 FLOPS = 2 * W * DH * (X * NW * TRI + X * (NW - 1) * TRI + X * (NW - 1) * W * W)
 
 
-def first_pair(k):
-    u = k % HALF_W
-    return HALF_W * u + u * u - (u if k < HALF_W else 0)
+def squares(size):
+    return 512 - 32 * size, 512 - 16 * size
 
 
 def weave(long_ones, short_ones):
@@ -61,6 +65,8 @@ def tile_localtrittention_pa_kernel(tc, a, b, c, out_0, out_1):
             "c": keep.tile([P, NW, DH], BF16, name="raw_c"),
         }
         a_t = keep.tile([P, NW, P, PACK], BF16, name="a_t", align_bytes=64)
+        b_shared = [keep.tile([P, X, SHARED_ROWS, PACK], BF16, name="b_shared%d" % i, align_bytes=64) for i in range(2)]
+        b_scalar = [keep.tile([P, X, SCALAR_ROWS, PACK], F32, name="b_scalar%d" % i) for i in range(2)]
         ident = keep.tile([P, P], F32, name="ident")
 
         c_t = [keep.tile([P, P, PACK], BF16, name="c_t%d" % i, align_bytes=64) for i in range(2)]
@@ -86,19 +92,22 @@ def tile_localtrittention_pa_kernel(tc, a, b, c, out_0, out_1):
         banks = [psum.tile([P, BANK], F32, name="bank%d" % i) for i in range(SCORE_BANKS)]
         turned = [psum.tile([P, BANK], F32, name="turned%d" % i) for i in range(2)]
 
-        exp_old_j = [keep.tile([P, 2 * W, W], F32, name="exp_old_j%d" % i) for i in range(2)]
-        exp_own_j = [keep.tile([P, W, W], F32, name="exp_own_j%d" % i) for i in range(2)]
-        folded = keep.tile([P, W, W], F32, name="folded")
-        folded_last = keep.tile([P, W, W], F32, name="folded_last")
-        unread = keep.tile([P, W * W + TRI], F32, name="unread")
+        sums_turned = psum.tile([P, BANK], F32, name="sums_turned")
+
+        exp_same = [keep.tile([P, 2, BANK], F32, name="exp_same%d" % i) for i in range(2)]
+        exp_cross = [keep.tile([P, W, W], F32, name="exp_cross%d" % i) for i in range(2)]
+        exp_turned = [keep.tile([P, PACK, P], F32, name="exp_turned%d" % i) for i in range(2)]
+        members = [keep.tile([P, BANK], F32, name="members%d" % i) for i in range(2)]
+        table = keep.tile([P, PACK, 2 * W], F32, name="table")
+        unread = keep.tile([P, W * W], F32, name="unread")
+        folded = keep.tile([P, HALF_W, W], F32, name="folded")
         gate = keep.tile([P, 1], U32, name="gate")
 
         tops = [keep.tile([P, 5], F32, name="tops%d" % i) for i in range(2)]
         top = [keep.tile([P, 1], F32, name="top%d" % i) for i in range(2)]
         shift = [keep.tile([P, 1], F32, name="shift%d" % i) for i in range(2)]
         masked_part = [keep.tile([P, 1], F32, name="masked_part%d" % i) for i in range(2)]
-        sums = [keep.tile([P, 4 * W], F32, name="sums%d" % i) for i in range(2)]
-        own_rows = [keep.tile([P, W], F32, name="own_rows%d" % i) for i in range(2)]
+        sums = [keep.tile([P, 2 * W], F32, name="sums%d" % i) for i in range(2)]
         full = [keep.tile([P, 4 * W], F32, name="full%d" % i) for i in range(2)]
         total = keep.tile([P, 1], F32, name="total")
         scale = [keep.tile([P, 1], F32, name="scale%d" % i) for i in range(2)]
@@ -106,7 +115,6 @@ def tile_localtrittention_pa_kernel(tc, a, b, c, out_0, out_1):
         half_shifts = keep.tile([P, 3], F32, name="half_shifts")
         lowest = keep.tile([P, 1], F32, name="lowest")
         factors = keep.tile([P, 3], F32, name="factors")
-        half_sums = [keep.tile([P, 4 * W], F32, name="half_sums%d" % half) for half in (FIRST, LAST)]
         result = keep.tile([P, NW, 4 * W], F32, name="result")
 
         p_minus_c_int = keep.tile([P, W], I32, name="p_minus_c_int")
@@ -122,6 +130,9 @@ def tile_localtrittention_pa_kernel(tc, a, b, c, out_0, out_1):
 
         def bank(n, region):
             return banks[(4 * n + region) % SCORE_BANKS]
+
+        def place_of(region):
+            return 1 if region == OWN else 0
 
         def masks_of(region):
             return (1 if region == CROSS_HIGH else 0), (0 if region == OWN else 1)
@@ -143,42 +154,67 @@ def tile_localtrittention_pa_kernel(tc, a, b, c, out_0, out_1):
             nc.gpsimd.memset(mask_keys[:, 0].bitcast(I32), 0)
             nc.gpsimd.memset(same_keys[:, :, TRI:BANK, :], 0.0)
             for i in range(2):
+                nc.gpsimd.memset(members[i][:, TRI:BANK], 0.0)
+            for i in range(2):
                 nc.gpsimd.memset(wide_codes[i][:].bitcast(I32), 0)
                 nc.gpsimd.memset(wide_scales[i][:].bitcast(I32), 0)
                 nc.gpsimd.memset(c_scales[i][:].bitcast(I32), 0)
+                nc.gpsimd.memset(exp_same[i][:], 0.0)
                 nc.gpsimd.memset(sums[i][:], 0.0)
-                nc.gpsimd.memset(own_rows[i][:], 0.0)
-                nc.gpsimd.memset(half_sums[i][:], 0.0)
                 nc.vector.memset(tops[i][:, 0:4], MASKED)
                 nc.vector.memset(tops[i][:, 4:5], IGNORE)
             nc.gpsimd.memset(half_shifts[:, NONE : NONE + 1], -IGNORE * INV_DH)
 
-        def clear_exponentials():
-            zero = p_minus_c[:, 0:1].unsqueeze(2).to_broadcast([P, W, W])
+        def build_the_table():
+            for size in LEVELS:
+                first, end = squares(size)
+                halves = ident[:, 0:W].rearrange("p (s h w) -> p s h w", h=2, w=size)
+                shape = [P, HALF_W // size, size, size]
+                views = (
+                    halves[:, :, 1, :].unsqueeze(3).to_broadcast(shape),
+                    halves[:, :, 0, :].unsqueeze(2).to_broadcast(shape),
+                )
+                for i in range(2):
+                    nc.scalar.copy(
+                        out=members[i][:, first:end].rearrange("p (s k j) -> p s k j", k=size, j=size), in_=views[i]
+                    )
+                nc.scalar.activation(
+                    out=mask_keys[:, 0, first:end, 0].rearrange("p (s k j) -> p s k j", k=size, j=size),
+                    in_=views[0],
+                    func=ACT.Copy,
+                    scale=MASKED,
+                )
             for i in range(2):
-                for rows in (exp_own_j[i][:], exp_old_j[i][:, 0:W, :]):
-                    nc.scalar.activation(out=rows, in_=zero, func=ACT.Copy, scale=0.0)
+                for piece in range(PACK):
+                    cols = slice(piece * P, (piece + 1) * P)
+                    nc.tensor.transpose(sums_turned[:, cols], members[i][:, cols], ident[:])
+                nc.scalar.copy(
+                    out=table[:, :, i * W : (i + 1) * W],
+                    in_=sums_turned[:].rearrange("p (c r) -> p c r", c=PACK)[:, :, 0:W],
+                )
 
         def build_constants():
             nc.vector.tensor_copy(out=i_minus_c[:], in_=i_minus_c_int[:])
             nc.vector.tensor_copy(out=col[:], in_=col_int[:])
             nc.vector.tensor_scalar(out=seen[:], in0=i_minus_c[:], scalar1=0.0, scalar2=None, op0=ALU.is_ge)
+            old_j, own_j = slice(PA_OLD, PA_OLD + W), slice(PA_OWN, PA_OWN + W)
+            old_k, own_k = slice(PB_OLD, PB_OLD + W), slice(PB_OWN, PB_OWN + W)
             nc.vector.tensor_scalar(
-                out=masked_later[:, 0:W], in0=i_minus_c[:], scalar1=-1.0, scalar2=1.0 * W, op0=ALU.mult, op1=ALU.add
+                out=masked_later[:, old_j], in0=i_minus_c[:], scalar1=-1.0, scalar2=1.0 * W, op0=ALU.mult, op1=ALU.add
             )
             nc.vector.tensor_scalar(out=work[:], in0=i_minus_c[:], scalar1=0.0, scalar2=-1.0, op0=ALU.max, op1=ALU.mult)
-            nc.vector.tensor_scalar(out=masked_later[:, W : 2 * W], in0=work[:], scalar1=2.0 * W, scalar2=None, op0=ALU.add)
+            nc.vector.tensor_scalar(out=masked_later[:, own_j], in0=work[:], scalar1=2.0 * W, scalar2=None, op0=ALU.add)
             nc.vector.tensor_scalar(
-                out=masked_later[:, 2 * W : 3 * W], in0=col[:], scalar1=-1.0, scalar2=2.0 * W, op0=ALU.mult, op1=ALU.add
+                out=masked_later[:, old_k], in0=col[:], scalar1=-1.0, scalar2=2.0 * W, op0=ALU.mult, op1=ALU.add
             )
             nc.vector.tensor_scalar(out=work[:], in0=col[:], scalar1=1.0 * W, scalar2=-1.0, op0=ALU.add, op1=ALU.mult)
             nc.vector.tensor_tensor(out=work[:], in0=work[:], in1=seen[:], op=ALU.mult)
-            nc.vector.tensor_scalar(out=masked_later[:, 3 * W : 4 * W], in0=work[:], scalar1=2.0 * W, scalar2=None, op0=ALU.add)
+            nc.vector.tensor_scalar(out=masked_later[:, own_k], in0=work[:], scalar1=2.0 * W, scalar2=None, op0=ALU.add)
             nc.vector.memset(masked_first[:], 2.0 * W)
-            nc.vector.tensor_copy(out=masked_first[:, W : 2 * W], in_=masked_later[:, W : 2 * W])
+            nc.vector.tensor_copy(out=masked_first[:, own_j], in_=masked_later[:, own_j])
             nc.vector.tensor_tensor(out=work[:], in0=col[:], in1=seen[:], op=ALU.mult)
             nc.vector.tensor_scalar(
-                out=masked_first[:, 3 * W : 4 * W], in0=work[:], scalar1=-1.0, scalar2=2.0 * W, op0=ALU.mult, op1=ALU.add
+                out=masked_first[:, own_k], in0=work[:], scalar1=-1.0, scalar2=2.0 * W, op0=ALU.mult, op1=ALU.add
             )
 
         def build_the_masks():
@@ -198,13 +234,6 @@ def tile_localtrittention_pa_kernel(tc, a, b, c, out_0, out_1):
                 func=ACT.Copy,
                 scale=MASKED,
             )
-            for k in range(1, W):
-                nc.scalar.activation(
-                    out=mask_keys[:, 0, first_pair(k) : first_pair(k) + k, 0],
-                    in_=ident[:, k : k + 1].to_broadcast([P, k]),
-                    func=ACT.Copy,
-                    scale=MASKED,
-                )
 
         def quantise_mask_queries():
             nc.vector.quantize_mx(
@@ -235,8 +264,17 @@ def tile_localtrittention_pa_kernel(tc, a, b, c, out_0, out_1):
 
         def prepare_window(n):
             a_words = turn("a", n)
-            turn("b", n)
+            b_words = turn("b", n)
             (nc.vector.tensor_copy if n == 0 else nc.scalar.copy)(out=a_t[:, n].bitcast(F32), in_=a_words)
+            if n > 0:
+                nc.scalar.copy(
+                    out=b_shared[n % 2][:].rearrange("p x k t -> p x (k t)").bitcast(F32),
+                    in_=b_words.rearrange("p (x k) u -> p x (k u)", x=X)[:, :, 2 * (W - SHARED_ROWS) : 2 * W],
+                )
+                nc.scalar.copy(
+                    out=b_scalar[n % 2][:],
+                    in_=b_in_psum(n).rearrange("p (x k) t -> p x k t", x=X)[:, :, VECTOR_ROWS : VECTOR_ROWS + SCALAR_ROWS],
+                )
             nc.scalar.copy(out=c_t[n % 2][:].bitcast(F32), in_=turn("c", n))
 
         def quantise_queries(n):
@@ -277,12 +315,31 @@ def tile_localtrittention_pa_kernel(tc, a, b, c, out_0, out_1):
                 stop=(x == X - 1),
             )
 
+        def cross_product_shared(n, x):
+            shape = [P, SHARED_ROWS, W, PACK]
+            nc.gpsimd.tensor_tensor(
+                out=cross_keys[x][:, W - SHARED_ROWS : W],
+                in0=a_t[:, n - 1, x * W : (x + 1) * W, :].unsqueeze(1).to_broadcast(shape),
+                in1=b_shared[n % 2][:, x].unsqueeze(2).to_broadcast(shape),
+                op=ALU.mult,
+            )
+
+        def cross_product_scalar(n, x):
+            for kk in range(SCALAR_ROWS):
+                for t in range(PACK):
+                    nc.scalar.activation(
+                        out=cross_keys[x][:, VECTOR_ROWS + kk, :, t],
+                        in_=a_t[:, n - 1, x * W : (x + 1) * W, t],
+                        func=ACT.Copy,
+                        scale=b_scalar[n % 2][:, x, kk, t : t + 1],
+                    )
+
         def cross_product(n, x):
-            rows = slice(x * W, (x + 1) * W)
+            shape = [P, VECTOR_ROWS, W, PACK]
             nc.vector.tensor_tensor(
-                out=cross_keys[x][:],
-                in0=a_t[:, n - 1, rows, :].unsqueeze(1).to_broadcast([P, W, W, PACK]),
-                in1=b_in_psum(n)[:, rows, :].unsqueeze(2).to_broadcast([P, W, W, PACK]),
+                out=cross_keys[x][:, 0:VECTOR_ROWS],
+                in0=a_t[:, n - 1, x * W : (x + 1) * W, :].unsqueeze(1).to_broadcast(shape),
+                in1=b_in_psum(n)[:, x * W : x * W + VECTOR_ROWS, :].unsqueeze(2).to_broadcast(shape),
                 op=ALU.mult,
             )
 
@@ -298,13 +355,25 @@ def tile_localtrittention_pa_kernel(tc, a, b, c, out_0, out_1):
                 cols = slice(half * BANK, (half + 1) * BANK)
                 score_pass(n, region, x, cross_codes[x][:, cols], cross_scales[x][:, cols])
 
-        def same_product(n, k):
-            a_win = a_t[:, n].rearrange("p (x w) t -> p x w t", x=X)
-            b_win = b_in_psum(n).rearrange("p (x w) t -> p x w t", x=X)
+        def same_product_of_head(n, x):
+            shape = [P, HALF_W, HALF_W, PACK]
             nc.vector.tensor_tensor(
-                out=same_keys[:, :, first_pair(k) : first_pair(k) + k, :],
-                in0=a_win[:, :, 0:k, :],
-                in1=b_win[:, :, k : k + 1, :].to_broadcast([P, X, k, PACK]),
+                out=same_keys[:, x, 0:TOP_SQUARE, :].rearrange("p (k j) t -> p k j t", j=HALF_W),
+                in0=a_t[:, n, x * W : x * W + HALF_W, :].unsqueeze(1).to_broadcast(shape),
+                in1=b_in_psum(n)[:, x * W + HALF_W : (x + 1) * W, :].unsqueeze(2).to_broadcast(shape),
+                op=ALU.mult,
+            )
+
+        def same_product(n, size, kk):
+            first, end = squares(size)
+            count = HALF_W // size
+            halves = "p (x s h w) t -> p x s h w t"
+            a_half = a_t[:, n].rearrange(halves, x=X, h=2, w=size)[:, :, :, 0]
+            b_half = b_in_psum(n).rearrange(halves, x=X, h=2, w=size)[:, :, :, 1]
+            nc.vector.tensor_tensor(
+                out=same_keys[:, :, first:end, :].rearrange("p x (s k j) t -> p x s k j t", k=size, j=size)[:, :, :, kk],
+                in0=a_half,
+                in1=b_half[:, :, :, kk : kk + 1].to_broadcast([P, X, count, size, PACK]),
                 op=ALU.mult,
             )
 
@@ -349,81 +418,91 @@ def tile_localtrittention_pa_kernel(tc, a, b, c, out_0, out_1):
         def factors_of_halves():
             nc.scalar.activation(out=factors[:], in_=half_shifts[:], func=ACT.Exp, bias=lowest[:, 0:1], scale=-1.0)
 
-        def exponential(n, region, k, first_col, width, row):
-            scores = bank(n, region)[:, first_col : first_col + width]
+        def shift_for(n, region):
             if n == NW - 1:
                 half = LAST if region == OWN else FIRST
-                nc.scalar.activation(out=row, in_=scores, func=ACT.Exp, bias=half_shifts[:, half : half + 1], scale=INV_DH)
-                return
-            if region == OWN:
-                sum_out = own_rows[n % 2][:, k : k + 1]
-            else:
-                sum_col = (PB_OLD if region == OLD else PB_OWN) + k
-                sum_out = sums[n % 2][:, sum_col : sum_col + 1]
+                return half_shifts[:, half : half + 1]
+            return shift[n % 2][:, 0:1]
+
+        def same_exponentials(n, region):
             nc.scalar.activation(
-                out=row, in_=scores, func=ACT.Exp, bias=shift[n % 2][:, 0:1], scale=INV_DH, accum_out=sum_out
+                out=exp_same[n % 2][:, place_of(region), 0:TRI],
+                in_=bank(n, region)[:, 0:TRI],
+                func=ACT.Exp,
+                bias=shift_for(n, region),
+                scale=INV_DH,
             )
 
-        def old_exponentials(n):
-            for k in range(1, W):
-                exponential(n, OLD, k, first_pair(k), k, exp_old_j[n % 2][:, k, 0:k])
+        def turn_exponentials(n, region):
+            for piece in range(PACK):
+                cols = slice(piece * P, (piece + 1) * P)
+                nc.tensor.transpose(sums_turned[:, cols], exp_same[n % 2][:, place_of(region), cols], ident[:])
+            nc.scalar.copy(out=exp_turned[place_of(region)][:].rearrange("p c q -> p (c q)"), in_=sums_turned[:])
+
+        def same_sums(n):
+            return turned[n % 2][:, 2 * P : 3 * P]
+
+        def sum_same(n, region):
+            cols = slice(2 * W * place_of(region), 2 * W * (place_of(region) + 1))
+            for piece in range(PACK):
+                nc.tensor.matmul(
+                    out=same_sums(n)[:, cols],
+                    lhsT=exp_turned[place_of(region)][:, piece, :],
+                    rhs=table[:, piece, :],
+                    start=(piece == 0),
+                    stop=(piece == PACK - 1),
+                )
 
         def cross_exponentials(n):
             for k in range(W):
                 region = CROSS_LOW if k < HALF_W else CROSS_HIGH
-                exponential(n, region, k, (k % HALF_W) * W, W, exp_old_j[n % 2][:, W + k, :])
+                first_col = (k % HALF_W) * W
+                nc.scalar.activation(
+                    out=exp_cross[n % 2][:, k, :],
+                    in_=bank(n, region)[:, first_col : first_col + W],
+                    func=ACT.Exp,
+                    bias=shift_for(n, region),
+                    scale=INV_DH,
+                    accum_out=sums[n % 2][:, W + k : W + k + 1],
+                )
+
+        def cross_sums_over_k(n):
+            for j in range(W):
+                nc.scalar.activation(
+                    out=unread[:, j * W : (j + 1) * W],
+                    in_=exp_cross[n % 2][:, :, j],
+                    func=ACT.Copy,
+                    accum_out=sums[n % 2][:, j : j + 1],
+                )
 
         def cross_exponentials_of_last():
+            n = NW - 1
             for half, region in enumerate((CROSS_LOW, CROSS_HIGH)):
-                rows = slice(W + half * HALF_W, W + (half + 1) * HALF_W)
+                rows = slice(half * HALF_W, (half + 1) * HALF_W)
                 nc.scalar.activation(
-                    out=exp_old_j[(NW - 1) % 2][:, rows, :].rearrange("p k j -> p (k j)"),
-                    in_=bank(NW - 1, region)[:],
+                    out=exp_cross[n % 2][:, rows, :].rearrange("p k j -> p (k j)"),
+                    in_=bank(n, region)[:],
                     func=ACT.Exp,
-                    bias=half_shifts[:, FIRST : FIRST + 1],
+                    bias=shift_for(n, region),
                     scale=INV_DH,
                 )
 
-        def sums_over_j_of_last(half, rows, sum_col):
-            nc.vector.tensor_reduce(
-                out=half_sums[half][:, sum_col : sum_col + rows.shape[1]], in_=rows[:], axis=AXIS_X, op=ALU.add
-            )
+        def cross_sums_over_j_of_last():
+            i = (NW - 1) % 2
+            nc.vector.tensor_reduce(out=sums[i][:, W : 2 * W], in_=exp_cross[i][:], axis=AXIS_X, op=ALU.add)
 
-        def own_exponentials(n):
-            for k in range(1, W):
-                exponential(n, OWN, k, first_pair(k), k, exp_own_j[n % 2][:, k, 0:k])
-
-        def scalar_sums_over_k(n):
-            used = 0
-            for j in range(W):
-                column = exp_old_j[n % 2][:, j + 1 : 2 * W, j]
-                nc.scalar.activation(
-                    out=unread[:, used : used + column.shape[1]],
-                    in_=column,
-                    func=ACT.Copy,
-                    accum_out=(half_sums[FIRST] if n == NW - 1 else sums[n % 2])[:, PA_OLD + j : PA_OLD + j + 1],
-                )
-                used += column.shape[1]
-
-        def gpsimd_sums_over_k(n, rows, sum_col):
-            count = rows.shape[1] // 2
-            while count >= 1:
-                out = folded[:, 0:count, :] if count > 1 else sums[n % 2][:, sum_col : sum_col + W].unsqueeze(1)
-                nc.gpsimd.tensor_tensor(out=out, in0=rows[:, 0:count, :], in1=rows[:, count : 2 * count, :], op=ALU.add)
-                rows = folded
-                count //= 2
-
-        def vector_sums_over_k(half, rows, sum_col):
-            count = rows.shape[1] // 2
+        def cross_sums_over_k_of_last():
+            rows = exp_cross[(NW - 1) % 2]
+            count = W // 2
             while count >= LAST_ROWS:
                 nc.vector.tensor_tensor(
-                    out=folded_last[:, 0:count, :], in0=rows[:, 0:count, :], in1=rows[:, count : 2 * count, :], op=ALU.add
+                    out=folded[:, 0:count, :], in0=rows[:, 0:count, :], in1=rows[:, count : 2 * count, :], op=ALU.add
                 )
-                rows = folded_last
+                rows = folded
                 count //= 2
             nc.vector.tensor_reduce(
-                out=half_sums[half][:, sum_col : sum_col + W],
-                in_=rows[:, 0:LAST_ROWS, :].rearrange("p k j -> p j k"),
+                out=sums[(NW - 1) % 2][:, 0:W],
+                in_=folded[:, 0:LAST_ROWS, :].rearrange("p k j -> p j k"),
                 axis=AXIS_X,
                 op=ALU.add,
             )
@@ -433,53 +512,61 @@ def tile_localtrittention_pa_kernel(tc, a, b, c, out_0, out_1):
                 out=full[g % 2][:],
                 in0=(masked_first if g == 0 else masked_later)[:],
                 scalar=masked_part[g % 2][:, 0:1],
-                in1=sums[g % 2][:],
+                in1=same_sums(g),
                 op0=ALU.mult,
                 op1=ALU.add,
             )
 
-        def add_own_rows(g):
-            pb_own = full[g % 2][:, PB_OWN : PB_OWN + W]
-            nc.vector.tensor_tensor(out=pb_own, in0=pb_own, in1=own_rows[g % 2][:], op=ALU.add)
+        def add_cross(g):
+            middle = full[g % 2][:, PA_OLD : PB_OWN + W]
+            nc.vector.tensor_tensor(out=middle, in0=middle, in1=sums[g % 2][:], op=ALU.add)
 
         def add_masked_pairs_to_halves():
             nc.vector.tensor_scalar(
                 out=full[(NW - 1) % 2][:], in0=masked_later[:], scalar1=factors[:, NONE : NONE + 1], scalar2=None, op0=ALU.mult
             )
 
-        def add_half(half):
-            whole = full[(NW - 1) % 2][:]
+        def add_half(half, first_col, addend):
+            part = full[(NW - 1) % 2][:, first_col : first_col + 2 * W]
             nc.vector.scalar_tensor_tensor(
-                out=whole, in0=half_sums[half][:], scalar=factors[:, half : half + 1], in1=whole, op0=ALU.mult, op1=ALU.add
+                out=part, in0=addend, scalar=factors[:, half : half + 1], in1=part, op0=ALU.mult, op1=ALU.add
             )
 
+        def by_token(columns):
+            return columns.rearrange("p (o s w) -> p o s w", o=2, s=2)
+
         def sum_of_all(g):
-            nc.vector.tensor_reduce(out=total[:], in_=full[g % 2][:, 0 : 2 * W], axis=AXIS_X, op=ALU.add)
+            nc.vector.tensor_reduce(out=total[:], in_=by_token(full[g % 2][:])[:, :, 1, :], axis=mybir.AxisListType.XY, op=ALU.add)
 
         def invert_sum(g):
             nc.vector.reciprocal(out=scale[g % 2][:], in_=total[:])
 
+        def result_of(g):
+            return result[:, g, :].rearrange("p (s o w) -> p o s w", o=2, s=2)
+
         def normalise(g):
-            nc.scalar.activation(out=result[:, g, :], in_=full[g % 2][:], func=ACT.Copy, scale=scale[g % 2][:, 0:1])
+            nc.scalar.activation(out=result_of(g), in_=by_token(full[g % 2][:]), func=ACT.Copy, scale=scale[g % 2][:, 0:1])
 
         def normalise_last():
             g = NW - 1
             nc.vector.tensor_scalar(
-                out=result[:, g, :], in0=full[g % 2][:], scalar1=scale[g % 2][:, 0:1], scalar2=None, op0=ALU.mult
+                out=result_of(g), in0=by_token(full[g % 2][:]), scalar1=scale[g % 2][:, 0:1], scalar2=None, op0=ALU.mult
             )
 
         def store_outputs(first, end):
             for x in range(X):
                 rows = slice(x * W, (x + 1) * W)
                 nc.sync.dma_start(
-                    out=out_0[x].rearrange("n i j -> i n j")[:, first:end], in_=result[rows, first:end, 0 : 2 * W]
+                    out=out_0[x].rearrange("n i j -> i n j")[:, first:end], in_=result[rows, first:end, 2 * W : 4 * W]
                 )
                 nc.scalar.dma_start(
-                    out=out_1[x].rearrange("n i k -> i n k")[:, first:end], in_=result[rows, first:end, 2 * W : 4 * W]
+                    out=out_1[x].rearrange("n i k -> i n k")[:, first:end], in_=result[rows, first:end, 0 : 2 * W]
                 )
 
         def keys(n):
-            return [lambda k=k: same_product(n, k) for k in range(1, W)]
+            return [lambda x=x: same_product_of_head(n, x) for x in range(X)] + [
+                lambda size=size, kk=kk: same_product(n, size, kk) for size in reversed(LEVELS[1:]) for kk in range(size)
+            ]
 
         def crosses(n):
             return [lambda x=x: cross_product(n, x) for x in range(X)]
@@ -491,13 +578,25 @@ def tile_localtrittention_pa_kernel(tc, a, b, c, out_0, out_1):
         def finish(g):
             return [
                 lambda: add_masked_pairs(g),
-                lambda: add_own_rows(g),
+                lambda: add_cross(g),
                 lambda: sum_of_all(g),
                 lambda: invert_sum(g),
             ]
 
         def wait_for_quantising():
             nc.gpsimd.tensor_copy(out=gate[:], in_=cross_codes[X - 1][:, 0:1])
+
+        def exponentials(g):
+            if g > 0:
+                same_exponentials(g, OLD)
+            same_exponentials(g, OWN)
+            for region in (OLD, OWN):
+                turn_exponentials(g, region)
+            for region in (OLD, OWN):
+                sum_same(g, region)
+            if g > 0:
+                cross_exponentials(g)
+                cross_sums_over_k(g)
 
         with tc.manual_schedule():
             load_window(0)
@@ -508,7 +607,7 @@ def tile_localtrittention_pa_kernel(tc, a, b, c, out_0, out_1):
             quantise_mask_queries()
             prepare_window(0)
             load_window(1)
-            clear_exponentials()
+            build_the_table()
             for n in range(NW - 1):
                 has_cross = n > 0
                 g = n - 1
@@ -517,13 +616,16 @@ def tile_localtrittention_pa_kernel(tc, a, b, c, out_0, out_1):
                     load_window(n + 2)
                 if has_cross:
                     score_same(n, OLD, n - 1)
-                if g >= 1:
-                    wait_for_quantising()
-                    gpsimd_sums_over_k(g - 1, exp_own_j[(g - 1) % 2], PA_OWN)
+                    for x in range(X):
+                        cross_product_scalar(n, x)
+                    if g >= 1:
+                        wait_for_quantising()
+                    for x in range(X):
+                        cross_product_shared(n, x)
                 if n == 0:
-                    weave(keys(0)[:HALF_W], [])
+                    weave(keys(0)[:X], [])
                     quantise_queries(0)
-                    weave(keys(0)[HALF_W:], [])
+                    weave(keys(0)[X:], [])
                     quantise_mask_keys(0)
                     quantise_mask_keys(1)
                 else:
@@ -532,12 +634,7 @@ def tile_localtrittention_pa_kernel(tc, a, b, c, out_0, out_1):
                     weave(long_ones[-10:], finish(g - 1) if g >= 1 else [])
                 if g >= 0:
                     shift_of(g)
-                    if g > 0:
-                        cross_exponentials(g)
-                        old_exponentials(g)
-                    own_exponentials(g)
-                    if g > 0:
-                        scalar_sums_over_k(g)
+                    exponentials(g)
                     if g >= 1:
                         normalise(g - 1)
                 quantise_queries(n + 1)
@@ -551,8 +648,11 @@ def tile_localtrittention_pa_kernel(tc, a, b, c, out_0, out_1):
 
             n, g = NW - 1, NW - 2
             score_same(n, OLD, n - 1)
+            for x in range(X):
+                cross_product_scalar(n, x)
             wait_for_quantising()
-            gpsimd_sums_over_k(g - 1, exp_own_j[(g - 1) % 2], PA_OWN)
+            for x in range(X):
+                cross_product_shared(n, x)
             cross_product(n, 0)
             top_of(g, CROSS_LOW)
             top_of(g, CROSS_HIGH)
@@ -563,9 +663,7 @@ def tile_localtrittention_pa_kernel(tc, a, b, c, out_0, out_1):
             weave([lambda: cross_product(n, 2), lambda: cross_product(n, 3)], [lambda: top_of(n, OLD)])
             for x in range(X):
                 cross_quantise(x)
-            old_exponentials(g)
-            cross_exponentials(g)
-            own_exponentials(g)
+            exponentials(g)
             for x in range(X):
                 score_cross(n, x)
             weave(keys(n)[:ROWS_BEFORE_TOPS], [])
@@ -581,28 +679,29 @@ def tile_localtrittention_pa_kernel(tc, a, b, c, out_0, out_1):
             )
             normalise(g - 1)
             store_outputs(0, g)
+            same_exponentials(n, OLD)
+            turn_exponentials(n, OLD)
+            sum_same(n, OLD)
             cross_exponentials_of_last()
-            old_exponentials(n)
-            scalar_sums_over_k(n)
-            gpsimd_sums_over_k(g, exp_own_j[g % 2], PA_OWN)
-            gpsimd_sums_over_k(g, exp_old_j[g % 2], PA_OLD)
             same_quantise(n, 0)
             same_quantise(n, 1)
             score_same(n, OWN, n)
-            sums_over_j_of_last(FIRST, exp_old_j[n % 2], PB_OLD)
+            cross_sums_over_j_of_last()
             top_of(n, OWN)
             half_shift_of(LAST, tops[n % 2][:, OWN : OWN + 1])
             lowest_shift()
             factors_of_halves()
-            own_exponentials(n)
+            same_exponentials(n, OWN)
+            turn_exponentials(n, OWN)
+            sum_same(n, OWN)
+            cross_sums_over_k_of_last()
             for short_one in finish(g):
                 short_one()
             normalise(g)
             add_masked_pairs_to_halves()
-            add_half(FIRST)
-            sums_over_j_of_last(LAST, exp_own_j[n % 2], PB_OWN)
-            vector_sums_over_k(LAST, exp_own_j[n % 2], PA_OWN)
-            add_half(LAST)
+            add_half(FIRST, PA_OLD, sums[n % 2][:])
+            add_half(FIRST, PB_OLD, same_sums(n)[:, 0 : 2 * W])
+            add_half(LAST, PB_OWN, same_sums(n)[:, 2 * W : 4 * W])
             sum_of_all(n)
             invert_sum(n)
             normalise_last()

@@ -30,8 +30,8 @@ TOP_SQUARE = HALF_W * HALF_W
 LEVELS = (16, 8, 4, 2, 1)
 IGNORE = -1000000.0
 INV_DH = 1.0 / DH
-SHARED_ROWS = 5
-SCALAR_ROWS = 3
+SHARED_ROWS = 4
+SCALAR_ROWS = 4
 VECTOR_ROWS = W - SHARED_ROWS - SCALAR_ROWS
 LAST_ROWS = 8
 ROWS_BEFORE_TOPS = 6
@@ -99,8 +99,8 @@ def tile_localtrittention_pa_kernel(tc, a, b, c, out_0, out_1):
         exp_turned = [keep.tile([P, PACK, P], F32, name="exp_turned%d" % i) for i in range(2)]
         members = [keep.tile([P, BANK], F32, name="members%d" % i) for i in range(2)]
         table = keep.tile([P, PACK, 2 * W], F32, name="table")
-        unread = keep.tile([P, W * W], F32, name="unread")
         folded = keep.tile([P, HALF_W, W], F32, name="folded")
+        folded_last = keep.tile([P, HALF_W, W], F32, name="folded_last")
         gate = keep.tile([P, 1], U32, name="gate")
 
         tops = [keep.tile([P, 5], F32, name="tops%d" % i) for i in range(2)]
@@ -467,13 +467,13 @@ def tile_localtrittention_pa_kernel(tc, a, b, c, out_0, out_1):
                 )
 
         def cross_sums_over_k(n):
-            for j in range(W):
-                nc.scalar.activation(
-                    out=unread[:, j * W : (j + 1) * W],
-                    in_=exp_cross[n % 2][:, :, j],
-                    func=ACT.Copy,
-                    accum_out=sums[n % 2][:, j : j + 1],
-                )
+            rows = exp_cross[n % 2]
+            count = W // 2
+            while count >= 1:
+                out = folded[:, 0:count, :] if count > 1 else sums[n % 2][:, 0:W].unsqueeze(1)
+                nc.gpsimd.tensor_tensor(out=out, in0=rows[:, 0:count, :], in1=rows[:, count : 2 * count, :], op=ALU.add)
+                rows = folded
+                count //= 2
 
         def cross_exponentials_of_last():
             n = NW - 1
@@ -496,13 +496,13 @@ def tile_localtrittention_pa_kernel(tc, a, b, c, out_0, out_1):
             count = W // 2
             while count >= LAST_ROWS:
                 nc.vector.tensor_tensor(
-                    out=folded[:, 0:count, :], in0=rows[:, 0:count, :], in1=rows[:, count : 2 * count, :], op=ALU.add
+                    out=folded_last[:, 0:count, :], in0=rows[:, 0:count, :], in1=rows[:, count : 2 * count, :], op=ALU.add
                 )
-                rows = folded
+                rows = folded_last
                 count //= 2
             nc.vector.tensor_reduce(
                 out=sums[(NW - 1) % 2][:, 0:W],
-                in_=folded[:, 0:LAST_ROWS, :].rearrange("p k j -> p j k"),
+                in_=folded_last[:, 0:LAST_ROWS, :].rearrange("p k j -> p j k"),
                 axis=AXIS_X,
                 op=ALU.add,
             )
@@ -596,7 +596,6 @@ def tile_localtrittention_pa_kernel(tc, a, b, c, out_0, out_1):
                 sum_same(g, region)
             if g > 0:
                 cross_exponentials(g)
-                cross_sums_over_k(g)
 
         with tc.manual_schedule():
             load_window(0)
@@ -620,6 +619,8 @@ def tile_localtrittention_pa_kernel(tc, a, b, c, out_0, out_1):
                         cross_product_scalar(n, x)
                     if g >= 1:
                         wait_for_quantising()
+                    if g >= 2:
+                        cross_sums_over_k(g - 1)
                     for x in range(X):
                         cross_product_shared(n, x)
                 if n == 0:
@@ -653,6 +654,7 @@ def tile_localtrittention_pa_kernel(tc, a, b, c, out_0, out_1):
             wait_for_quantising()
             for x in range(X):
                 cross_product_shared(n, x)
+            cross_sums_over_k(g - 1)
             cross_product(n, 0)
             top_of(g, CROSS_LOW)
             top_of(g, CROSS_HIGH)
@@ -664,6 +666,7 @@ def tile_localtrittention_pa_kernel(tc, a, b, c, out_0, out_1):
             for x in range(X):
                 cross_quantise(x)
             exponentials(g)
+            cross_sums_over_k(g)
             for x in range(X):
                 score_cross(n, x)
             weave(keys(n)[:ROWS_BEFORE_TOPS], [])
@@ -680,12 +683,12 @@ def tile_localtrittention_pa_kernel(tc, a, b, c, out_0, out_1):
             normalise(g - 1)
             store_outputs(0, g)
             same_exponentials(n, OLD)
-            turn_exponentials(n, OLD)
-            sum_same(n, OLD)
             cross_exponentials_of_last()
+            turn_exponentials(n, OLD)
             same_quantise(n, 0)
             same_quantise(n, 1)
             score_same(n, OWN, n)
+            sum_same(n, OLD)
             cross_sums_over_j_of_last()
             top_of(n, OWN)
             half_shift_of(LAST, tops[n % 2][:, OWN : OWN + 1])

@@ -33,6 +33,7 @@ INV_DH = 1.0 / DH
 SHARED_ROWS = 4
 SCALAR_ROWS = 4
 VECTOR_ROWS = W - SHARED_ROWS - SCALAR_ROWS
+HEADS_BEFORE_SHIFT = 2
 LAST_ROWS = 8
 ROWS_BEFORE_TOPS = 6
 MASKED = -(2.0**100)
@@ -115,6 +116,7 @@ def tile_localtrittention_pa_kernel(tc, a, b, c, out_0, out_1):
         half_shifts = keep.tile([P, 3], F32, name="half_shifts")
         lowest = keep.tile([P, 1], F32, name="lowest")
         factors = keep.tile([P, 3], F32, name="factors")
+        own_total = keep.tile([P, 1], F32, name="own_total")
         result = keep.tile([P, NW, 4 * W], F32, name="result")
 
         p_minus_c_int = keep.tile([P, W], I32, name="p_minus_c_int")
@@ -425,12 +427,14 @@ def tile_localtrittention_pa_kernel(tc, a, b, c, out_0, out_1):
             return shift[n % 2][:, 0:1]
 
         def same_exponentials(n, region):
+            wanted = {"accum_out": own_total[:]} if (n, region) == (NW - 1, OWN) else {}
             nc.scalar.activation(
                 out=exp_same[n % 2][:, place_of(region), 0:TRI],
                 in_=bank(n, region)[:, 0:TRI],
                 func=ACT.Exp,
                 bias=shift_for(n, region),
                 scale=INV_DH,
+                **wanted,
             )
 
         def turn_exponentials(n, region):
@@ -538,6 +542,11 @@ def tile_localtrittention_pa_kernel(tc, a, b, c, out_0, out_1):
         def sum_of_all(g):
             nc.vector.tensor_reduce(out=total[:], in_=by_token(full[g % 2][:])[:, :, 1, :], axis=mybir.AxisListType.XY, op=ALU.add)
 
+        def add_total_of_last_half():
+            nc.vector.scalar_tensor_tensor(
+                out=total[:], in0=own_total[:], scalar=factors[:, LAST : LAST + 1], in1=total[:], op0=ALU.mult, op1=ALU.add
+            )
+
         def invert_sum(g):
             nc.vector.reciprocal(out=scale[g % 2][:], in_=total[:])
 
@@ -573,7 +582,7 @@ def tile_localtrittention_pa_kernel(tc, a, b, c, out_0, out_1):
 
         def tops_of(g):
             regions = (CROSS_LOW, CROSS_HIGH, OWN) if g > 0 else (OWN,)
-            return [lambda region=region: top_of(g, region) for region in regions] + [lambda: top_of_all(g)]
+            return [lambda region=region: top_of(g, region) for region in regions]
 
         def finish(g):
             return [
@@ -590,10 +599,6 @@ def tile_localtrittention_pa_kernel(tc, a, b, c, out_0, out_1):
             if g > 0:
                 same_exponentials(g, OLD)
             same_exponentials(g, OWN)
-            for region in (OLD, OWN):
-                turn_exponentials(g, region)
-            for region in (OLD, OWN):
-                sum_same(g, region)
             if g > 0:
                 cross_exponentials(g)
 
@@ -615,7 +620,7 @@ def tile_localtrittention_pa_kernel(tc, a, b, c, out_0, out_1):
                     load_window(n + 2)
                 if has_cross:
                     score_same(n, OLD, n - 1)
-                    for x in range(X):
+                    for x in range(HEADS_BEFORE_SHIFT):
                         cross_product_scalar(n, x)
                     if g >= 1:
                         wait_for_quantising()
@@ -631,11 +636,19 @@ def tile_localtrittention_pa_kernel(tc, a, b, c, out_0, out_1):
                     quantise_mask_keys(1)
                 else:
                     long_ones = crosses(n) + keys(n)
-                    weave(long_ones[:-10], tops_of(g) + [lambda: top_of(n, OLD)])
+                    long_ones[0]()
+                    for top_one in tops_of(g):
+                        top_one()
+                    weave(long_ones[1:-10], [lambda: top_of_all(g), lambda: top_of(n, OLD)])
                     weave(long_ones[-10:], finish(g - 1) if g >= 1 else [])
                 if g >= 0:
                     shift_of(g)
                     exponentials(g)
+                    for place, region in enumerate((OLD, OWN)):
+                        turn_exponentials(g, region)
+                        cross_product_scalar(n, HEADS_BEFORE_SHIFT + place)
+                    for region in (OLD, OWN):
+                        sum_same(g, region)
                     if g >= 1:
                         normalise(g - 1)
                 quantise_queries(n + 1)
@@ -649,7 +662,7 @@ def tile_localtrittention_pa_kernel(tc, a, b, c, out_0, out_1):
 
             n, g = NW - 1, NW - 2
             score_same(n, OLD, n - 1)
-            for x in range(X):
+            for x in range(HEADS_BEFORE_SHIFT):
                 cross_product_scalar(n, x)
             wait_for_quantising()
             for x in range(X):
@@ -663,12 +676,20 @@ def tile_localtrittention_pa_kernel(tc, a, b, c, out_0, out_1):
             top_of_all(g)
             shift_of(g)
             weave([lambda: cross_product(n, 2), lambda: cross_product(n, 3)], [lambda: top_of(n, OLD)])
+            same_exponentials(g, OLD)
+            same_exponentials(g, OWN)
+            for x in range(HEADS_BEFORE_SHIFT, X):
+                cross_product_scalar(n, x)
             for x in range(X):
                 cross_quantise(x)
-            exponentials(g)
+            cross_exponentials(g)
             cross_sums_over_k(g)
             for x in range(X):
                 score_cross(n, x)
+            for region in (OLD, OWN):
+                turn_exponentials(g, region)
+            for region in (OLD, OWN):
+                sum_same(g, region)
             weave(keys(n)[:ROWS_BEFORE_TOPS], [])
             weave(
                 keys(n)[ROWS_BEFORE_TOPS:],
@@ -693,8 +714,8 @@ def tile_localtrittention_pa_kernel(tc, a, b, c, out_0, out_1):
             top_of(n, OWN)
             half_shift_of(LAST, tops[n % 2][:, OWN : OWN + 1])
             lowest_shift()
-            factors_of_halves()
             same_exponentials(n, OWN)
+            factors_of_halves()
             turn_exponentials(n, OWN)
             sum_same(n, OWN)
             cross_sums_over_k_of_last()
@@ -704,8 +725,9 @@ def tile_localtrittention_pa_kernel(tc, a, b, c, out_0, out_1):
             add_masked_pairs_to_halves()
             add_half(FIRST, PA_OLD, sums[n % 2][:])
             add_half(FIRST, PB_OLD, same_sums(n)[:, 0 : 2 * W])
-            add_half(LAST, PB_OWN, same_sums(n)[:, 2 * W : 4 * W])
             sum_of_all(n)
+            add_total_of_last_half()
             invert_sum(n)
+            add_half(LAST, PB_OWN, same_sums(n)[:, 2 * W : 4 * W])
             normalise_last()
             store_outputs(g, NW)

@@ -31,9 +31,9 @@ LEVELS = (16, 8, 4, 2, 1)
 IGNORE = -1000000.0
 INV_DH = 1.0 / DH
 SHARED_ROWS = 4
-SCALAR_ROWS = 4
+SCALAR_ROWS = 6
 VECTOR_ROWS = W - SHARED_ROWS - SCALAR_ROWS
-HEADS_BEFORE_SHIFT = 2
+HEADS_BEFORE_SHIFT = 3
 LAST_ROWS = 8
 ROWS_BEFORE_TOPS = 6
 MASKED = -(2.0**100)
@@ -611,13 +611,14 @@ def tile_localtrittention_pa_kernel(tc, a, b, c, out_0, out_1):
             quantise_mask_queries()
             prepare_window(0)
             load_window(1)
+            load_window(2)
             build_the_table()
+            prepare_window(1)
             for n in range(NW - 1):
                 has_cross = n > 0
                 g = n - 1
-                prepare_window(n + 1)
-                if n + 2 < NW:
-                    load_window(n + 2)
+                if n + 3 < NW:
+                    load_window(n + 3)
                 if has_cross:
                     score_same(n, OLD, n - 1)
                     for x in range(HEADS_BEFORE_SHIFT):
@@ -644,13 +645,16 @@ def tile_localtrittention_pa_kernel(tc, a, b, c, out_0, out_1):
                 if g >= 0:
                     shift_of(g)
                     exponentials(g)
-                    for place, region in enumerate((OLD, OWN)):
-                        turn_exponentials(g, region)
-                        cross_product_scalar(n, HEADS_BEFORE_SHIFT + place)
+                    turn_exponentials(g, OLD)
+                    for x in range(HEADS_BEFORE_SHIFT, X):
+                        cross_product_scalar(n, x)
+                    turn_exponentials(g, OWN)
                     for region in (OLD, OWN):
                         sum_same(g, region)
                     if g >= 1:
                         normalise(g - 1)
+                if n + 2 < NW:
+                    prepare_window(n + 2)
                 quantise_queries(n + 1)
                 same_quantise(n, 0)
                 same_quantise(n, 1)

from contextlib import ExitStack

import concourse.mybir as mybir
from concourse.masks import make_identity

F32 = mybir.dt.float32
BF16 = mybir.dt.bfloat16
I32 = mybir.dt.int32
U32 = mybir.dt.uint32
U8 = mybir.dt.uint8
FP8X4 = mybir.dt.float8_e4m3fn_x4
ALU = mybir.AluOpType
ACT = mybir.ActivationFunctionType
AXIS_X = mybir.AxisListType.X

P = 128
PACK = 4
X = 4
NW = 10
W = 32
HALF_W = W // 2
DH = 512
TRI = W * (W - 1) // 2
BANK = 512
SCORE_BANKS = 5
OLD, CROSS_LOW, CROSS_HIGH, OWN = 0, 1, 2, 3
FIRST, LAST, NONE = 0, 1, 2
PB_OLD, PA_OLD, PB_OWN, PA_OWN = 0, W, 2 * W, 3 * W
TOP_SQUARE = HALF_W * HALF_W
LEVELS = (16, 8, 4, 2, 1)
IGNORE = -1000000.0
INV_DH = 1.0 / DH
SHARED_ROWS = 4
SCALAR_ROWS = 6
VECTOR_ROWS = W - SHARED_ROWS - SCALAR_ROWS
HEADS_BEFORE_SHIFT = 3
LAST_ROWS = 8
ROWS_BEFORE_TOPS = 6
MASKED = -(2.0**100)

FLOPS = 2 * W * DH * (X * NW * TRI + X * (NW - 1) * TRI + X * (NW - 1) * W * W)


def squares(size):
    return 512 - 32 * size, 512 - 16 * size


def weave(long_ones, short_ones):
    for place, long_one in enumerate(long_ones):
        long_one()
        for short_one in short_ones[place : place + 1]:
            short_one()
    for short_one in short_ones[len(long_ones) :]:
        short_one()


def tile_localtrittention_pa_kernel(tc, a, b, c, out_0, out_1):
    nc = tc.nc
    with ExitStack() as ctx:
        keep = ctx.enter_context(tc.tile_pool(name="keep", bufs=1))
        psum = ctx.enter_context(tc.psum_pool(name="psum", bufs=1))

        raw = {
            "a": keep.tile([P, NW, DH], BF16, name="raw_a"),
            "b": keep.tile([P, NW, DH], BF16, name="raw_b"),
            "c": keep.tile([P, NW, DH], BF16, name="raw_c"),
        }
        a_t = keep.tile([P, NW, P, PACK], BF16, name="a_t", align_bytes=64)
        b_shared = [keep.tile([P, X, SHARED_ROWS, PACK], BF16, name="b_shared%d" % i, align_bytes=64) for i in range(2)]
        b_scalar = [keep.tile([P, X, SCALAR_ROWS, PACK], F32, name="b_scalar%d" % i) for i in range(2)]
        ident = keep.tile([P, P], F32, name="ident")

        c_t = [keep.tile([P, P, PACK], BF16, name="c_t%d" % i, align_bytes=64) for i in range(2)]
        c_codes = [keep.tile([P, P], U32, name="c_codes%d" % i, align_bytes=64) for i in range(2)]
        c_scales = [keep.tile([P, P], U8, name="c_scales%d" % i, align_bytes=64) for i in range(2)]
        wide_codes = [keep.tile([P, X * (P + W)], U32, name="wide_codes%d" % i, align_bytes=64) for i in range(2)]
        wide_scales = [keep.tile([P, X * (P + W)], U8, name="wide_scales%d" % i, align_bytes=64) for i in range(2)]

        cross_keys = [keep.tile([P, W, W, PACK], BF16, name="cross_keys%d" % i, align_bytes=64) for i in range(X)]
        cross_codes = [keep.tile([P, W * W], U32, name="cross_codes%d" % i, align_bytes=64) for i in range(X)]
        cross_scales = [keep.tile([P, W * W], U8, name="cross_scales%d" % i, align_bytes=64) for i in range(X)]
        same_keys = keep.tile([P, X, BANK, PACK], BF16, name="same_keys", align_bytes=64)
        same_codes = [keep.tile([P, X, BANK], U32, name="same_codes%d" % i, align_bytes=64) for i in range(2)]
        same_scales = [keep.tile([P, X, BANK], U8, name="same_scales%d" % i, align_bytes=64) for i in range(2)]

        mask_queries = keep.tile([P, 2, P, PACK], BF16, name="mask_queries", align_bytes=64)
        mask_query_codes = keep.tile([P, 2, P], U32, name="mask_query_codes", align_bytes=64)
        mask_query_scales = keep.tile([P, 2, P], U8, name="mask_query_scales", align_bytes=64)
        mask_keys = keep.tile([P, 2, BANK, PACK], BF16, name="mask_keys", align_bytes=64)
        mask_key_codes = keep.tile([P, 2, BANK], U32, name="mask_key_codes", align_bytes=64)
        mask_key_scales = keep.tile([P, 2, BANK], U8, name="mask_key_scales", align_bytes=64)

        banks = [psum.tile([P, BANK], F32, name="bank%d" % i) for i in range(SCORE_BANKS)]
        turned = [psum.tile([P, BANK], F32, name="turned%d" % i) for i in range(2)]

        sums_turned = psum.tile([P, BANK], F32, name="sums_turned")

        exp_same = [keep.tile([P, 2, BANK], F32, name="exp_same%d" % i) for i in range(2)]
        exp_cross = [keep.tile([P, W, W], F32, name="exp_cross%d" % i) for i in range(2)]
        exp_turned = [keep.tile([P, PACK, P], F32, name="exp_turned%d" % i) for i in range(2)]
        members = [keep.tile([P, BANK], F32, name="members%d" % i) for i in range(2)]
        table = keep.tile([P, PACK, 2 * W], F32, name="table")
        folded = keep.tile([P, HALF_W, W], F32, name="folded")
        folded_last = keep.tile([P, HALF_W, W], F32, name="folded_last")
        gate = keep.tile([P, 1], U32, name="gate")

        tops = [keep.tile([P, 5], F32, name="tops%d" % i) for i in range(2)]
        top = [keep.tile([P, 1], F32, name="top%d" % i) for i in range(2)]
        shift = [keep.tile([P, 1], F32, name="shift%d" % i) for i in range(2)]
        masked_part = [keep.tile([P, 1], F32, name="masked_part%d" % i) for i in range(2)]
        sums = [keep.tile([P, 2 * W], F32, name="sums%d" % i) for i in range(2)]
        full = [keep.tile([P, 4 * W], F32, name="full%d" % i) for i in range(2)]
        total = keep.tile([P, 1], F32, name="total")
        scale = [keep.tile([P, 1], F32, name="scale%d" % i) for i in range(2)]
        top_first = keep.tile([P, 1], F32, name="top_first")
        half_shifts = keep.tile([P, 3], F32, name="half_shifts")
        lowest = keep.tile([P, 1], F32, name="lowest")
        factors = keep.tile([P, 3], F32, name="factors")
        own_total = keep.tile([P, 1], F32, name="own_total")
        result = keep.tile([P, NW, 4 * W], F32, name="result")

        p_minus_c_int = keep.tile([P, W], I32, name="p_minus_c_int")
        p_minus_c = keep.tile([P, W], F32, name="p_minus_c")
        i_minus_c_int = keep.tile([P, W], I32, name="i_minus_c_int")
        col_int = keep.tile([P, W], I32, name="col_int")
        i_minus_c = keep.tile([P, W], F32, name="i_minus_c")
        col = keep.tile([P, W], F32, name="col")
        seen = keep.tile([P, W], F32, name="seen")
        work = keep.tile([P, W], F32, name="work")
        masked_first = keep.tile([P, 4 * W], F32, name="masked_first")
        masked_later = keep.tile([P, 4 * W], F32, name="masked_later")

        def bank(n, region):
            return banks[(4 * n + region) % SCORE_BANKS]

        def place_of(region):
            return 1 if region == OWN else 0

        def masks_of(region):
            return (1 if region == CROSS_HIGH else 0), (0 if region == OWN else 1)

        def load_window(n):
            for name, src, queue in (("a", a, nc.sync), ("b", b, nc.scalar if n == 0 else nc.sync), ("c", c, nc.sync)):
                for x in range(X):
                    queue.dma_start(out=raw[name][x * W : (x + 1) * W, n, :], in_=src[x, n])

        def count_rows_and_columns():
            nc.gpsimd.iota(p_minus_c_int[:], pattern=[[-1, W]], base=0, channel_multiplier=1)
            make_identity(nc, ident[:])
            for x in range(X):
                nc.gpsimd.iota(i_minus_c_int[x * W : (x + 1) * W, :], pattern=[[-1, W]], base=0, channel_multiplier=1)
            nc.gpsimd.iota(col_int[:], pattern=[[1, W]], base=0, channel_multiplier=0)

        def fill_what_is_never_written():
            nc.gpsimd.memset(mask_keys[:, 1].bitcast(I32), 0)
            nc.gpsimd.memset(mask_keys[:, 0].bitcast(I32), 0)
            nc.gpsimd.memset(same_keys[:, :, TRI:BANK, :], 0.0)
            for i in range(2):
                nc.gpsimd.memset(members[i][:, TRI:BANK], 0.0)
            for i in range(2):
                nc.gpsimd.memset(wide_codes[i][:].bitcast(I32), 0)
                nc.gpsimd.memset(wide_scales[i][:].bitcast(I32), 0)
                nc.gpsimd.memset(c_scales[i][:].bitcast(I32), 0)
                nc.gpsimd.memset(exp_same[i][:], 0.0)
                nc.gpsimd.memset(sums[i][:], 0.0)
                nc.vector.memset(tops[i][:, 0:4], MASKED)
                nc.vector.memset(tops[i][:, 4:5], IGNORE)
            nc.gpsimd.memset(half_shifts[:, NONE : NONE + 1], -IGNORE * INV_DH)

        def build_the_table():
            for size in LEVELS:
                first, end = squares(size)
                halves = ident[:, 0:W].rearrange("p (s h w) -> p s h w", h=2, w=size)
                shape = [P, HALF_W // size, size, size]
                views = (
                    halves[:, :, 1, :].unsqueeze(3).to_broadcast(shape),
                    halves[:, :, 0, :].unsqueeze(2).to_broadcast(shape),
                )
                for i in range(2):
                    nc.scalar.copy(
                        out=members[i][:, first:end].rearrange("p (s k j) -> p s k j", k=size, j=size), in_=views[i]
                    )
                nc.scalar.activation(
                    out=mask_keys[:, 0, first:end, 0].rearrange("p (s k j) -> p s k j", k=size, j=size),
                    in_=views[0],
                    func=ACT.Copy,
                    scale=MASKED,
                )
            for i in range(2):
                for piece in range(PACK):
                    cols = slice(piece * P, (piece + 1) * P)
                    nc.tensor.transpose(sums_turned[:, cols], members[i][:, cols], ident[:])
                nc.scalar.copy(
                    out=table[:, :, i * W : (i + 1) * W],
                    in_=sums_turned[:].rearrange("p (c r) -> p c r", c=PACK)[:, :, 0:W],
                )

        def build_constants():
            nc.vector.tensor_copy(out=i_minus_c[:], in_=i_minus_c_int[:])
            nc.vector.tensor_copy(out=col[:], in_=col_int[:])
            nc.vector.tensor_scalar(out=seen[:], in0=i_minus_c[:], scalar1=0.0, scalar2=None, op0=ALU.is_ge)
            old_j, own_j = slice(PA_OLD, PA_OLD + W), slice(PA_OWN, PA_OWN + W)
            old_k, own_k = slice(PB_OLD, PB_OLD + W), slice(PB_OWN, PB_OWN + W)
            nc.vector.tensor_scalar(
                out=masked_later[:, old_j], in0=i_minus_c[:], scalar1=-1.0, scalar2=1.0 * W, op0=ALU.mult, op1=ALU.add
            )
            nc.vector.tensor_scalar(out=work[:], in0=i_minus_c[:], scalar1=0.0, scalar2=-1.0, op0=ALU.max, op1=ALU.mult)
            nc.vector.tensor_scalar(out=masked_later[:, own_j], in0=work[:], scalar1=2.0 * W, scalar2=None, op0=ALU.add)
            nc.vector.tensor_scalar(
                out=masked_later[:, old_k], in0=col[:], scalar1=-1.0, scalar2=2.0 * W, op0=ALU.mult, op1=ALU.add
            )
            nc.vector.tensor_scalar(out=work[:], in0=col[:], scalar1=1.0 * W, scalar2=-1.0, op0=ALU.add, op1=ALU.mult)
            nc.vector.tensor_tensor(out=work[:], in0=work[:], in1=seen[:], op=ALU.mult)
            nc.vector.tensor_scalar(out=masked_later[:, own_k], in0=work[:], scalar1=2.0 * W, scalar2=None, op0=ALU.add)
            nc.vector.memset(masked_first[:], 2.0 * W)
            nc.vector.tensor_copy(out=masked_first[:, own_j], in_=masked_later[:, own_j])
            nc.vector.tensor_tensor(out=work[:], in0=col[:], in1=seen[:], op=ALU.mult)
            nc.vector.tensor_scalar(
                out=masked_first[:, own_k], in0=work[:], scalar1=-1.0, scalar2=2.0 * W, op0=ALU.mult, op1=ALU.add
            )

        def build_the_masks():
            nc.vector.memset(mask_queries[:].bitcast(I32), 0)
            nc.vector.tensor_copy(out=p_minus_c[:], in_=p_minus_c_int[:])
            for high in range(2):
                nc.vector.tensor_scalar(
                    out=mask_queries[:, high].rearrange("p (x i) t -> p x i t", x=X)[:, :, :, 0],
                    in0=p_minus_c[:].unsqueeze(1).to_broadcast([P, X, W]),
                    scalar1=-1.0 * HALF_W * high,
                    scalar2=None,
                    op0=ALU.is_gt,
                )
            nc.scalar.activation(
                out=mask_keys[:, 1].rearrange("p (k j) t -> p k j t", j=W)[:, :, :, 0],
                in_=ident[:, 0:HALF_W].unsqueeze(2).to_broadcast([P, HALF_W, W]),
                func=ACT.Copy,
                scale=MASKED,
            )

        def quantise_mask_queries():
            nc.vector.quantize_mx(
                out=mask_query_codes[:].rearrange("p h q -> p (h q)").bitcast(FP8X4),
                scales=mask_query_scales[:].rearrange("p h q -> p (h q)"),
                in_=mask_queries[:].rearrange("p h q t -> p (h q t)"),
            )

        def quantise_mask_keys(table):
            nc.vector.quantize_mx(
                out=mask_key_codes[:, table, :].bitcast(FP8X4),
                scales=mask_key_scales[:, table, :],
                in_=mask_keys[:, table].rearrange("p c t -> p (c t)"),
            )

        def turn(name, n):
            words = raw[name][:, n, :].bitcast(F32)
            if name == "b":
                turned_words = turned[n % 2][:, 0 : 2 * P].rearrange("p (r u) -> p r u", u=2)
            else:
                turned_words = turned[n % 2][:, 2 * P : 4 * P].rearrange("p (u r) -> p r u", u=2)
            for u in range(2):
                nc.tensor.transpose(turned_words[:, :, u], words[:, u * P : (u + 1) * P], ident[:])
            return turned_words

        def b_in_psum(n):
            return turned[n % 2][:, 0 : 2 * P].bitcast(BF16).rearrange("p (r t) -> p r t", t=PACK)

        def prepare_window(n):
            a_words = turn("a", n)
            b_words = turn("b", n)
            (nc.vector.tensor_copy if n == 0 else nc.scalar.copy)(out=a_t[:, n].bitcast(F32), in_=a_words)
            if n > 0:
                nc.scalar.copy(
                    out=b_shared[n % 2][:].rearrange("p x k t -> p x (k t)").bitcast(F32),
                    in_=b_words.rearrange("p (x k) u -> p x (k u)", x=X)[:, :, 2 * (W - SHARED_ROWS) : 2 * W],
                )
                nc.scalar.copy(
                    out=b_scalar[n % 2][:],
                    in_=b_in_psum(n).rearrange("p (x k) t -> p x k t", x=X)[:, :, VECTOR_ROWS : VECTOR_ROWS + SCALAR_ROWS],
                )
            nc.scalar.copy(out=c_t[n % 2][:].bitcast(F32), in_=turn("c", n))

        def quantise_queries(n):
            nc.vector.quantize_mx(
                out=c_codes[n % 2][:].bitcast(FP8X4),
                scales=c_scales[n % 2][:],
                in_=c_t[n % 2][:].rearrange("p r t -> p (r t)"),
            )
            for wide, narrow, words in ((wide_codes, c_codes, W), (wide_scales, c_scales, W // PACK)):
                nc.sync.dma_start(
                    out=wide[n % 2][:].bitcast(I32).rearrange("p (x q) -> p x q", x=X)[:, :, 0:words],
                    in_=narrow[n % 2][:].bitcast(I32).rearrange("p (x i) -> p x i", x=X),
                )

        def mask_pass(n, region):
            queries, keys_of_mask = masks_of(region)
            nc.tensor.matmul_mx(
                out=bank(n, region)[:],
                lhsT=mask_query_codes[:, queries, :].bitcast(FP8X4),
                lhsT_scale=mask_query_scales[:, queries, :],
                rhs=mask_key_codes[:, keys_of_mask, :].bitcast(FP8X4),
                rhs_scale=mask_key_scales[:, keys_of_mask, :],
                start=True,
                stop=False,
            )

        def score_pass(n, region, x, codes, scales):
            if x == 0 and region != OLD:
                mask_pass(n, region)
            cols = slice(x * P, (x + 1) * P)
            nc.tensor.matmul_mx(
                out=bank(n, region)[:],
                lhsT=wide_codes[n % 2][:, cols].bitcast(FP8X4),
                lhsT_scale=wide_scales[n % 2][:, cols],
                rhs=codes.bitcast(FP8X4),
                rhs_scale=scales,
                start=(x == 0 and region == OLD),
                stop=(x == X - 1),
            )

        def cross_product_shared(n, x):
            shape = [P, SHARED_ROWS, W, PACK]
            nc.gpsimd.tensor_tensor(
                out=cross_keys[x][:, W - SHARED_ROWS : W],
                in0=a_t[:, n - 1, x * W : (x + 1) * W, :].unsqueeze(1).to_broadcast(shape),
                in1=b_shared[n % 2][:, x].unsqueeze(2).to_broadcast(shape),
                op=ALU.mult,
            )

        def cross_product_scalar(n, x):
            for kk in range(SCALAR_ROWS):
                for t in range(PACK):
                    nc.scalar.activation(
                        out=cross_keys[x][:, VECTOR_ROWS + kk, :, t],
                        in_=a_t[:, n - 1, x * W : (x + 1) * W, t],
                        func=ACT.Copy,
                        scale=b_scalar[n % 2][:, x, kk, t : t + 1],
                    )

        def cross_product(n, x):
            shape = [P, VECTOR_ROWS, W, PACK]
            nc.vector.tensor_tensor(
                out=cross_keys[x][:, 0:VECTOR_ROWS],
                in0=a_t[:, n - 1, x * W : (x + 1) * W, :].unsqueeze(1).to_broadcast(shape),
                in1=b_in_psum(n)[:, x * W : x * W + VECTOR_ROWS, :].unsqueeze(2).to_broadcast(shape),
                op=ALU.mult,
            )

        def cross_quantise(x):
            nc.vector.quantize_mx(
                out=cross_codes[x][:].bitcast(FP8X4),
                scales=cross_scales[x][:],
                in_=cross_keys[x][:].rearrange("p k j t -> p (k j t)"),
            )

        def score_cross(n, x):
            for half, region in enumerate((CROSS_LOW, CROSS_HIGH)):
                cols = slice(half * BANK, (half + 1) * BANK)
                score_pass(n, region, x, cross_codes[x][:, cols], cross_scales[x][:, cols])

        def same_product_of_head(n, x):
            shape = [P, HALF_W, HALF_W, PACK]
            nc.vector.tensor_tensor(
                out=same_keys[:, x, 0:TOP_SQUARE, :].rearrange("p (k j) t -> p k j t", j=HALF_W),
                in0=a_t[:, n, x * W : x * W + HALF_W, :].unsqueeze(1).to_broadcast(shape),
                in1=b_in_psum(n)[:, x * W + HALF_W : (x + 1) * W, :].unsqueeze(2).to_broadcast(shape),
                op=ALU.mult,
            )

        def same_product(n, size, kk):
            first, end = squares(size)
            count = HALF_W // size
            halves = "p (x s h w) t -> p x s h w t"
            a_half = a_t[:, n].rearrange(halves, x=X, h=2, w=size)[:, :, :, 0]
            b_half = b_in_psum(n).rearrange(halves, x=X, h=2, w=size)[:, :, :, 1]
            nc.vector.tensor_tensor(
                out=same_keys[:, :, first:end, :].rearrange("p x (s k j) t -> p x s k j t", k=size, j=size)[:, :, :, kk],
                in0=a_half,
                in1=b_half[:, :, :, kk : kk + 1].to_broadcast([P, X, count, size, PACK]),
                op=ALU.mult,
            )

        def same_quantise(n, half):
            heads = slice(2 * half, 2 * half + 2)
            nc.vector.quantize_mx(
                out=same_codes[n % 2][:, heads, :].rearrange("p x c -> p (x c)").bitcast(FP8X4),
                scales=same_scales[n % 2][:, heads, :].rearrange("p x c -> p (x c)"),
                in_=same_keys[:, heads, :, :].rearrange("p x c t -> p (x c t)"),
            )

        def score_same(n, region, key_window):
            for x in range(X):
                score_pass(n, region, x, same_codes[key_window % 2][:, x, :], same_scales[key_window % 2][:, x, :])

        def top_of(n, region):
            width = BANK if region in (CROSS_LOW, CROSS_HIGH) else TRI
            nc.vector.tensor_reduce(
                out=tops[n % 2][:, region : region + 1], in_=bank(n, region)[:, 0:width], axis=AXIS_X, op=ALU.max
            )

        def top_of_all(g):
            nc.vector.tensor_reduce(out=top[g % 2][:], in_=tops[g % 2][:], axis=AXIS_X, op=ALU.max)

        def shift_of(g):
            nc.scalar.activation(out=shift[g % 2][:], in_=top[g % 2][:], func=ACT.Copy, scale=-INV_DH)
            nc.scalar.activation(
                out=masked_part[g % 2][:], in_=tops[g % 2][:, 4:5], func=ACT.Exp, bias=shift[g % 2][:, 0:1], scale=INV_DH
            )

        def top_of_first_half():
            nc.vector.tensor_reduce(out=top_first[:], in_=tops[(NW - 1) % 2][:, OLD : CROSS_HIGH + 1], axis=AXIS_X, op=ALU.max)

        def half_shift_of(half, half_top):
            nc.vector.tensor_scalar(
                out=half_shifts[:, half : half + 1], in0=half_top, scalar1=IGNORE, scalar2=-INV_DH, op0=ALU.max, op1=ALU.mult
            )

        def lowest_shift():
            nc.vector.tensor_reduce(out=lowest[:], in_=half_shifts[:], axis=AXIS_X, op=ALU.min)

        def factors_of_halves():
            nc.scalar.activation(out=factors[:], in_=half_shifts[:], func=ACT.Exp, bias=lowest[:, 0:1], scale=-1.0)

        def shift_for(n, region):
            if n == NW - 1:
                half = LAST if region == OWN else FIRST
                return half_shifts[:, half : half + 1]
            return shift[n % 2][:, 0:1]

        def same_exponentials(n, region):
            wanted = {"accum_out": own_total[:]} if (n, region) == (NW - 1, OWN) else {}
            nc.scalar.activation(
                out=exp_same[n % 2][:, place_of(region), 0:TRI],
                in_=bank(n, region)[:, 0:TRI],
                func=ACT.Exp,
                bias=shift_for(n, region),
                scale=INV_DH,
                **wanted,
            )

        def turn_exponentials(n, region):
            for piece in range(PACK):
                cols = slice(piece * P, (piece + 1) * P)
                nc.tensor.transpose(sums_turned[:, cols], exp_same[n % 2][:, place_of(region), cols], ident[:])
            nc.scalar.copy(out=exp_turned[place_of(region)][:].rearrange("p c q -> p (c q)"), in_=sums_turned[:])

        def same_sums(n):
            return turned[n % 2][:, 2 * P : 3 * P]

        def sum_same(n, region):
            cols = slice(2 * W * place_of(region), 2 * W * (place_of(region) + 1))
            for piece in range(PACK):
                nc.tensor.matmul(
                    out=same_sums(n)[:, cols],
                    lhsT=exp_turned[place_of(region)][:, piece, :],
                    rhs=table[:, piece, :],
                    start=(piece == 0),
                    stop=(piece == PACK - 1),
                )

        def cross_exponentials(n):
            for k in range(W):
                region = CROSS_LOW if k < HALF_W else CROSS_HIGH
                first_col = (k % HALF_W) * W
                nc.scalar.activation(
                    out=exp_cross[n % 2][:, k, :],
                    in_=bank(n, region)[:, first_col : first_col + W],
                    func=ACT.Exp,
                    bias=shift_for(n, region),
                    scale=INV_DH,
                    accum_out=sums[n % 2][:, W + k : W + k + 1],
                )

        def cross_sums_over_k(n):
            rows = exp_cross[n % 2]
            count = W // 2
            while count >= 1:
                out = folded[:, 0:count, :] if count > 1 else sums[n % 2][:, 0:W].unsqueeze(1)
                nc.gpsimd.tensor_tensor(out=out, in0=rows[:, 0:count, :], in1=rows[:, count : 2 * count, :], op=ALU.add)
                rows = folded
                count //= 2

        def cross_exponentials_of_last():
            n = NW - 1
            for half, region in enumerate((CROSS_LOW, CROSS_HIGH)):
                rows = slice(half * HALF_W, (half + 1) * HALF_W)
                nc.scalar.activation(
                    out=exp_cross[n % 2][:, rows, :].rearrange("p k j -> p (k j)"),
                    in_=bank(n, region)[:],
                    func=ACT.Exp,
                    bias=shift_for(n, region),
                    scale=INV_DH,
                )

        def cross_sums_over_j_of_last():
            i = (NW - 1) % 2
            nc.vector.tensor_reduce(out=sums[i][:, W : 2 * W], in_=exp_cross[i][:], axis=AXIS_X, op=ALU.add)

        def cross_sums_over_k_of_last():
            rows = exp_cross[(NW - 1) % 2]
            count = W // 2
            while count >= LAST_ROWS:
                nc.vector.tensor_tensor(
                    out=folded_last[:, 0:count, :], in0=rows[:, 0:count, :], in1=rows[:, count : 2 * count, :], op=ALU.add
                )
                rows = folded_last
                count //= 2
            nc.vector.tensor_reduce(
                out=sums[(NW - 1) % 2][:, 0:W],
                in_=folded_last[:, 0:LAST_ROWS, :].rearrange("p k j -> p j k"),
                axis=AXIS_X,
                op=ALU.add,
            )

        def add_masked_pairs(g):
            nc.vector.scalar_tensor_tensor(
                out=full[g % 2][:],
                in0=(masked_first if g == 0 else masked_later)[:],
                scalar=masked_part[g % 2][:, 0:1],
                in1=same_sums(g),
                op0=ALU.mult,
                op1=ALU.add,
            )

        def add_cross(g):
            middle = full[g % 2][:, PA_OLD : PB_OWN + W]
            nc.vector.tensor_tensor(out=middle, in0=middle, in1=sums[g % 2][:], op=ALU.add)

        def add_masked_pairs_to_halves():
            nc.vector.tensor_scalar(
                out=full[(NW - 1) % 2][:], in0=masked_later[:], scalar1=factors[:, NONE : NONE + 1], scalar2=None, op0=ALU.mult
            )

        def add_half(half, first_col, addend):
            part = full[(NW - 1) % 2][:, first_col : first_col + 2 * W]
            nc.vector.scalar_tensor_tensor(
                out=part, in0=addend, scalar=factors[:, half : half + 1], in1=part, op0=ALU.mult, op1=ALU.add
            )

        def by_token(columns):
            return columns.rearrange("p (o s w) -> p o s w", o=2, s=2)

        def sum_of_all(g):
            nc.vector.tensor_reduce(out=total[:], in_=by_token(full[g % 2][:])[:, :, 1, :], axis=mybir.AxisListType.XY, op=ALU.add)

        def add_total_of_last_half():
            nc.vector.scalar_tensor_tensor(
                out=total[:], in0=own_total[:], scalar=factors[:, LAST : LAST + 1], in1=total[:], op0=ALU.mult, op1=ALU.add
            )

        def invert_sum(g):
            nc.vector.reciprocal(out=scale[g % 2][:], in_=total[:])

        def result_of(g):
            return result[:, g, :].rearrange("p (s o w) -> p o s w", o=2, s=2)

        def normalise(g):
            nc.scalar.activation(out=result_of(g), in_=by_token(full[g % 2][:]), func=ACT.Copy, scale=scale[g % 2][:, 0:1])

        def normalise_last():
            g = NW - 1
            nc.vector.tensor_scalar(
                out=result_of(g), in0=by_token(full[g % 2][:]), scalar1=scale[g % 2][:, 0:1], scalar2=None, op0=ALU.mult
            )

        def store_outputs(first, end):
            for x in range(X):
                rows = slice(x * W, (x + 1) * W)
                nc.sync.dma_start(
                    out=out_0[x].rearrange("n i j -> i n j")[:, first:end], in_=result[rows, first:end, 2 * W : 4 * W]
                )
                nc.scalar.dma_start(
                    out=out_1[x].rearrange("n i k -> i n k")[:, first:end], in_=result[rows, first:end, 0 : 2 * W]
                )

        def keys(n):
            return [lambda x=x: same_product_of_head(n, x) for x in range(X)] + [
                lambda size=size, kk=kk: same_product(n, size, kk) for size in reversed(LEVELS[1:]) for kk in range(size)
            ]

        def crosses(n):
            return [lambda x=x: cross_product(n, x) for x in range(X)]

        def tops_of(g):
            regions = (CROSS_LOW, CROSS_HIGH, OWN) if g > 0 else (OWN,)
            return [lambda region=region: top_of(g, region) for region in regions]

        def finish(g):
            return [
                lambda: add_masked_pairs(g),
                lambda: add_cross(g),
                lambda: sum_of_all(g),
                lambda: invert_sum(g),
            ]

        def wait_for_quantising():
            nc.gpsimd.tensor_copy(out=gate[:], in_=cross_codes[X - 1][:, 0:1])

        def exponentials(g):
            if g > 0:
                same_exponentials(g, OLD)
            same_exponentials(g, OWN)
            if g > 0:
                cross_exponentials(g)

        with tc.manual_schedule():
            load_window(0)
            count_rows_and_columns()
            fill_what_is_never_written()
            build_the_masks()
            build_constants()
            quantise_mask_queries()
            prepare_window(0)
            load_window(1)
            load_window(2)
            build_the_table()
            prepare_window(1)
            for n in range(NW - 1):
                has_cross = n > 0
                g = n - 1
                if n + 3 < NW:
                    load_window(n + 3)
                if has_cross:
                    score_same(n, OLD, n - 1)
                    for x in range(HEADS_BEFORE_SHIFT):
                        cross_product_scalar(n, x)
                    if g >= 1:
                        wait_for_quantising()
                    if g >= 2:
                        cross_sums_over_k(g - 1)
                    for x in range(X):
                        cross_product_shared(n, x)
                if n == 0:
                    weave(keys(0)[:X], [])
                    quantise_queries(0)
                    weave(keys(0)[X:], [])
                    quantise_mask_keys(0)
                    quantise_mask_keys(1)
                else:
                    long_ones = crosses(n) + keys(n)
                    long_ones[0]()
                    for top_one in tops_of(g):
                        top_one()
                    weave(long_ones[1:-10], [lambda: top_of_all(g), lambda: top_of(n, OLD)])
                    weave(long_ones[-10:], finish(g - 1) if g >= 1 else [])
                if g >= 0:
                    shift_of(g)
                    exponentials(g)
                    turn_exponentials(g, OLD)
                    for x in range(HEADS_BEFORE_SHIFT, X):
                        cross_product_scalar(n, x)
                    turn_exponentials(g, OWN)
                    for region in (OLD, OWN):
                        sum_same(g, region)
                    if g >= 1:
                        normalise(g - 1)
                if n + 2 < NW:
                    prepare_window(n + 2)
                quantise_queries(n + 1)
                same_quantise(n, 0)
                same_quantise(n, 1)
                score_same(n, OWN, n)
                if has_cross:
                    for x in range(X):
                        cross_quantise(x)
                        score_cross(n, x)

            n, g = NW - 1, NW - 2
            score_same(n, OLD, n - 1)
            for x in range(HEADS_BEFORE_SHIFT):
                cross_product_scalar(n, x)
            wait_for_quantising()
            for x in range(X):
                cross_product_shared(n, x)
            cross_sums_over_k(g - 1)
            cross_product(n, 0)
            top_of(g, CROSS_LOW)
            top_of(g, CROSS_HIGH)
            top_of(g, OWN)
            cross_product(n, 1)
            top_of_all(g)
            shift_of(g)
            weave([lambda: cross_product(n, 2), lambda: cross_product(n, 3)], [lambda: top_of(n, OLD)])
            same_exponentials(g, OLD)
            same_exponentials(g, OWN)
            for x in range(HEADS_BEFORE_SHIFT, X):
                cross_product_scalar(n, x)
            for x in range(X):
                cross_quantise(x)
            cross_exponentials(g)
            cross_sums_over_k(g)
            for x in range(X):
                score_cross(n, x)
            for region in (OLD, OWN):
                turn_exponentials(g, region)
            for region in (OLD, OWN):
                sum_same(g, region)
            weave(keys(n)[:ROWS_BEFORE_TOPS], [])
            weave(
                keys(n)[ROWS_BEFORE_TOPS:],
                [
                    lambda: top_of(n, CROSS_LOW),
                    lambda: top_of(n, CROSS_HIGH),
                    top_of_first_half,
                    lambda: half_shift_of(FIRST, top_first[:]),
                ]
                + finish(g - 1),
            )
            normalise(g - 1)
            store_outputs(0, g)
            same_exponentials(n, OLD)
            cross_exponentials_of_last()
            turn_exponentials(n, OLD)
            same_quantise(n, 0)
            same_quantise(n, 1)
            score_same(n, OWN, n)
            sum_same(n, OLD)
            cross_sums_over_j_of_last()
            top_of(n, OWN)
            half_shift_of(LAST, tops[n % 2][:, OWN : OWN + 1])
            lowest_shift()
            same_exponentials(n, OWN)
            factors_of_halves()
            turn_exponentials(n, OWN)
            sum_same(n, OWN)
            cross_sums_over_k_of_last()
            for short_one in finish(g):
                short_one()
            normalise(g)
            add_masked_pairs_to_halves()
            add_half(FIRST, PA_OLD, sums[n % 2][:])
            add_half(FIRST, PB_OLD, same_sums(n)[:, 0 : 2 * W])
            sum_of_all(n)
            add_total_of_last_half()
            invert_sum(n)
            add_half(LAST, PB_OWN, same_sums(n)[:, 2 * W : 4 * W])
            normalise_last()
            store_outputs(g, NW)
